import numpy as np
import ml_dtypes


def mxq(x, axis, fmt="e4m3"):
    dtype, down = {"e4m3": (ml_dtypes.float8_e4m3fn, 7), "e5m2": (ml_dtypes.float8_e5m2, 14)}[fmt]
    v = np.moveaxis(np.asarray(x, np.float32).astype(ml_dtypes.bfloat16).astype(np.float64), axis, -1)
    blocks = v.reshape(v.shape[:-1] + (-1, 32))
    amax = np.abs(blocks).max(-1, keepdims=True)
    byte = np.maximum(np.where(amax > 0, np.frexp(amax)[1] - 1 + 127, 0) - down, 1)
    scale = np.exp2(byte - 127.0)
    codes = (blocks / scale).astype(np.float32).astype(dtype).astype(np.float64)
    return np.moveaxis((codes * scale).reshape(v.shape), -1, axis)


WIDE = False


def mx_kscale(k):
    if not WIDE:
        return np.ones(k)
    levels = np.array([10, -10, 5, -5, 0])
    a = np.random.permutation(np.resize(levels, k // 512 * 4)).reshape(k // 512, 4)
    idx = np.arange(k)
    return np.exp2(a[idx // 512, idx % 128 // 32])


BF16 = ml_dtypes.bfloat16


def bf(x):
    return np.asarray(x, np.float32).astype(BF16)


def f64(x):
    return np.asarray(x).astype(np.float64)


E2M1 = np.array([0.0, 0.5, 1.0, 1.5, 2.0, 3.0, 4.0, 6.0, -0.0, -0.5, -1.0, -1.5, -2.0, -3.0, -4.0, -6.0])


def pack_weight(w, fmt):
    k, n = w.shape
    w = f64(bf(w)).reshape(k // 32, 32, n)
    amax = np.abs(w).max(1)
    if fmt == "e4m3":
        byte = np.frexp(amax)[1] - 1 + 127 - 7
    else:
        mant, ex = np.frexp(amax / 6.0)
        byte = np.where(mant > 0.5, ex, ex - 1) + 127
    byte = np.clip(np.where(amax > 0, byte, 1), 1, 254)
    scaled = (w * np.exp2(127.0 - byte)[:, None, :]).reshape(k, n).astype(np.float32)
    by_word = np.ascontiguousarray(scaled.reshape(k // 512, 128, 4, n).transpose(0, 1, 3, 2))
    if fmt == "e4m3":
        words = by_word.astype(ml_dtypes.float8_e4m3fn).view(np.uint8)
    else:
        c = by_word.astype(ml_dtypes.float4_e2m1fn).view(np.uint8) & 0xF
        words = c[..., 0::2] | (c[..., 1::2] << 4)
    return np.ascontiguousarray(words), np.ascontiguousarray(byte.astype(np.uint8).reshape(k // 512, 16, n))


def unpack_weight(words, scales, fmt):
    g, p, n, _ = words.shape
    if fmt == "e4m3":
        vals = np.ascontiguousarray(words).view(ml_dtypes.float8_e4m3fn).astype(np.float64)
    else:
        nib = np.empty((g, p, n, 4), np.uint8)
        nib[..., 0::2] = words & 0xF
        nib[..., 1::2] = words >> 4
        vals = E2M1[nib]
    vals = vals * np.repeat(np.exp2(scales.astype(np.float64) - 127.0), 8, axis=1)[..., None]
    return vals.transpose(0, 1, 3, 2).reshape(g * 512, n)


B, N, C, H, D = 1, 2048, 512, 16, 32
EPS = 1e-12
SCALE = float(D) ** 0.25
VG = 4.0
FMT = "e4m3"


def normalize(t):
    n = np.sqrt((t * t).sum(-1, keepdims=True))
    return t / np.maximum(n, EPS)


def heads(t):
    return t.reshape(B, N, H, D).transpose(0, 2, 1, 3)


def setup_inputs():
    s = mx_kscale(C)
    x = bf(np.random.standard_normal((B, N, C)) * s)
    Wk = np.random.standard_normal((H * D, C)) / np.sqrt(C) / s
    Wk_words, Wk_scales = pack_weight(np.ascontiguousarray(Wk.T), FMT)
    bk = bf(np.random.standard_normal(H * D) * 0.1)
    Wv = np.random.standard_normal((H * D, C)) * VG / np.sqrt(C) / s
    Wv_words, Wv_scales = pack_weight(np.ascontiguousarray(Wv.T), FMT)
    bv = bf(np.random.standard_normal(H * D) * 0.1)
    return {'x': x,
            'Wk_words': Wk_words,
            'Wk_scales': Wk_scales,
            'bk': bk,
            'Wv_words': Wv_words,
            'Wv_scales': Wv_scales,
            'bv': bv}


def reference(x, Wk_words, Wk_scales, bk, Wv_words, Wv_scales, bv):
    xq = mxq(f64(x), 2, 'e4m3')
    k = heads((xq @ unpack_weight(Wk_words, Wk_scales, FMT)) + f64(bk))
    v = heads((xq @ unpack_weight(Wv_words, Wv_scales, FMT)) + f64(bv))
    kn = normalize(k) * SCALE
    vN = v / N
    kk = (kn[..., :, None] * kn[..., None, :]).reshape(B, H, N, D * D)
    vq = mxq(vN, 2, 'e4m3')
    mod_v = mxq(kk, 2, 'e4m3').transpose(0, 1, 3, 2) @ vq
    mod_n = kk.sum(2) / N
    kv_mod = np.concatenate([mod_n[..., None], mod_v], axis=-1).reshape(B, H, D, D, D + 1)
    kv_v = mxq(kn, 2, 'e4m3').transpose(0, 1, 3, 2) @ vq
    kv_n = kn.sum(2) / N
    kv = np.concatenate([kv_n[..., None], kv_v], axis=-1)
    vsum = np.concatenate([np.ones((B, H, 1)), vN.sum(2)], axis=-1)[:, :, None, :]
    return kv_mod, kv, vsum

@@ -1,0 +1,363 @@
+from contextlib import ExitStack
+
+import concourse.mybir as mybir
+from concourse.masks import make_identity
+
+F32 = mybir.dt.float32
+BF16 = mybir.dt.bfloat16
+I32 = mybir.dt.int32
+U32 = mybir.dt.uint32
+U8 = mybir.dt.uint8
+FP8X4 = mybir.dt.float8_e4m3fn_x4
+ALU = mybir.AluOpType
+ACT = mybir.ActivationFunctionType
+
+P = 128
+PACK = 4
+TOKENS = 2048
+FEATURES = 512
+HEADS = 16
+WIDTH = 32
+PASSES = TOKENS // (P * PACK)
+GROUPS = 4
+HG = HEADS // GROUPS
+SHIFTS = WIDTH // 2
+EXT = WIDTH + SHIFTS
+HALF = WIDTH // 2
+EPS = 1e-12
+SCALE = 32.0 ** 0.25
+
+FLOPS = 2 * TOKENS * FEATURES * FEATURES * 2 + 2 * HEADS * TOKENS * WIDTH * (WIDTH * WIDTH + WIDTH)
+
+
+def tile_taylorsoftmaxattention_pa_kernel(
+    tc, x, wk_words, wk_scales, bk, wv_words, wv_scales, bv, kv_mod, kv, vsum
+):
+    nc = tc.nc
+    with ExitStack() as ctx:
+        const = ctx.enter_context(tc.tile_pool(name="const", bufs=1))
+        stage = ctx.enter_context(tc.tile_pool(name="stage", bufs=1))
+        prod = ctx.enter_context(tc.tile_pool(name="prod", bufs=2))
+        aux_ps = ctx.enter_context(tc.psum_pool(name="aux_ps", bufs=3))
+        acc_ps = ctx.enter_context(tc.psum_pool(name="acc_ps", bufs=1))
+
+        one_col = const.tile([P, 1], F32)
+        nc.vector.memset(one_col[:], 1.0)
+        warm = const.tile([P, 1], F32)
+        nc.scalar.sqrt(out=warm[:], in_=one_col[:])
+
+        ident = const.tile([P, P], F32)
+        make_identity(nc, ident[:])
+        ones = const.tile([P, P], F32)
+        nc.gpsimd.memset(ones[:], 1.0)
+
+        w_words = const.tile([P, 2, FEATURES], U32, align_bytes=64)
+        w_planes = const.tile([P, 2, FEATURES], U8, align_bytes=64)
+        nc.vector.memset(w_planes[:].rearrange("p w n -> p (w n)").bitcast(I32), 0)
+        z = const.tile([P, 2, HALF * (WIDTH + 1)], F32)
+        nc.vector.memset(z[:], 0.0)
+
+        x_sb = []
+        for c in range(PASSES):
+            x_sb.append(stage.tile([P, PACK, FEATURES], BF16, name="x_sb%d" % c))
+
+        def load_x(c):
+            rows = x[0, c * P * PACK : (c + 1) * P * PACK, :]
+            nc.sync.dma_start(out=x_sb[c][:], in_=rows.rearrange("(p t) k -> p t k", t=PACK))
+
+        def load_weight(which, words, scales):
+            nc.sync.dma_start(
+                out=w_words[:, which, :].bitcast(I32),
+                in_=words[0].rearrange("p n t -> p (n t)").bitcast(I32),
+            )
+            for r in range(4):
+                nc.sync.dma_start(
+                    out=w_planes[r:P:32, which, :].bitcast(I32),
+                    in_=scales[0, r:16:4, :].bitcast(I32),
+                )
+
+        load_x(0)
+        load_weight(0, wk_words, wk_scales)
+        load_x(1)
+        load_weight(1, wv_words, wv_scales)
+        load_x(2)
+        load_x(3)
+
+        bias_bf = const.tile([P, 2, FEATURES], BF16)
+        nc.scalar.dma_start(out=bias_bf[:, 0, :], in_=bk.partition_broadcast(P))
+        nc.scalar.dma_start(out=bias_bf[:, 1, :], in_=bv.partition_broadcast(P))
+        bk_f = const.tile([P, FEATURES], F32)
+        nc.scalar.copy(out=bk_f[:], in_=bias_bf[:, 0, :])
+        bvn_f = const.tile([P, FEATURES], F32)
+        nc.scalar.mul(out=bvn_f[:], in_=bias_bf[:, 1, :], mul=1.0 / TOKENS)
+
+        x_codes, x_planes, ke, v_codes, v_planes, sm_codes, sm_planes = [], [], [], [], [], [], []
+        for c in range(PASSES):
+            x_codes.append(const.tile([P, FEATURES], U32, name="x_codes%d" % c, align_bytes=64))
+            x_planes.append(const.tile([P, FEATURES], U8, name="x_planes%d" % c, align_bytes=64))
+            ke.append(const.tile([P, HEADS, EXT, PACK], F32, name="ke%d" % c))
+            v_codes.append(const.tile([P, FEATURES], U32, name="v_codes%d" % c, align_bytes=64))
+            v_planes.append(const.tile([P, FEATURES], U8, name="v_planes%d" % c, align_bytes=64))
+            sm_codes.append(const.tile([P, 2 * FEATURES], U32, name="sm_codes%d" % c, align_bytes=64))
+            sm_planes.append(const.tile([P, 2 * FEATURES], U8, name="sm_planes%d" % c, align_bytes=64))
+
+        def project(c, g, which):
+            bank = aux_ps.tile([P, PACK, P], F32, tag="aux")
+            cols = slice(g * P, (g + 1) * P)
+            for t in range(PACK):
+                toks = slice(t * P, (t + 1) * P)
+                nc.tensor.matmul_mx(
+                    out=bank[:, t, :],
+                    lhsT=x_codes[c][:, toks].bitcast(FP8X4),
+                    lhsT_scale=x_planes[c][:, toks],
+                    rhs=w_words[:, which, cols].bitcast(FP8X4),
+                    rhs_scale=w_planes[:, which, cols],
+                    start=True,
+                    stop=True,
+                )
+            return bank
+
+        def head(c):
+            xg = stage.tile([P, PACK, P, PACK], BF16, align_bytes=64)
+            xg_words = xg[:].bitcast(F32)
+            for half in range(2):
+                xt = aux_ps.tile([P, 2, 2, P], F32, tag="aux")
+                for s in range(2):
+                    words = x_sb[c][:, 2 * half + s, :].bitcast(F32)
+                    for u in range(2):
+                        nc.tensor.transpose(xt[:, s, u, :], words[:, u : FEATURES // 2 : 2], ident[:])
+                nc.scalar.copy(
+                    out=xg_words[:, 2 * half : 2 * half + 2, :, :],
+                    in_=xt[:].rearrange("q s u p -> q s p u"),
+                )
+            nc.vector.quantize_mx(
+                out=x_codes[c][:].bitcast(FP8X4),
+                scales=x_planes[c][:],
+                in_=xg[:].rearrange("q t p j -> q (t p j)"),
+            )
+
+            for g in range(GROUPS):
+                kp = project(c, g, 0)
+                nc.vector.tensor_tensor(
+                    out=ke[c][:, g * HG : (g + 1) * HG, 0:WIDTH, :],
+                    in0=kp[:].rearrange("p t (h d) -> p h d t", h=HG),
+                    in1=bk_f[:, g * P : (g + 1) * P]
+                    .rearrange("p (h d) -> p h d", h=HG)
+                    .unsqueeze(3)
+                    .to_broadcast([P, HG, WIDTH, PACK]),
+                    op=ALU.add,
+                )
+            sq = stage.tile([P, HEADS, WIDTH, PACK], F32)
+            nc.scalar.activation(out=sq[:], in_=ke[c][:, :, 0:WIDTH, :], func=ACT.Square)
+            width = WIDTH // 2
+            while width >= 1:
+                nc.gpsimd.tensor_tensor(
+                    out=sq[:, :, 0:width, :],
+                    in0=sq[:, :, 0:width, :],
+                    in1=sq[:, :, width : 2 * width, :],
+                    op=ALU.add,
+                )
+                width //= 2
+            norm = stage.tile([P, HEADS, PACK], F32, bufs=2)
+            nc.scalar.sqrt(out=norm[:], in_=sq[:, :, 0, :])
+            nc.vector.tensor_scalar(
+                out=norm[:], in0=norm[:], scalar1=EPS, scalar2=1.0 / SCALE, op0=ALU.max, op1=ALU.mult
+            )
+            gain = stage.tile([P, HEADS, PACK], F32, bufs=2)
+            nc.vector.reciprocal(out=gain[:], in_=norm[:])
+            nc.gpsimd.tensor_tensor(
+                out=ke[c][:, :, 0:WIDTH, :],
+                in0=ke[c][:, :, 0:WIDTH, :],
+                in1=gain[:].unsqueeze(2).to_broadcast([P, HEADS, WIDTH, PACK]),
+                op=ALU.mult,
+            )
+            nc.scalar.copy(out=ke[c][:, :, WIDTH:EXT, :], in_=ke[c][:, :, 0:SHIFTS, :])
+
+            sm_bf = stage.tile([P, GROUPS, 2, P * PACK], BF16, align_bytes=64)
+            kn_by_group = ke[c][:, :, 0:WIDTH, :].rearrange("p (g h) d t -> p g h (d t)", g=GROUPS)
+            nc.scalar.activation(
+                out=sm_bf[:, :, 0, :].rearrange("p g (h e) -> p g h e", h=HG), in_=kn_by_group, func=ACT.Square
+            )
+            nc.scalar.copy(out=sm_bf[:, :, 1, :].rearrange("p g (h e) -> p g h e", h=HG), in_=kn_by_group)
+
+            v_bf = stage.tile([P, FEATURES, PACK], BF16, align_bytes=64)
+            for g in range(GROUPS):
+                vp = project(c, g, 1)
+                nc.vector.scalar_tensor_tensor(
+                    out=v_bf[:, g * P : (g + 1) * P, :],
+                    in0=vp[:].rearrange("p t f -> p f t"),
+                    scalar=1.0 / TOKENS,
+                    in1=bvn_f[:, g * P : (g + 1) * P].unsqueeze(2).to_broadcast([P, P, PACK]),
+                    op0=ALU.mult,
+                    op1=ALU.add,
+                )
+            nc.vector.quantize_mx(
+                out=v_codes[c][:].bitcast(FP8X4),
+                scales=v_planes[c][:],
+                in_=v_bf[:].rearrange("p f t -> p (f t)"),
+            )
+            nc.vector.quantize_mx(
+                out=sm_codes[c][:].bitcast(FP8X4),
+                scales=sm_planes[c][:],
+                in_=sm_bf[:].rearrange("p g k e -> p (g k e)"),
+            )
+
+        def value_sums():
+            part = aux_ps.tile([P, FEATURES], F32, tag="aux")
+            for c in range(PASSES):
+                for t in range(PACK):
+                    toks = slice(t * P, (t + 1) * P)
+                    nc.tensor.matmul_mx(
+                        out=part[:],
+                        lhsT=x_codes[c][:, toks].bitcast(FP8X4),
+                        lhsT_scale=x_planes[c][:, toks],
+                        rhs=w_words[:, 1, :].bitcast(FP8X4),
+                        rhs_scale=w_planes[:, 1, :],
+                        start=(c == 0 and t == 0),
+                        stop=(c == PASSES - 1 and t == PACK - 1),
+                    )
+            part_sb = stage.tile([P, FEATURES], F32)
+            nc.scalar.copy(out=part_sb[:], in_=part[:])
+            total = aux_ps.tile([P, FEATURES], F32, tag="aux")
+            nc.tensor.matmul(out=total[:], lhsT=ones[:], rhs=part_sb[:], start=True, stop=True)
+            vsum_sb = const.tile([1, HEADS, WIDTH + 1], F32)
+            nc.vector.memset(vsum_sb[:, :, 0:1], 1.0)
+            nc.vector.scalar_tensor_tensor(
+                out=vsum_sb[:, :, 1 : WIDTH + 1],
+                in0=total[0:1, :].rearrange("p (h e) -> p h e", h=HEADS),
+                scalar=1.0 / TOKENS,
+                in1=bias_bf[0:1, 1, :].rearrange("p (h e) -> p h e", h=HEADS),
+                op0=ALU.mult,
+                op1=ALU.add,
+            )
+            nc.sync.dma_start(
+                out=vsum.rearrange("b h o e -> (b o) (h e)"), in_=vsum_sb[:].rearrange("p h e -> p (h e)")
+            )
+
+        kv_out = const.tile([P, GROUPS, WIDTH + 1], F32)
+
+        def plain_sums(g, o_sb):
+            knp = stage.tile([P, PASSES * PACK, P + 1], F32)
+            nc.scalar.copy(out=knp[:, :, P : P + 1], in_=ones[:, 0 : PASSES * PACK].unsqueeze(2))
+            for c in range(PASSES):
+                nc.scalar.copy(
+                    out=knp[:, c * PACK : (c + 1) * PACK, 0:P].rearrange("p t (h d) -> p t h d", h=HG),
+                    in_=ke[c][:, g * HG : (g + 1) * HG, 0:WIDTH, :].rearrange("p h d t -> p t h d"),
+                )
+            gram = aux_ps.tile([P, P + 1], F32, tag="aux")
+            for s in range(PASSES * PACK):
+                nc.tensor.matmul(
+                    out=gram[:],
+                    lhsT=knp[:, s, 0:P],
+                    rhs=knp[:, s, :],
+                    start=(s == 0),
+                    stop=(s == PASSES * PACK - 1),
+                )
+            for hh in range(HG):
+                q = slice(hh * WIDTH, (hh + 1) * WIDTH)
+                nc.scalar.mul(out=o_sb[q, :, 0:1], in_=gram[q, q].unsqueeze(2), mul=1.0 / TOKENS)
+            nc.scalar.mul(out=kv_out[:, g, 0:1], in_=gram[:, P : P + 1], mul=1.0 / TOKENS)
+
+        def unit(g, c, banks, small_bank):
+            heads = slice(g * HG, (g + 1) * HG)
+            kk_bf = prod.tile([P, HG, SHIFTS, WIDTH * PACK], BF16, align_bytes=64)
+            for dl in range(SHIFTS):
+                nc.vector.tensor_tensor(
+                    out=kk_bf[:, :, dl, :],
+                    in0=ke[c][:, heads, 0:WIDTH, :].rearrange("p h d t -> p h (d t)"),
+                    in1=ke[c][:, heads, dl + 1 : dl + 1 + WIDTH, :].rearrange("p h d t -> p h (d t)"),
+                    op=ALU.mult,
+                )
+            kk_codes = prod.tile([P, HG * SHIFTS * WIDTH], U32, align_bytes=64)
+            kk_planes = prod.tile([P, HG * SHIFTS * WIDTH], U8, align_bytes=64)
+            per_head = SHIFTS * WIDTH
+            for pair in range(HG // 2):
+                cols = slice(2 * pair * per_head, 2 * (pair + 1) * per_head)
+                nc.vector.quantize_mx(
+                    out=kk_codes[:, cols].bitcast(FP8X4),
+                    scales=kk_planes[:, cols],
+                    in_=kk_bf[:, 2 * pair : 2 * pair + 2, :, :].rearrange("p h l e -> p (h l e)"),
+                )
+            vcols = slice(g * P, (g + 1) * P)
+            for hh in range(HG):
+                cols = slice(hh * per_head, (hh + 1) * per_head)
+                nc.tensor.matmul_mx(
+                    out=banks[hh][:],
+                    lhsT=v_codes[c][:, vcols].bitcast(FP8X4),
+                    lhsT_scale=v_planes[c][:, vcols],
+                    rhs=kk_codes[:, cols].bitcast(FP8X4),
+                    rhs_scale=kk_planes[:, cols],
+                    start=(c == 0),
+                    stop=(c == PASSES - 1),
+                )
+            scols = slice(g * 2 * P, (g + 1) * 2 * P)
+            nc.tensor.matmul_mx(
+                out=small_bank[:],
+                lhsT=v_codes[c][:, vcols].bitcast(FP8X4),
+                lhsT_scale=v_planes[c][:, vcols],
+                rhs=sm_codes[c][:, scols].bitcast(FP8X4),
+                rhs_scale=sm_planes[c][:, scols],
+                start=(c == 0),
+                stop=(c == PASSES - 1),
+            )
+
+        def finish(g, banks, small_bank, o_sb):
+            z_skew = z[:].rearrange("p s (i w) -> p s i w", w=WIDTH + 1)
+            z_rows = z[:, :, 0 : HALF * WIDTH].rearrange("p s (i c) -> p s i c", c=WIDTH)
+            full = stage.tile([P, WIDTH * WIDTH + WIDTH], F32, align_bytes=64)
+            full_m = full[:, 0 : WIDTH * WIDTH].rearrange("p (a b) -> p a b", b=WIDTH)
+            full_diag = full[:].rearrange("p (a w) -> p a w", w=WIDTH + 1)
+            for hh in range(HG):
+                q = slice(hh * WIDTH, (hh + 1) * WIDTH)
+                by_row = banks[hh][q, :].rearrange("p (l s i) -> p s i l", l=SHIFTS, s=2)
+                nc.scalar.copy(out=z_skew[q, :, :, 1:SHIFTS], in_=by_row[:, :, :, 0 : SHIFTS - 1])
+                nc.scalar.copy(out=z_skew[q, 0, :, SHIFTS : SHIFTS + 1], in_=by_row[:, 0, :, SHIFTS - 1 : SHIFTS])
+            for s in range(2):
+                rows = slice(s * HALF, (s + 1) * HALF)
+                other = slice((1 - s) * HALF, (2 - s) * HALF)
+                nc.gpsimd.tensor_tensor(
+                    out=full_m[:, rows, rows],
+                    in0=z_rows[:, s, :, 0:HALF],
+                    in1=z_rows[:, s, :, 0:HALF].rearrange("p i c -> p c i"),
+                    op=ALU.add,
+                )
+                nc.gpsimd.tensor_tensor(
+                    out=full_m[:, rows, other],
+                    in0=z_rows[:, s, :, HALF:WIDTH],
+                    in1=z_rows[:, 1 - s, :, HALF:WIDTH].rearrange("p i c -> p c i"),
+                    op=ALU.add,
+                )
+            for hh in range(HG):
+                q = slice(hh * WIDTH, (hh + 1) * WIDTH)
+                nc.scalar.copy(out=full_diag[q, :, 0:1], in_=small_bank[q, q].unsqueeze(2))
+                nc.scalar.copy(
+                    out=full[q, WIDTH * WIDTH : WIDTH * WIDTH + WIDTH],
+                    in_=small_bank[q, P + hh * WIDTH : P + (hh + 1) * WIDTH],
+                )
+            turned = stage.tile([P, WIDTH * WIDTH + WIDTH], F32, align_bytes=64)
+            nc.vector.transpose(out=turned[:, 0 : WIDTH * WIDTH], in_=full[:, 0 : WIDTH * WIDTH])
+            nc.vector.transpose(out=turned[:, WIDTH * WIDTH :], in_=full[:, WIDTH * WIDTH :])
+            nc.scalar.copy(
+                out=o_sb[:, :, 1 : WIDTH + 1],
+                in_=turned[:, 0 : WIDTH * WIDTH].rearrange("p (j e) -> p j e", e=WIDTH),
+            )
+            nc.scalar.copy(out=kv_out[:, g, 1 : WIDTH + 1], in_=turned[:, WIDTH * WIDTH :])
+            nc.sync.dma_start(
+                out=kv_mod[0, g * HG : (g + 1) * HG].rearrange("h i j e -> (h i) (j e)"),
+                in_=o_sb[:].rearrange("p j e -> p (j e)"),
+            )
+
+        for c in range(PASSES):
+            head(c)
+        value_sums()
+        for g in range(GROUPS):
+            o_sb = stage.tile([P, WIDTH, WIDTH + 1], F32, bufs=2)
+            plain_sums(g, o_sb)
+            banks = []
+            for hh in range(HG):
+                banks.append(acc_ps.tile([P, SHIFTS * WIDTH], F32, name="bank%d" % hh))
+            small_bank = acc_ps.tile([P, 2 * P], F32)
+            for c in range(PASSES):
+                unit(g, c, banks, small_bank)
+            finish(g, banks, small_bank, o_sb)
+        nc.sync.dma_start(out=kv[0].rearrange("(g h) d e -> (h d) g e", g=GROUPS), in_=kv_out[:])

@@ -21,9 +21,13 @@ WIDTH = 32
 PASSES = TOKENS // (P * PACK)
 GROUPS = 4
 HG = HEADS // GROUPS
+STEPS = GROUPS * PASSES
 SHIFTS = WIDTH // 2
 EXT = WIDTH + SHIFTS
 HALF = WIDTH // 2
+RUN = WIDTH * PACK
+VECTOR_SHIFTS = 10
+MASK_PITCH = P + WIDTH
 EPS = 1e-12
 SCALE = 32.0 ** 0.25
 
@@ -35,31 +39,19 @@ def tile_taylorsoftmaxattention_pa_kernel(
 ):
     nc = tc.nc
     with ExitStack() as ctx:
+        ctx.enter_context(tc.manual_schedule())
         const = ctx.enter_context(tc.tile_pool(name="const", bufs=1))
-        stage = ctx.enter_context(tc.tile_pool(name="stage", bufs=1))
-        prod = ctx.enter_context(tc.tile_pool(name="prod", bufs=2))
-        aux_ps = ctx.enter_context(tc.psum_pool(name="aux_ps", bufs=3))
+        ring = ctx.enter_context(tc.tile_pool(name="ring", bufs=2))
+        aux_ps = ctx.enter_context(tc.psum_pool(name="aux_ps", bufs=4))
+        kn_pool = ctx.enter_context(tc.psum_pool(name="kn_pool", bufs=2))
         acc_ps = ctx.enter_context(tc.psum_pool(name="acc_ps", bufs=1))
-
-        one_col = const.tile([P, 1], F32)
-        nc.vector.memset(one_col[:], 1.0)
-        warm = const.tile([P, 1], F32)
-        nc.scalar.sqrt(out=warm[:], in_=one_col[:])
-
-        ident = const.tile([P, P], F32)
-        make_identity(nc, ident[:])
-        ones = const.tile([P, P], F32)
-        nc.gpsimd.memset(ones[:], 1.0)
 
         w_words = const.tile([P, 2, FEATURES], U32, align_bytes=64)
         w_planes = const.tile([P, 2, FEATURES], U8, align_bytes=64)
         nc.vector.memset(w_planes[:].rearrange("p w n -> p (w n)").bitcast(I32), 0)
-        z = const.tile([P, 2, HALF * (WIDTH + 1)], F32)
-        nc.vector.memset(z[:], 0.0)
-
         x_sb = []
         for c in range(PASSES):
-            x_sb.append(stage.tile([P, PACK, FEATURES], BF16, name="x_sb%d" % c))
+            x_sb.append(const.tile([P, PACK, FEATURES], BF16, name="x_sb%d" % c))
 
         def load_x(c):
             rows = x[0, c * P * PACK : (c + 1) * P * PACK, :]
@@ -78,48 +70,54 @@ def tile_taylorsoftmaxattention_pa_kernel(
 
         load_x(0)
         load_weight(0, wk_words, wk_scales)
-        load_x(1)
         load_weight(1, wv_words, wv_scales)
-        load_x(2)
-        load_x(3)
+        for c in range(1, PASSES):
+            load_x(c)
 
-        bias_bf = const.tile([P, 2, FEATURES], BF16)
-        nc.scalar.dma_start(out=bias_bf[:, 0, :], in_=bk.partition_broadcast(P))
-        nc.scalar.dma_start(out=bias_bf[:, 1, :], in_=bv.partition_broadcast(P))
-        bk_f = const.tile([P, FEATURES], F32)
-        nc.scalar.copy(out=bk_f[:], in_=bias_bf[:, 0, :])
-        bvn_f = const.tile([P, FEATURES], F32)
-        nc.scalar.mul(out=bvn_f[:], in_=bias_bf[:, 1, :], mul=1.0 / TOKENS)
+        bias_rows = const.tile([P, P], BF16)
+        nc.vector.memset(bias_rows[:], 0.0)
+        nc.scalar.dma_start(out=bias_rows[0:GROUPS, :], in_=bk.rearrange("(g f) -> g f", g=GROUPS))
+        nc.scalar.dma_start(out=bias_rows[GROUPS : 2 * GROUPS, :], in_=bv.rearrange("(g f) -> g f", g=GROUPS))
 
-        x_codes, x_planes, ke, v_codes, v_planes, sm_codes, sm_planes = [], [], [], [], [], [], []
+        one_cols = const.tile([P, PASSES * PACK], F32)
+        nc.vector.memset(one_cols[:], 1.0)
+        warm = const.tile([P, 1], F32)
+        nc.scalar.sqrt(out=warm[:], in_=one_cols[:, 0:1])
+        ident = const.tile([P, P], F32)
+        make_identity(nc, ident[:])
+        ident_bf = const.tile([P, P], BF16)
+        make_identity(nc, ident_bf[:])
+        head_of_row = const.tile([P, HG], F32)
+        nc.gpsimd.memset(head_of_row[:], 0.0)
+        for hh in range(HG):
+            nc.gpsimd.memset(head_of_row[hh * WIDTH : (hh + 1) * WIDTH, hh : hh + 1], 1.0)
+        z = const.tile([P, 2, HALF * (WIDTH + 1)], F32)
+        nc.vector.memset(z[:], 0.0)
+        vs_cols = const.tile([P, PASSES, P], F32)
+        nc.vector.memset(vs_cols[:], 0.0)
+        masked = []
+        for k in range(2):
+            masked.append(const.tile([P, HG * MASK_PITCH], U32, name="masked%d" % k, align_bytes=64))
+            nc.vector.memset(masked[k][:].bitcast(I32), 0)
+        kv_out = const.tile([P, GROUPS, WIDTH + 1], F32)
+
+        bias_t = aux_ps.tile([P, P], BF16, tag="aux")
+        nc.tensor.transpose(bias_t[:], bias_rows[:], ident_bf[:])
+        bias_cols = const.tile([P, 2 * GROUPS], F32)
+        nc.scalar.copy(out=bias_cols[:, 0:GROUPS], in_=bias_t[:, 0:GROUPS])
+        nc.scalar.mul(out=bias_cols[:, GROUPS : 2 * GROUPS], in_=bias_t[:, GROUPS : 2 * GROUPS], mul=1.0 / TOKENS)
+
+        x_codes, x_planes = [], []
         for c in range(PASSES):
             x_codes.append(const.tile([P, FEATURES], U32, name="x_codes%d" % c, align_bytes=64))
             x_planes.append(const.tile([P, FEATURES], U8, name="x_planes%d" % c, align_bytes=64))
-            ke.append(const.tile([P, HEADS, EXT, PACK], F32, name="ke%d" % c))
-            v_codes.append(const.tile([P, FEATURES], U32, name="v_codes%d" % c, align_bytes=64))
-            v_planes.append(const.tile([P, FEATURES], U8, name="v_planes%d" % c, align_bytes=64))
-            sm_codes.append(const.tile([P, 2 * FEATURES], U32, name="sm_codes%d" % c, align_bytes=64))
-            sm_planes.append(const.tile([P, 2 * FEATURES], U8, name="sm_planes%d" % c, align_bytes=64))
 
-        def project(c, g, which):
-            bank = aux_ps.tile([P, PACK, P], F32, tag="aux")
-            cols = slice(g * P, (g + 1) * P)
-            for t in range(PACK):
-                toks = slice(t * P, (t + 1) * P)
-                nc.tensor.matmul_mx(
-                    out=bank[:, t, :],
-                    lhsT=x_codes[c][:, toks].bitcast(FP8X4),
-                    lhsT_scale=x_planes[c][:, toks],
-                    rhs=w_words[:, which, cols].bitcast(FP8X4),
-                    rhs_scale=w_planes[:, which, cols],
-                    start=True,
-                    stop=True,
-                )
-            return bank
+        xg, kb_ps, norm, gain, win, kn_ps, sm_bf, v_bf, knp, o_sb = {}, {}, {}, {}, {}, {}, {}, {}, {}, {}
+        sm_codes, sm_planes, v_codes, v_planes, kk_bf, acc, small_acc, full = {}, {}, {}, {}, {}, {}, {}, {}
 
-        def head(c):
-            xg = stage.tile([P, PACK, P, PACK], BF16, align_bytes=64)
-            xg_words = xg[:].bitcast(F32)
+        def transpose_x(c):
+            xg[c] = ring.tile([P, PACK, P, PACK], BF16, name="xg", align_bytes=64)
+            xg_words = xg[c][:].bitcast(F32)
             for half in range(2):
                 xt = aux_ps.tile([P, 2, 2, P], F32, tag="aux")
                 for s in range(2):
@@ -130,188 +128,220 @@ def tile_taylorsoftmaxattention_pa_kernel(
                     out=xg_words[:, 2 * half : 2 * half + 2, :, :],
                     in_=xt[:].rearrange("q s u p -> q s p u"),
                 )
+
+        def quantise_x(c):
             nc.vector.quantize_mx(
                 out=x_codes[c][:].bitcast(FP8X4),
                 scales=x_planes[c][:],
-                in_=xg[:].rearrange("q t p j -> q (t p j)"),
+                in_=xg[c][:].rearrange("q t p j -> q (t p j)"),
             )
 
-            for g in range(GROUPS):
-                kp = project(c, g, 0)
-                nc.vector.tensor_tensor(
-                    out=ke[c][:, g * HG : (g + 1) * HG, 0:WIDTH, :],
-                    in0=kp[:].rearrange("p t (h d) -> p h d t", h=HG),
-                    in1=bk_f[:, g * P : (g + 1) * P]
-                    .rearrange("p (h d) -> p h d", h=HG)
-                    .unsqueeze(3)
-                    .to_broadcast([P, HG, WIDTH, PACK]),
-                    op=ALU.add,
-                )
-            sq = stage.tile([P, HEADS, WIDTH, PACK], F32)
-            nc.scalar.activation(out=sq[:], in_=ke[c][:, :, 0:WIDTH, :], func=ACT.Square)
-            width = WIDTH // 2
-            while width >= 1:
-                nc.gpsimd.tensor_tensor(
-                    out=sq[:, :, 0:width, :],
-                    in0=sq[:, :, 0:width, :],
-                    in1=sq[:, :, width : 2 * width, :],
-                    op=ALU.add,
-                )
-                width //= 2
-            norm = stage.tile([P, HEADS, PACK], F32, bufs=2)
-            nc.scalar.sqrt(out=norm[:], in_=sq[:, :, 0, :])
-            nc.vector.tensor_scalar(
-                out=norm[:], in0=norm[:], scalar1=EPS, scalar2=1.0 / SCALE, op0=ALU.max, op1=ALU.mult
+        def project_turned(c, g, which):
+            bank = aux_ps.tile([P, PACK * P], F32, tag="aux")
+            cols = slice(g * P, (g + 1) * P)
+            nc.tensor.matmul_mx(
+                out=bank[:],
+                lhsT=w_words[:, which, cols].bitcast(FP8X4),
+                lhsT_scale=w_planes[:, which, cols],
+                rhs=x_codes[c][:].bitcast(FP8X4),
+                rhs_scale=x_planes[c][:],
+                start=True,
+                stop=True,
             )
-            gain = stage.tile([P, HEADS, PACK], F32, bufs=2)
-            nc.vector.reciprocal(out=gain[:], in_=norm[:])
-            nc.gpsimd.tensor_tensor(
-                out=ke[c][:, :, 0:WIDTH, :],
-                in0=ke[c][:, :, 0:WIDTH, :],
-                in1=gain[:].unsqueeze(2).to_broadcast([P, HEADS, WIDTH, PACK]),
-                op=ALU.mult,
-            )
-            nc.scalar.copy(out=ke[c][:, :, WIDTH:EXT, :], in_=ke[c][:, :, 0:SHIFTS, :])
+            return bank
 
-            sm_bf = stage.tile([P, GROUPS, 2, P * PACK], BF16, align_bytes=64)
-            kn_by_group = ke[c][:, :, 0:WIDTH, :].rearrange("p (g h) d t -> p g h (d t)", g=GROUPS)
+        def turn_back(turned):
+            bank = aux_ps.tile([P, PACK, P], F32, tag="aux")
+            for t in range(PACK):
+                nc.tensor.transpose(bank[:, t, :], turned[:, t * P : (t + 1) * P], ident[:])
+            return bank
+
+        def project(s):
+            g, c = divmod(s, PASSES)
+            kt = project_turned(c, g, 0)
+            vt = project_turned(c, g, 1)
+            kb_t = ring.tile([P, PACK * P], F32, name="kb_t")
+            nc.scalar.activation(out=kb_t[:], in_=kt[:], func=ACT.Identity, bias=bias_cols[:, g : g + 1])
+            sq_t = ring.tile([P, PACK * P], F32, name="sq_t")
+            nc.scalar.activation(out=sq_t[:], in_=kt[:], func=ACT.Square, bias=bias_cols[:, g : g + 1])
+            v_t = ring.tile([P, PACK * P], F32, name="v_t")
             nc.scalar.activation(
-                out=sm_bf[:, :, 0, :].rearrange("p g (h e) -> p g h e", h=HG), in_=kn_by_group, func=ACT.Square
+                out=v_t[:],
+                in_=vt[:],
+                func=ACT.Identity,
+                scale=1.0 / TOKENS,
+                bias=bias_cols[:, GROUPS + g : GROUPS + g + 1],
+                accum_out=vs_cols[:, c, g : g + 1],
             )
-            nc.scalar.copy(out=sm_bf[:, :, 1, :].rearrange("p g (h e) -> p g h e", h=HG), in_=kn_by_group)
-
-            v_bf = stage.tile([P, FEATURES, PACK], BF16, align_bytes=64)
-            for g in range(GROUPS):
-                vp = project(c, g, 1)
-                nc.vector.scalar_tensor_tensor(
-                    out=v_bf[:, g * P : (g + 1) * P, :],
-                    in0=vp[:].rearrange("p t f -> p f t"),
-                    scalar=1.0 / TOKENS,
-                    in1=bvn_f[:, g * P : (g + 1) * P].unsqueeze(2).to_broadcast([P, P, PACK]),
-                    op0=ALU.mult,
-                    op1=ALU.add,
+            kb_ps[s] = turn_back(kb_t)
+            ss = aux_ps.tile([P, PACK, HG], F32, tag="aux")
+            for t in range(PACK):
+                nc.tensor.matmul(
+                    out=ss[:, t, :], lhsT=sq_t[:, t * P : (t + 1) * P], rhs=head_of_row[:], start=True, stop=True
                 )
-            nc.vector.quantize_mx(
-                out=v_codes[c][:].bitcast(FP8X4),
-                scales=v_planes[c][:],
-                in_=v_bf[:].rearrange("p f t -> p (f t)"),
-            )
-            nc.vector.quantize_mx(
-                out=sm_codes[c][:].bitcast(FP8X4),
-                scales=sm_planes[c][:],
-                in_=sm_bf[:].rearrange("p g k e -> p (g k e)"),
-            )
+            norm[s] = ring.tile([P, PACK, HG], F32, name="norm", bufs=3)
+            nc.scalar.sqrt(out=norm[s][:], in_=ss[:])
+            v_ps = turn_back(v_t)
+            v_bf[s] = ring.tile([P, P, PACK], BF16, name="v_bf", align_bytes=64, bufs=3)
+            nc.scalar.copy(out=v_bf[s][:], in_=v_ps[:].rearrange("p t f -> p f t"))
+            if s == STEPS - 1:
+                value_sums()
 
         def value_sums():
-            part = aux_ps.tile([P, FEATURES], F32, tag="aux")
+            total = aux_ps.tile([P, P], F32, tag="aux")
             for c in range(PASSES):
-                for t in range(PACK):
-                    toks = slice(t * P, (t + 1) * P)
-                    nc.tensor.matmul_mx(
-                        out=part[:],
-                        lhsT=x_codes[c][:, toks].bitcast(FP8X4),
-                        lhsT_scale=x_planes[c][:, toks],
-                        rhs=w_words[:, 1, :].bitcast(FP8X4),
-                        rhs_scale=w_planes[:, 1, :],
-                        start=(c == 0 and t == 0),
-                        stop=(c == PASSES - 1 and t == PACK - 1),
-                    )
-            part_sb = stage.tile([P, FEATURES], F32)
-            nc.scalar.copy(out=part_sb[:], in_=part[:])
-            total = aux_ps.tile([P, FEATURES], F32, tag="aux")
-            nc.tensor.matmul(out=total[:], lhsT=ones[:], rhs=part_sb[:], start=True, stop=True)
-            vsum_sb = const.tile([1, HEADS, WIDTH + 1], F32)
-            nc.vector.memset(vsum_sb[:, :, 0:1], 1.0)
-            nc.vector.scalar_tensor_tensor(
-                out=vsum_sb[:, :, 1 : WIDTH + 1],
-                in0=total[0:1, :].rearrange("p (h e) -> p h e", h=HEADS),
-                scalar=1.0 / TOKENS,
-                in1=bias_bf[0:1, 1, :].rearrange("p (h e) -> p h e", h=HEADS),
-                op0=ALU.mult,
-                op1=ALU.add,
+                nc.tensor.matmul(
+                    out=total[:], lhsT=vs_cols[:, c, :], rhs=ident[:], start=(c == 0), stop=(c == PASSES - 1)
+                )
+            vsum_sb = const.tile([GROUPS, HG, WIDTH + 1], F32)
+            nc.scalar.copy(out=vsum_sb[:, :, 0:1], in_=one_cols[0:GROUPS, 0:HG].unsqueeze(2))
+            nc.scalar.copy(
+                out=vsum_sb[:, :, 1 : WIDTH + 1], in_=total[0:GROUPS, :].rearrange("g (h e) -> g h e", h=HG)
             )
             nc.sync.dma_start(
-                out=vsum.rearrange("b h o e -> (b o) (h e)"), in_=vsum_sb[:].rearrange("p h e -> p (h e)")
+                out=vsum.rearrange("b (g h) o e -> (b g) (h o e)", g=GROUPS),
+                in_=vsum_sb[:].rearrange("g h e -> g (h e)"),
             )
 
-        kv_out = const.tile([P, GROUPS, WIDTH + 1], F32)
+        def gains(s):
+            nc.vector.tensor_scalar(
+                out=norm[s][:], in0=norm[s][:], scalar1=EPS, scalar2=1.0 / SCALE, op0=ALU.max, op1=ALU.mult
+            )
+            gain[s] = ring.tile([P, PACK, HG], F32, name="gain", bufs=3)
+            nc.vector.reciprocal(out=gain[s][:], in_=norm[s][:])
 
-        def plain_sums(g, o_sb):
-            knp = stage.tile([P, PASSES * PACK, P + 1], F32)
-            nc.scalar.copy(out=knp[:, :, P : P + 1], in_=ones[:, 0 : PASSES * PACK].unsqueeze(2))
-            for c in range(PASSES):
-                nc.scalar.copy(
-                    out=knp[:, c * PACK : (c + 1) * PACK, 0:P].rearrange("p t (h d) -> p t h d", h=HG),
-                    in_=ke[c][:, g * HG : (g + 1) * HG, 0:WIDTH, :].rearrange("p h d t -> p t h d"),
-                )
+        def normalise(s):
+            win[s] = ring.tile([P, 2, HG, EXT, PACK], F32, name="win", bufs=4)
+            nc.vector.tensor_tensor(
+                out=win[s][:, 0, :, 0:WIDTH, :],
+                in0=kb_ps[s][:].rearrange("p t (h d) -> p h d t", h=HG),
+                in1=gain[s][:].rearrange("p t h -> p h t").unsqueeze(2).to_broadcast([P, HG, WIDTH, PACK]),
+                op=ALU.mult,
+            )
+
+        def spread(s):
+            g, c = divmod(s, PASSES)
+            kn = win[s][:, 0, :, 0:WIDTH, :]
+            nc.scalar.copy(out=win[s][:, 0, :, WIDTH:EXT, :], in_=win[s][:, 0, :, 0:SHIFTS, :])
+            nc.scalar.copy(out=win[s][:, 1, :, 0 : EXT - 1, :], in_=win[s][:, 0, :, 1:EXT, :])
+            there = aux_ps.tile([P, HG, P], F32, tag="aux")
+            for hh in range(HG):
+                nc.tensor.transpose(there[:, hh, :], win[s][:, 0, hh, 0:WIDTH, :].rearrange("p d t -> p (d t)"), ident[:])
+            there_sb = ring.tile([P, HG, P], F32, name="there_sb")
+            nc.scalar.copy(out=there_sb[:], in_=there[:])
+            kn_ps[s] = kn_pool.tile([P, HG, RUN], F32, name="kn_ps")
+            for hh in range(HG):
+                nc.tensor.transpose(kn_ps[s][:, hh, :], there_sb[:, hh, :], ident[:])
+            sm_bf[s] = ring.tile([P, 2, HG, RUN], BF16, name="sm_bf", align_bytes=64)
+            by_head = kn.rearrange("p h d t -> p h (d t)")
+            nc.scalar.activation(out=sm_bf[s][:, 0, :, :], in_=by_head, func=ACT.Square)
+            nc.scalar.copy(out=sm_bf[s][:, 1, :, :], in_=by_head)
+            if c == 0:
+                knp[g] = ring.tile([P, PASSES * PACK, P + 1], F32, name="knp")
+                nc.scalar.copy(out=knp[g][:, :, P : P + 1], in_=one_cols[:].unsqueeze(2))
+            nc.scalar.copy(
+                out=knp[g][:, c * PACK : (c + 1) * PACK, 0:P].rearrange("p t (h d) -> p t h d", h=HG),
+                in_=kn.rearrange("p h d t -> p t h d"),
+            )
+
+        def plain_sums(g):
             gram = aux_ps.tile([P, P + 1], F32, tag="aux")
             for s in range(PASSES * PACK):
                 nc.tensor.matmul(
                     out=gram[:],
-                    lhsT=knp[:, s, 0:P],
-                    rhs=knp[:, s, :],
+                    lhsT=knp[g][:, s, 0:P],
+                    rhs=knp[g][:, s, :],
                     start=(s == 0),
                     stop=(s == PASSES * PACK - 1),
                 )
+            o_sb[g] = ring.tile([P, WIDTH, WIDTH + 1], F32, name="o_sb")
             for hh in range(HG):
                 q = slice(hh * WIDTH, (hh + 1) * WIDTH)
-                nc.scalar.mul(out=o_sb[q, :, 0:1], in_=gram[q, q].unsqueeze(2), mul=1.0 / TOKENS)
+                nc.scalar.mul(out=o_sb[g][q, :, 0:1], in_=gram[q, q].unsqueeze(2), mul=1.0 / TOKENS)
             nc.scalar.mul(out=kv_out[:, g, 0:1], in_=gram[:, P : P + 1], mul=1.0 / TOKENS)
 
-        def unit(g, c, banks, small_bank):
-            heads = slice(g * HG, (g + 1) * HG)
-            kk_bf = prod.tile([P, HG, SHIFTS, WIDTH * PACK], BF16, align_bytes=64)
-            for dl in range(SHIFTS):
-                nc.vector.tensor_tensor(
-                    out=kk_bf[:, :, dl, :],
-                    in0=ke[c][:, heads, 0:WIDTH, :].rearrange("p h d t -> p h (d t)"),
-                    in1=ke[c][:, heads, dl + 1 : dl + 1 + WIDTH, :].rearrange("p h d t -> p h (d t)"),
-                    op=ALU.mult,
-                )
-            kk_codes = prod.tile([P, HG * SHIFTS * WIDTH], U32, align_bytes=64)
-            kk_planes = prod.tile([P, HG * SHIFTS * WIDTH], U8, align_bytes=64)
+        def products(s):
+            kk_bf[s] = ring.tile([P, HG, SHIFTS, RUN], BF16, name="kk_bf", align_bytes=64)
+            for first in range(0, SHIFTS, 2):
+                out = kk_bf[s][:, :, first : first + 2, :].rearrange("p h l e -> p l h e")
+                moved = win[s][:, :, :, first + 1 : first + 1 + WIDTH, :].rearrange("p l h d t -> p l h (d t)")
+                if first < VECTOR_SHIFTS:
+                    still = kn_ps[s][:].unsqueeze(1).to_broadcast([P, 2, HG, RUN])
+                    nc.vector.tensor_tensor(out=out, in0=still, in1=moved, op=ALU.mult)
+                else:
+                    still = win[s][:, 0, :, 0:WIDTH, :].rearrange("p h d t -> p h (d t)")
+                    still = still.unsqueeze(1).to_broadcast([P, 2, HG, RUN])
+                    nc.gpsimd.tensor_tensor(out=out, in0=still, in1=moved, op=ALU.mult)
+
+        def quantise_small(s):
+            sm_codes[s] = ring.tile([P, 2 * P], U32, name="sm_codes", align_bytes=64, bufs=3)
+            sm_planes[s] = ring.tile([P, 2 * P], U8, name="sm_planes", align_bytes=64, bufs=3)
+            nc.vector.quantize_mx(
+                out=sm_codes[s][:].bitcast(FP8X4),
+                scales=sm_planes[s][:],
+                in_=sm_bf[s][:].rearrange("p k h e -> p (k h e)"),
+            )
+
+        def quantise_values(s):
+            v_codes[s] = ring.tile([P, P], U32, name="v_codes", align_bytes=64, bufs=3)
+            v_planes[s] = ring.tile([P, P], U8, name="v_planes", align_bytes=64, bufs=3)
+            nc.vector.quantize_mx(
+                out=v_codes[s][:].bitcast(FP8X4),
+                scales=v_planes[s][:],
+                in_=v_bf[s][:].rearrange("p f t -> p (f t)"),
+            )
+
+        def mask_values(s):
+            nc.vector.tensor_copy(
+                out=masked[s % 2][:].bitcast(I32).rearrange("p (h w) -> p h w", w=MASK_PITCH)[:, :, 0:WIDTH],
+                in_=v_codes[s][:].bitcast(I32).rearrange("p (h e) -> p h e", h=HG),
+            )
+
+        def contract(s):
+            g, c = divmod(s, PASSES)
             per_head = SHIFTS * WIDTH
+            kk_codes = ring.tile([P, HG * per_head], U32, name="kk_codes", align_bytes=64)
+            kk_planes = ring.tile([P, HG * per_head], U8, name="kk_planes", align_bytes=64)
             for pair in range(HG // 2):
                 cols = slice(2 * pair * per_head, 2 * (pair + 1) * per_head)
                 nc.vector.quantize_mx(
                     out=kk_codes[:, cols].bitcast(FP8X4),
                     scales=kk_planes[:, cols],
-                    in_=kk_bf[:, 2 * pair : 2 * pair + 2, :, :].rearrange("p h l e -> p (h l e)"),
+                    in_=kk_bf[s][:, 2 * pair : 2 * pair + 2, :, :].rearrange("p h l e -> p (h l e)"),
                 )
-            vcols = slice(g * P, (g + 1) * P)
+            if c == 0:
+                acc[g] = acc_ps.tile([P, per_head], F32, name="acc")
+                small_acc[g] = acc_ps.tile([P, 2 * P], F32, name="small_acc")
             for hh in range(HG):
                 cols = slice(hh * per_head, (hh + 1) * per_head)
                 nc.tensor.matmul_mx(
-                    out=banks[hh][:],
-                    lhsT=v_codes[c][:, vcols].bitcast(FP8X4),
-                    lhsT_scale=v_planes[c][:, vcols],
+                    out=acc[g][:],
+                    lhsT=masked[s % 2][:, hh * P : (hh + 1) * P].bitcast(FP8X4),
+                    lhsT_scale=v_planes[s][:],
                     rhs=kk_codes[:, cols].bitcast(FP8X4),
                     rhs_scale=kk_planes[:, cols],
-                    start=(c == 0),
-                    stop=(c == PASSES - 1),
+                    start=(c == 0 and hh == 0),
+                    stop=(c == PASSES - 1 and hh == HG - 1),
                 )
-            scols = slice(g * 2 * P, (g + 1) * 2 * P)
             nc.tensor.matmul_mx(
-                out=small_bank[:],
-                lhsT=v_codes[c][:, vcols].bitcast(FP8X4),
-                lhsT_scale=v_planes[c][:, vcols],
-                rhs=sm_codes[c][:, scols].bitcast(FP8X4),
-                rhs_scale=sm_planes[c][:, scols],
+                out=small_acc[g][:],
+                lhsT=v_codes[s][:].bitcast(FP8X4),
+                lhsT_scale=v_planes[s][:],
+                rhs=sm_codes[s][:].bitcast(FP8X4),
+                rhs_scale=sm_planes[s][:],
                 start=(c == 0),
                 stop=(c == PASSES - 1),
             )
 
-        def finish(g, banks, small_bank, o_sb):
+        def unfold(g):
             z_skew = z[:].rearrange("p s (i w) -> p s i w", w=WIDTH + 1)
             z_rows = z[:, :, 0 : HALF * WIDTH].rearrange("p s (i c) -> p s i c", c=WIDTH)
-            full = stage.tile([P, WIDTH * WIDTH + WIDTH], F32, align_bytes=64)
-            full_m = full[:, 0 : WIDTH * WIDTH].rearrange("p (a b) -> p a b", b=WIDTH)
-            full_diag = full[:].rearrange("p (a w) -> p a w", w=WIDTH + 1)
-            for hh in range(HG):
-                q = slice(hh * WIDTH, (hh + 1) * WIDTH)
-                by_row = banks[hh][q, :].rearrange("p (l s i) -> p s i l", l=SHIFTS, s=2)
-                nc.scalar.copy(out=z_skew[q, :, :, 1:SHIFTS], in_=by_row[:, :, :, 0 : SHIFTS - 1])
-                nc.scalar.copy(out=z_skew[q, 0, :, SHIFTS : SHIFTS + 1], in_=by_row[:, 0, :, SHIFTS - 1 : SHIFTS])
+            by_row = acc[g][:].rearrange("p (l s i) -> p s i l", l=SHIFTS, s=2)
+            nc.scalar.copy(out=z_skew[:, :, :, 1:SHIFTS], in_=by_row[:, :, :, 0 : SHIFTS - 1])
+            nc.scalar.copy(out=z_skew[:, 0, :, SHIFTS : SHIFTS + 1], in_=by_row[:, 0, :, SHIFTS - 1 : SHIFTS])
+            full[g] = ring.tile([P, WIDTH * WIDTH + WIDTH], F32, name="full", align_bytes=64, bufs=1)
+            full_m = full[g][:, 0 : WIDTH * WIDTH].rearrange("p (a b) -> p a b", b=WIDTH)
+            full_diag = full[g][:].rearrange("p (a w) -> p a w", w=WIDTH + 1)
             for s in range(2):
                 rows = slice(s * HALF, (s + 1) * HALF)
                 other = slice((1 - s) * HALF, (2 - s) * HALF)
@@ -329,35 +359,47 @@ def tile_taylorsoftmaxattention_pa_kernel(
                 )
             for hh in range(HG):
                 q = slice(hh * WIDTH, (hh + 1) * WIDTH)
-                nc.scalar.copy(out=full_diag[q, :, 0:1], in_=small_bank[q, q].unsqueeze(2))
+                nc.scalar.copy(out=full_diag[q, :, 0:1], in_=small_acc[g][q, q].unsqueeze(2))
                 nc.scalar.copy(
-                    out=full[q, WIDTH * WIDTH : WIDTH * WIDTH + WIDTH],
-                    in_=small_bank[q, P + hh * WIDTH : P + (hh + 1) * WIDTH],
+                    out=full[g][q, WIDTH * WIDTH : WIDTH * WIDTH + WIDTH],
+                    in_=small_acc[g][q, P + hh * WIDTH : P + (hh + 1) * WIDTH],
                 )
-            turned = stage.tile([P, WIDTH * WIDTH + WIDTH], F32, align_bytes=64)
-            nc.vector.transpose(out=turned[:, 0 : WIDTH * WIDTH], in_=full[:, 0 : WIDTH * WIDTH])
-            nc.vector.transpose(out=turned[:, WIDTH * WIDTH :], in_=full[:, WIDTH * WIDTH :])
+
+        def store(g):
+            turned = ring.tile([P, WIDTH * WIDTH + WIDTH], F32, name="turned", align_bytes=64, bufs=1)
+            nc.vector.transpose(out=turned[:, 0 : WIDTH * WIDTH], in_=full[g][:, 0 : WIDTH * WIDTH])
+            nc.vector.transpose(out=turned[:, WIDTH * WIDTH :], in_=full[g][:, WIDTH * WIDTH :])
             nc.scalar.copy(
-                out=o_sb[:, :, 1 : WIDTH + 1],
+                out=o_sb[g][:, :, 1 : WIDTH + 1],
                 in_=turned[:, 0 : WIDTH * WIDTH].rearrange("p (j e) -> p j e", e=WIDTH),
             )
             nc.scalar.copy(out=kv_out[:, g, 1 : WIDTH + 1], in_=turned[:, WIDTH * WIDTH :])
             nc.sync.dma_start(
                 out=kv_mod[0, g * HG : (g + 1) * HG].rearrange("h i j e -> (h i) (j e)"),
-                in_=o_sb[:].rearrange("p j e -> p (j e)"),
+                in_=o_sb[g][:].rearrange("p j e -> p (j e)"),
             )
 
-        for c in range(PASSES):
-            head(c)
-        value_sums()
-        for g in range(GROUPS):
-            o_sb = stage.tile([P, WIDTH, WIDTH + 1], F32, bufs=2)
-            plain_sums(g, o_sb)
-            banks = []
-            for hh in range(HG):
-                banks.append(acc_ps.tile([P, SHIFTS * WIDTH], F32, name="bank%d" % hh))
-            small_bank = acc_ps.tile([P, 2 * P], F32)
-            for c in range(PASSES):
-                unit(g, c, banks, small_bank)
-            finish(g, banks, small_bank, o_sb)
+        def at(stage, step, count):
+            if 0 <= step < count:
+                stage(step)
+
+        def at_group_end(stage, step):
+            if 0 <= step < STEPS and step % PASSES == PASSES - 1:
+                stage(step // PASSES)
+
+        for s in range(-3, STEPS + 1):
+            at_group_end(unfold, s - 1)
+            at(transpose_x, s + 3, PASSES)
+            at(project, s + 2, STEPS)
+            at(spread, s + 1, STEPS)
+            at_group_end(plain_sums, s)
+            at(products, s, STEPS)
+            at(gains, s + 2, STEPS)
+            at(quantise_small, s + 1, STEPS)
+            at(normalise, s + 2, STEPS)
+            at(quantise_values, s + 1, STEPS)
+            at(quantise_x, s + 3, PASSES)
+            at(mask_values, s + 1, STEPS)
+            at_group_end(store, s - 1)
+            at(contract, s, STEPS)
         nc.sync.dma_start(out=kv[0].rearrange("(g h) d e -> (h d) g e", g=GROUPS), in_=kv_out[:])

@@ -26,7 +26,7 @@ SHIFTS = WIDTH // 2
 EXT = WIDTH + SHIFTS
 HALF = WIDTH // 2
 RUN = WIDTH * PACK
-VECTOR_SHIFTS = 10
+VECTOR_SHIFTS = 11
 MASK_PITCH = P + WIDTH
 EPS = 1e-12
 SCALE = 32.0 ** 0.25
@@ -42,7 +42,8 @@ def tile_taylorsoftmaxattention_pa_kernel(
         ctx.enter_context(tc.manual_schedule())
         const = ctx.enter_context(tc.tile_pool(name="const", bufs=1))
         ring = ctx.enter_context(tc.tile_pool(name="ring", bufs=2))
-        aux_ps = ctx.enter_context(tc.psum_pool(name="aux_ps", bufs=4))
+        aux_ps = ctx.enter_context(tc.psum_pool(name="aux_ps", bufs=2))
+        kb_pool = ctx.enter_context(tc.psum_pool(name="kb_pool", bufs=2))
         kn_pool = ctx.enter_context(tc.psum_pool(name="kn_pool", bufs=2))
         acc_ps = ctx.enter_context(tc.psum_pool(name="acc_ps", bufs=1))
 
@@ -150,8 +151,7 @@ def tile_taylorsoftmaxattention_pa_kernel(
             )
             return bank
 
-        def turn_back(turned):
-            bank = aux_ps.tile([P, PACK, P], F32, tag="aux")
+        def turn_back(turned, bank):
             for t in range(PACK):
                 nc.tensor.transpose(bank[:, t, :], turned[:, t * P : (t + 1) * P], ident[:])
             return bank
@@ -173,7 +173,7 @@ def tile_taylorsoftmaxattention_pa_kernel(
                 bias=bias_cols[:, GROUPS + g : GROUPS + g + 1],
                 accum_out=vs_cols[:, c, g : g + 1],
             )
-            kb_ps[s] = turn_back(kb_t)
+            kb_ps[s] = turn_back(kb_t, kb_pool.tile([P, PACK, P], F32, name="kb_ps"))
             ss = aux_ps.tile([P, PACK, HG], F32, tag="aux")
             for t in range(PACK):
                 nc.tensor.matmul(
@@ -181,7 +181,7 @@ def tile_taylorsoftmaxattention_pa_kernel(
                 )
             norm[s] = ring.tile([P, PACK, HG], F32, name="norm", bufs=3)
             nc.scalar.sqrt(out=norm[s][:], in_=ss[:])
-            v_ps = turn_back(v_t)
+            v_ps = turn_back(v_t, aux_ps.tile([P, PACK, P], F32, name="v_ps", tag="aux"))
             v_bf[s] = ring.tile([P, P, PACK], BF16, name="v_bf", align_bytes=64, bufs=3)
             nc.scalar.copy(out=v_bf[s][:], in_=v_ps[:].rearrange("p t f -> p f t"))
             if s == STEPS - 1:
@@ -203,17 +203,19 @@ def tile_taylorsoftmaxattention_pa_kernel(
                 in_=vsum_sb[:].rearrange("g h e -> g (h e)"),
             )
 
-        def gains(s):
+        def clamp_norms(s):
             nc.vector.tensor_scalar(
                 out=norm[s][:], in0=norm[s][:], scalar1=EPS, scalar2=1.0 / SCALE, op0=ALU.max, op1=ALU.mult
             )
+
+        def gains(s):
             gain[s] = ring.tile([P, PACK, HG], F32, name="gain", bufs=3)
             nc.vector.reciprocal(out=gain[s][:], in_=norm[s][:])
 
         def normalise(s):
-            win[s] = ring.tile([P, 2, HG, EXT, PACK], F32, name="win", bufs=4)
+            win[s] = ring.tile([P, HG, EXT, PACK], F32, name="win", bufs=4)
             nc.vector.tensor_tensor(
-                out=win[s][:, 0, :, 0:WIDTH, :],
+                out=win[s][:, :, 0:WIDTH, :],
                 in0=kb_ps[s][:].rearrange("p t (h d) -> p h d t", h=HG),
                 in1=gain[s][:].rearrange("p t h -> p h t").unsqueeze(2).to_broadcast([P, HG, WIDTH, PACK]),
                 op=ALU.mult,
@@ -221,21 +223,20 @@ def tile_taylorsoftmaxattention_pa_kernel(
 
         def spread(s):
             g, c = divmod(s, PASSES)
-            kn = win[s][:, 0, :, 0:WIDTH, :]
-            nc.scalar.copy(out=win[s][:, 0, :, WIDTH:EXT, :], in_=win[s][:, 0, :, 0:SHIFTS, :])
-            nc.scalar.copy(out=win[s][:, 1, :, 0 : EXT - 1, :], in_=win[s][:, 0, :, 1:EXT, :])
+            kn = win[s][:, :, 0:WIDTH, :]
+            by_head = kn.rearrange("p h d t -> p h (d t)")
             there = aux_ps.tile([P, HG, P], F32, tag="aux")
             for hh in range(HG):
-                nc.tensor.transpose(there[:, hh, :], win[s][:, 0, hh, 0:WIDTH, :].rearrange("p d t -> p (d t)"), ident[:])
+                nc.tensor.transpose(there[:, hh, :], by_head[:, hh, :], ident[:])
+            sm_bf[s] = ring.tile([P, 2, HG, RUN], BF16, name="sm_bf", align_bytes=64)
+            nc.scalar.activation(out=sm_bf[s][:, 0, :, :], in_=by_head, func=ACT.Square)
+            nc.scalar.copy(out=sm_bf[s][:, 1, :, :], in_=by_head)
             there_sb = ring.tile([P, HG, P], F32, name="there_sb")
             nc.scalar.copy(out=there_sb[:], in_=there[:])
             kn_ps[s] = kn_pool.tile([P, HG, RUN], F32, name="kn_ps")
             for hh in range(HG):
                 nc.tensor.transpose(kn_ps[s][:, hh, :], there_sb[:, hh, :], ident[:])
-            sm_bf[s] = ring.tile([P, 2, HG, RUN], BF16, name="sm_bf", align_bytes=64)
-            by_head = kn.rearrange("p h d t -> p h (d t)")
-            nc.scalar.activation(out=sm_bf[s][:, 0, :, :], in_=by_head, func=ACT.Square)
-            nc.scalar.copy(out=sm_bf[s][:, 1, :, :], in_=by_head)
+            nc.scalar.copy(out=win[s][:, :, WIDTH:EXT, :], in_=win[s][:, :, 0:SHIFTS, :])
             if c == 0:
                 knp[g] = ring.tile([P, PASSES * PACK, P + 1], F32, name="knp")
                 nc.scalar.copy(out=knp[g][:, :, P : P + 1], in_=one_cols[:].unsqueeze(2))
@@ -262,16 +263,13 @@ def tile_taylorsoftmaxattention_pa_kernel(
 
         def products(s):
             kk_bf[s] = ring.tile([P, HG, SHIFTS, RUN], BF16, name="kk_bf", align_bytes=64)
-            for first in range(0, SHIFTS, 2):
-                out = kk_bf[s][:, :, first : first + 2, :].rearrange("p h l e -> p l h e")
-                moved = win[s][:, :, :, first + 1 : first + 1 + WIDTH, :].rearrange("p l h d t -> p l h (d t)")
-                if first < VECTOR_SHIFTS:
-                    still = kn_ps[s][:].unsqueeze(1).to_broadcast([P, 2, HG, RUN])
-                    nc.vector.tensor_tensor(out=out, in0=still, in1=moved, op=ALU.mult)
+            for dl in range(SHIFTS):
+                moved = win[s][:, :, dl + 1 : dl + 1 + WIDTH, :].rearrange("p h d t -> p h (d t)")
+                if dl < VECTOR_SHIFTS:
+                    nc.vector.tensor_tensor(out=kk_bf[s][:, :, dl, :], in0=kn_ps[s][:], in1=moved, op=ALU.mult)
                 else:
-                    still = win[s][:, 0, :, 0:WIDTH, :].rearrange("p h d t -> p h (d t)")
-                    still = still.unsqueeze(1).to_broadcast([P, 2, HG, RUN])
-                    nc.gpsimd.tensor_tensor(out=out, in0=still, in1=moved, op=ALU.mult)
+                    still = win[s][:, :, 0:WIDTH, :].rearrange("p h d t -> p h (d t)")
+                    nc.gpsimd.tensor_tensor(out=kk_bf[s][:, :, dl, :], in0=still, in1=moved, op=ALU.mult)
 
         def quantise_small(s):
             sm_codes[s] = ring.tile([P, 2 * P], U32, name="sm_codes", align_bytes=64, bufs=3)
@@ -341,7 +339,6 @@ def tile_taylorsoftmaxattention_pa_kernel(
             nc.scalar.copy(out=z_skew[:, 0, :, SHIFTS : SHIFTS + 1], in_=by_row[:, 0, :, SHIFTS - 1 : SHIFTS])
             full[g] = ring.tile([P, WIDTH * WIDTH + WIDTH], F32, name="full", align_bytes=64, bufs=1)
             full_m = full[g][:, 0 : WIDTH * WIDTH].rearrange("p (a b) -> p a b", b=WIDTH)
-            full_diag = full[g][:].rearrange("p (a w) -> p a w", w=WIDTH + 1)
             for s in range(2):
                 rows = slice(s * HALF, (s + 1) * HALF)
                 other = slice((1 - s) * HALF, (2 - s) * HALF)
@@ -357,6 +354,9 @@ def tile_taylorsoftmaxattention_pa_kernel(
                     in1=z_rows[:, 1 - s, :, HALF:WIDTH].rearrange("p i c -> p c i"),
                     op=ALU.add,
                 )
+
+        def fill_diagonal(g):
+            full_diag = full[g][:].rearrange("p (a w) -> p a w", w=WIDTH + 1)
             for hh in range(HG):
                 q = slice(hh * WIDTH, (hh + 1) * WIDTH)
                 nc.scalar.copy(out=full_diag[q, :, 0:1], in_=small_acc[g][q, q].unsqueeze(2))
@@ -387,18 +387,20 @@ def tile_taylorsoftmaxattention_pa_kernel(
             if 0 <= step < STEPS and step % PASSES == PASSES - 1:
                 stage(step // PASSES)
 
-        for s in range(-3, STEPS + 1):
+        for s in range(-4, STEPS + 1):
             at_group_end(unfold, s - 1)
-            at(transpose_x, s + 3, PASSES)
-            at(project, s + 2, STEPS)
             at(spread, s + 1, STEPS)
             at_group_end(plain_sums, s)
+            at_group_end(fill_diagonal, s - 1)
+            at(transpose_x, s + 4, PASSES)
+            at(project, s + 3, STEPS)
             at(products, s, STEPS)
-            at(gains, s + 2, STEPS)
+            at(clamp_norms, s + 2, STEPS)
             at(quantise_small, s + 1, STEPS)
-            at(normalise, s + 2, STEPS)
+            at(gains, s + 2, STEPS)
             at(quantise_values, s + 1, STEPS)
-            at(quantise_x, s + 3, PASSES)
+            at(normalise, s + 2, STEPS)
+            at(quantise_x, s + 4, PASSES)
             at(mask_values, s + 1, STEPS)
             at_group_end(store, s - 1)
             at(contract, s, STEPS)

@@ -26,7 +26,8 @@ SHIFTS = WIDTH // 2
 EXT = WIDTH + SHIFTS
 HALF = WIDTH // 2
 RUN = WIDTH * PACK
-VECTOR_SHIFTS = 11
+COPIES = 4
+VECTOR_SHIFTS = 10
 MASK_PITCH = P + WIDTH
 EPS = 1e-12
 SCALE = 32.0 ** 0.25
@@ -179,8 +180,12 @@ def tile_taylorsoftmaxattention_pa_kernel(
                 nc.tensor.matmul(
                     out=ss[:, t, :], lhsT=sq_t[:, t * P : (t + 1) * P], rhs=head_of_row[:], start=True, stop=True
                 )
+            above = ring.tile([P, PACK, HG], F32, name="above")
+            nc.scalar.activation(out=above[:], in_=ss[:], func=ACT.Relu, bias=-EPS * EPS)
             norm[s] = ring.tile([P, PACK, HG], F32, name="norm", bufs=3)
-            nc.scalar.sqrt(out=norm[s][:], in_=ss[:])
+            nc.scalar.activation(
+                out=norm[s][:], in_=above[:], func=ACT.Sqrt, scale=1.0 / (SCALE * SCALE), bias=EPS * EPS / (SCALE * SCALE)
+            )
             v_ps = turn_back(v_t, aux_ps.tile([P, PACK, P], F32, name="v_ps", tag="aux"))
             v_bf[s] = ring.tile([P, P, PACK], BF16, name="v_bf", align_bytes=64, bufs=3)
             nc.scalar.copy(out=v_bf[s][:], in_=v_ps[:].rearrange("p t f -> p f t"))
@@ -203,19 +208,14 @@ def tile_taylorsoftmaxattention_pa_kernel(
                 in_=vsum_sb[:].rearrange("g h e -> g (h e)"),
             )
 
-        def clamp_norms(s):
-            nc.vector.tensor_scalar(
-                out=norm[s][:], in0=norm[s][:], scalar1=EPS, scalar2=1.0 / SCALE, op0=ALU.max, op1=ALU.mult
-            )
-
         def gains(s):
             gain[s] = ring.tile([P, PACK, HG], F32, name="gain", bufs=3)
             nc.vector.reciprocal(out=gain[s][:], in_=norm[s][:])
 
         def normalise(s):
-            win[s] = ring.tile([P, HG, EXT, PACK], F32, name="win", bufs=4)
+            win[s] = ring.tile([P, COPIES, HG, EXT, PACK], F32, name="win", bufs=4)
             nc.vector.tensor_tensor(
-                out=win[s][:, :, 0:WIDTH, :],
+                out=win[s][:, 0, :, 0:WIDTH, :],
                 in0=kb_ps[s][:].rearrange("p t (h d) -> p h d t", h=HG),
                 in1=gain[s][:].rearrange("p t h -> p h t").unsqueeze(2).to_broadcast([P, HG, WIDTH, PACK]),
                 op=ALU.mult,
@@ -223,8 +223,12 @@ def tile_taylorsoftmaxattention_pa_kernel(
 
         def spread(s):
             g, c = divmod(s, PASSES)
-            kn = win[s][:, :, 0:WIDTH, :]
+            kn = win[s][:, 0, :, 0:WIDTH, :]
             by_head = kn.rearrange("p h d t -> p h (d t)")
+            nc.scalar.copy(out=win[s][:, 0, :, WIDTH:EXT, :], in_=win[s][:, 0, :, 0:SHIFTS, :])
+            kept = EXT - COPIES + 1
+            for l in range(1, COPIES):
+                nc.sync.dma_start(out=win[s][:, l, :, 0:kept, :], in_=win[s][:, 0, :, l : l + kept, :])
             there = aux_ps.tile([P, HG, P], F32, tag="aux")
             for hh in range(HG):
                 nc.tensor.transpose(there[:, hh, :], by_head[:, hh, :], ident[:])
@@ -236,7 +240,6 @@ def tile_taylorsoftmaxattention_pa_kernel(
             kn_ps[s] = kn_pool.tile([P, HG, RUN], F32, name="kn_ps")
             for hh in range(HG):
                 nc.tensor.transpose(kn_ps[s][:, hh, :], there_sb[:, hh, :], ident[:])
-            nc.scalar.copy(out=win[s][:, :, WIDTH:EXT, :], in_=win[s][:, :, 0:SHIFTS, :])
             if c == 0:
                 knp[g] = ring.tile([P, PASSES * PACK, P + 1], F32, name="knp")
                 nc.scalar.copy(out=knp[g][:, :, P : P + 1], in_=one_cols[:].unsqueeze(2))
@@ -263,13 +266,19 @@ def tile_taylorsoftmaxattention_pa_kernel(
 
         def products(s):
             kk_bf[s] = ring.tile([P, HG, SHIFTS, RUN], BF16, name="kk_bf", align_bytes=64)
-            for dl in range(SHIFTS):
-                moved = win[s][:, :, dl + 1 : dl + 1 + WIDTH, :].rearrange("p h d t -> p h (d t)")
-                if dl < VECTOR_SHIFTS:
-                    nc.vector.tensor_tensor(out=kk_bf[s][:, :, dl, :], in0=kn_ps[s][:], in1=moved, op=ALU.mult)
-                else:
-                    still = win[s][:, :, 0:WIDTH, :].rearrange("p h d t -> p h (d t)")
-                    nc.gpsimd.tensor_tensor(out=kk_bf[s][:, :, dl, :], in0=still, in1=moved, op=ALU.mult)
+            for first in range(0, SHIFTS, COPIES):
+                out = kk_bf[s][:, :, first : first + COPIES, :].rearrange("p h l e -> p l h e")
+                moved = win[s][:, :, :, first + 1 : first + 1 + WIDTH, :].rearrange("p l h d t -> p l h (d t)")
+                mine = min(max(VECTOR_SHIFTS - first, 0), COPIES)
+                if mine > 0:
+                    still = kn_ps[s][:].unsqueeze(1).to_broadcast([P, mine, HG, RUN])
+                    nc.vector.tensor_tensor(out=out[:, 0:mine], in0=still, in1=moved[:, 0:mine], op=ALU.mult)
+                if mine < COPIES:
+                    still = win[s][:, 0, :, 0:WIDTH, :].rearrange("p h d t -> p h (d t)")
+                    still = still.unsqueeze(1).to_broadcast([P, COPIES - mine, HG, RUN])
+                    nc.gpsimd.tensor_tensor(
+                        out=out[:, mine:COPIES], in0=still, in1=moved[:, mine:COPIES], op=ALU.mult
+                    )
 
         def quantise_small(s):
             sm_codes[s] = ring.tile([P, 2 * P], U32, name="sm_codes", align_bytes=64, bufs=3)
@@ -337,6 +346,13 @@ def tile_taylorsoftmaxattention_pa_kernel(
             by_row = acc[g][:].rearrange("p (l s i) -> p s i l", l=SHIFTS, s=2)
             nc.scalar.copy(out=z_skew[:, :, :, 1:SHIFTS], in_=by_row[:, :, :, 0 : SHIFTS - 1])
             nc.scalar.copy(out=z_skew[:, 0, :, SHIFTS : SHIFTS + 1], in_=by_row[:, 0, :, SHIFTS - 1 : SHIFTS])
+            for hh in range(HG):
+                q = slice(hh * WIDTH, (hh + 1) * WIDTH)
+                nc.scalar.mul(
+                    out=z_skew[q, :, :, 0:1],
+                    in_=small_acc[g][q, q].rearrange("p (s i) -> p s i", s=2).unsqueeze(3),
+                    mul=0.5,
+                )
             full[g] = ring.tile([P, WIDTH * WIDTH + WIDTH], F32, name="full", align_bytes=64, bufs=1)
             full_m = full[g][:, 0 : WIDTH * WIDTH].rearrange("p (a b) -> p a b", b=WIDTH)
             for s in range(2):
@@ -355,11 +371,8 @@ def tile_taylorsoftmaxattention_pa_kernel(
                     op=ALU.add,
                 )
 
-        def fill_diagonal(g):
-            full_diag = full[g][:].rearrange("p (a w) -> p a w", w=WIDTH + 1)
             for hh in range(HG):
                 q = slice(hh * WIDTH, (hh + 1) * WIDTH)
-                nc.scalar.copy(out=full_diag[q, :, 0:1], in_=small_acc[g][q, q].unsqueeze(2))
                 nc.scalar.copy(
                     out=full[g][q, WIDTH * WIDTH : WIDTH * WIDTH + WIDTH],
                     in_=small_acc[g][q, P + hh * WIDTH : P + (hh + 1) * WIDTH],
@@ -391,13 +404,11 @@ def tile_taylorsoftmaxattention_pa_kernel(
             at_group_end(unfold, s - 1)
             at(spread, s + 1, STEPS)
             at_group_end(plain_sums, s)
-            at_group_end(fill_diagonal, s - 1)
             at(transpose_x, s + 4, PASSES)
             at(project, s + 3, STEPS)
             at(products, s, STEPS)
-            at(clamp_norms, s + 2, STEPS)
-            at(quantise_small, s + 1, STEPS)
             at(gains, s + 2, STEPS)
+            at(quantise_small, s + 1, STEPS)
             at(quantise_values, s + 1, STEPS)
             at(normalise, s + 2, STEPS)
             at(quantise_x, s + 4, PASSES)

@@ -27,7 +27,7 @@ EXT = WIDTH + SHIFTS
 HALF = WIDTH // 2
 RUN = WIDTH * PACK
 COPIES = 4
-VECTOR_SHIFTS = 10
+VECTOR_SHIFTS = 11
 MASK_PITCH = P + WIDTH
 EPS = 1e-12
 SCALE = 32.0 ** 0.25
@@ -265,7 +265,7 @@ def tile_taylorsoftmaxattention_pa_kernel(
             nc.scalar.mul(out=kv_out[:, g, 0:1], in_=gram[:, P : P + 1], mul=1.0 / TOKENS)
 
         def products(s):
-            kk_bf[s] = ring.tile([P, HG, SHIFTS, RUN], BF16, name="kk_bf", align_bytes=64)
+            kk_bf[s] = ring.tile([P, HG, SHIFTS, RUN], BF16, name="kk_bf", align_bytes=64, bufs=1)
             for first in range(0, SHIFTS, COPIES):
                 out = kk_bf[s][:, :, first : first + COPIES, :].rearrange("p h l e -> p l h e")
                 moved = win[s][:, :, :, first + 1 : first + 1 + WIDTH, :].rearrange("p l h d t -> p l h (d t)")
@@ -299,7 +299,7 @@ def tile_taylorsoftmaxattention_pa_kernel(
             )
 
         def mask_values(s):
-            nc.vector.tensor_copy(
+            nc.sync.dma_start(
                 out=masked[s % 2][:].bitcast(I32).rearrange("p (h w) -> p h w", w=MASK_PITCH)[:, :, 0:WIDTH],
                 in_=v_codes[s][:].bitcast(I32).rearrange("p (h e) -> p h e", h=HG),
             )
@@ -406,13 +406,13 @@ def tile_taylorsoftmaxattention_pa_kernel(
             at_group_end(plain_sums, s)
             at(transpose_x, s + 4, PASSES)
             at(project, s + 3, STEPS)
-            at(products, s, STEPS)
             at(gains, s + 2, STEPS)
+            at(products, s, STEPS)
+            at(normalise, s + 2, STEPS)
             at(quantise_small, s + 1, STEPS)
             at(quantise_values, s + 1, STEPS)
-            at(normalise, s + 2, STEPS)
-            at(quantise_x, s + 4, PASSES)
             at(mask_values, s + 1, STEPS)
+            at(quantise_x, s + 4, PASSES)
             at_group_end(store, s - 1)
             at(contract, s, STEPS)
         nc.sync.dma_start(out=kv[0].rearrange("(g h) d e -> (h d) g e", g=GROUPS), in_=kv_out[:])

@@ -27,7 +27,7 @@ EXT = WIDTH + SHIFTS
 HALF = WIDTH // 2
 RUN = WIDTH * PACK
 COPIES = 4
-VECTOR_SHIFTS = 11
+VECTOR_SHIFTS = 10
 MASK_PITCH = P + WIDTH
 EPS = 1e-12
 SCALE = 32.0 ** 0.25
@@ -84,7 +84,7 @@ def tile_taylorsoftmaxattention_pa_kernel(
         one_cols = const.tile([P, PASSES * PACK], F32)
         nc.vector.memset(one_cols[:], 1.0)
         warm = const.tile([P, 1], F32)
-        nc.scalar.sqrt(out=warm[:], in_=one_cols[:, 0:1])
+        nc.scalar.activation(out=warm[:], in_=one_cols[:, 0:1], func=ACT.Abs_reciprocal_sqrt)
         ident = const.tile([P, P], F32)
         make_identity(nc, ident[:])
         ident_bf = const.tile([P, P], BF16)
@@ -114,7 +114,7 @@ def tile_taylorsoftmaxattention_pa_kernel(
             x_codes.append(const.tile([P, FEATURES], U32, name="x_codes%d" % c, align_bytes=64))
             x_planes.append(const.tile([P, FEATURES], U8, name="x_planes%d" % c, align_bytes=64))
 
-        xg, kb_ps, norm, gain, win, kn_ps, sm_bf, v_bf, knp, o_sb = {}, {}, {}, {}, {}, {}, {}, {}, {}, {}
+        xg, kb_ps, gain, win, kn_ps, sm_bf, v_bf, knp, o_sb = {}, {}, {}, {}, {}, {}, {}, {}, {}
         sm_codes, sm_planes, v_codes, v_planes, kk_bf, acc, small_acc, full = {}, {}, {}, {}, {}, {}, {}, {}
 
         def transpose_x(c):
@@ -126,7 +126,7 @@ def tile_taylorsoftmaxattention_pa_kernel(
                     words = x_sb[c][:, 2 * half + s, :].bitcast(F32)
                     for u in range(2):
                         nc.tensor.transpose(xt[:, s, u, :], words[:, u : FEATURES // 2 : 2], ident[:])
-                nc.scalar.copy(
+                nc.vector.tensor_copy(
                     out=xg_words[:, 2 * half : 2 * half + 2, :, :],
                     in_=xt[:].rearrange("q s u p -> q s p u"),
                 )
@@ -157,14 +157,33 @@ def tile_taylorsoftmaxattention_pa_kernel(
                 nc.tensor.transpose(bank[:, t, :], turned[:, t * P : (t + 1) * P], ident[:])
             return bank
 
-        def project(s):
+        def keys(s):
             g, c = divmod(s, PASSES)
             kt = project_turned(c, g, 0)
-            vt = project_turned(c, g, 1)
             kb_t = ring.tile([P, PACK * P], F32, name="kb_t")
             nc.scalar.activation(out=kb_t[:], in_=kt[:], func=ACT.Identity, bias=bias_cols[:, g : g + 1])
             sq_t = ring.tile([P, PACK * P], F32, name="sq_t")
             nc.scalar.activation(out=sq_t[:], in_=kt[:], func=ACT.Square, bias=bias_cols[:, g : g + 1])
+            kb_ps[s] = turn_back(kb_t, kb_pool.tile([P, PACK, P], F32, name="kb_ps"))
+            ss = aux_ps.tile([P, PACK, HG], F32, tag="aux")
+            for t in range(PACK):
+                nc.tensor.matmul(
+                    out=ss[:, t, :], lhsT=sq_t[:, t * P : (t + 1) * P], rhs=head_of_row[:], start=True, stop=True
+                )
+            above = ring.tile([P, PACK, HG], F32, name="above")
+            nc.scalar.activation(out=above[:], in_=ss[:], func=ACT.Relu, bias=-EPS * EPS)
+            gain[s] = ring.tile([P, PACK, HG], F32, name="gain", bufs=3)
+            nc.scalar.activation(
+                out=gain[s][:],
+                in_=above[:],
+                func=ACT.Abs_reciprocal_sqrt,
+                scale=1.0 / (SCALE * SCALE),
+                bias=EPS * EPS / (SCALE * SCALE),
+            )
+
+        def values(s):
+            g, c = divmod(s, PASSES)
+            vt = project_turned(c, g, 1)
             v_t = ring.tile([P, PACK * P], F32, name="v_t")
             nc.scalar.activation(
                 out=v_t[:],
@@ -174,20 +193,8 @@ def tile_taylorsoftmaxattention_pa_kernel(
                 bias=bias_cols[:, GROUPS + g : GROUPS + g + 1],
                 accum_out=vs_cols[:, c, g : g + 1],
             )
-            kb_ps[s] = turn_back(kb_t, kb_pool.tile([P, PACK, P], F32, name="kb_ps"))
-            ss = aux_ps.tile([P, PACK, HG], F32, tag="aux")
-            for t in range(PACK):
-                nc.tensor.matmul(
-                    out=ss[:, t, :], lhsT=sq_t[:, t * P : (t + 1) * P], rhs=head_of_row[:], start=True, stop=True
-                )
-            above = ring.tile([P, PACK, HG], F32, name="above")
-            nc.scalar.activation(out=above[:], in_=ss[:], func=ACT.Relu, bias=-EPS * EPS)
-            norm[s] = ring.tile([P, PACK, HG], F32, name="norm", bufs=3)
-            nc.scalar.activation(
-                out=norm[s][:], in_=above[:], func=ACT.Sqrt, scale=1.0 / (SCALE * SCALE), bias=EPS * EPS / (SCALE * SCALE)
-            )
             v_ps = turn_back(v_t, aux_ps.tile([P, PACK, P], F32, name="v_ps", tag="aux"))
-            v_bf[s] = ring.tile([P, P, PACK], BF16, name="v_bf", align_bytes=64, bufs=3)
+            v_bf[s] = ring.tile([P, P, PACK], BF16, name="v_bf", align_bytes=64)
             nc.scalar.copy(out=v_bf[s][:], in_=v_ps[:].rearrange("p t f -> p f t"))
             if s == STEPS - 1:
                 value_sums()
@@ -207,10 +214,6 @@ def tile_taylorsoftmaxattention_pa_kernel(
                 out=vsum.rearrange("b (g h) o e -> (b g) (h o e)", g=GROUPS),
                 in_=vsum_sb[:].rearrange("g h e -> g (h e)"),
             )
-
-        def gains(s):
-            gain[s] = ring.tile([P, PACK, HG], F32, name="gain", bufs=3)
-            nc.vector.reciprocal(out=gain[s][:], in_=norm[s][:])
 
         def normalise(s):
             win[s] = ring.tile([P, COPIES, HG, EXT, PACK], F32, name="win", bufs=4)
@@ -319,6 +322,15 @@ def tile_taylorsoftmaxattention_pa_kernel(
             if c == 0:
                 acc[g] = acc_ps.tile([P, per_head], F32, name="acc")
                 small_acc[g] = acc_ps.tile([P, 2 * P], F32, name="small_acc")
+            nc.tensor.matmul_mx(
+                out=small_acc[g][:],
+                lhsT=v_codes[s][:].bitcast(FP8X4),
+                lhsT_scale=v_planes[s][:],
+                rhs=sm_codes[s][:].bitcast(FP8X4),
+                rhs_scale=sm_planes[s][:],
+                start=(c == 0),
+                stop=(c == PASSES - 1),
+            )
             for hh in range(HG):
                 cols = slice(hh * per_head, (hh + 1) * per_head)
                 nc.tensor.matmul_mx(
@@ -330,22 +342,10 @@ def tile_taylorsoftmaxattention_pa_kernel(
                     start=(c == 0 and hh == 0),
                     stop=(c == PASSES - 1 and hh == HG - 1),
                 )
-            nc.tensor.matmul_mx(
-                out=small_acc[g][:],
-                lhsT=v_codes[s][:].bitcast(FP8X4),
-                lhsT_scale=v_planes[s][:],
-                rhs=sm_codes[s][:].bitcast(FP8X4),
-                rhs_scale=sm_planes[s][:],
-                start=(c == 0),
-                stop=(c == PASSES - 1),
-            )
 
         def unfold(g):
             z_skew = z[:].rearrange("p s (i w) -> p s i w", w=WIDTH + 1)
-            z_rows = z[:, :, 0 : HALF * WIDTH].rearrange("p s (i c) -> p s i c", c=WIDTH)
-            by_row = acc[g][:].rearrange("p (l s i) -> p s i l", l=SHIFTS, s=2)
-            nc.scalar.copy(out=z_skew[:, :, :, 1:SHIFTS], in_=by_row[:, :, :, 0 : SHIFTS - 1])
-            nc.scalar.copy(out=z_skew[:, 0, :, SHIFTS : SHIFTS + 1], in_=by_row[:, 0, :, SHIFTS - 1 : SHIFTS])
+            full[g] = ring.tile([P, WIDTH * WIDTH + WIDTH], F32, name="full", align_bytes=64, bufs=1)
             for hh in range(HG):
                 q = slice(hh * WIDTH, (hh + 1) * WIDTH)
                 nc.scalar.mul(
@@ -353,32 +353,32 @@ def tile_taylorsoftmaxattention_pa_kernel(
                     in_=small_acc[g][q, q].rearrange("p (s i) -> p s i", s=2).unsqueeze(3),
                     mul=0.5,
                 )
-            full[g] = ring.tile([P, WIDTH * WIDTH + WIDTH], F32, name="full", align_bytes=64, bufs=1)
+                nc.scalar.copy(
+                    out=full[g][q, WIDTH * WIDTH : WIDTH * WIDTH + WIDTH],
+                    in_=small_acc[g][q, P + hh * WIDTH : P + (hh + 1) * WIDTH],
+                )
+            by_row = acc[g][:].rearrange("p (l s i) -> p s i l", l=SHIFTS, s=2)
+            nc.scalar.copy(out=z_skew[:, :, :, 1:SHIFTS], in_=by_row[:, :, :, 0 : SHIFTS - 1])
+            nc.scalar.copy(out=z_skew[:, 0, :, SHIFTS : SHIFTS + 1], in_=by_row[:, 0, :, SHIFTS - 1 : SHIFTS])
+
+        def store(g):
+            z_rows = z[:, :, 0 : HALF * WIDTH].rearrange("p s (i c) -> p s i c", c=WIDTH)
             full_m = full[g][:, 0 : WIDTH * WIDTH].rearrange("p (a b) -> p a b", b=WIDTH)
             for s in range(2):
                 rows = slice(s * HALF, (s + 1) * HALF)
                 other = slice((1 - s) * HALF, (2 - s) * HALF)
-                nc.gpsimd.tensor_tensor(
+                nc.vector.tensor_tensor(
                     out=full_m[:, rows, rows],
                     in0=z_rows[:, s, :, 0:HALF],
                     in1=z_rows[:, s, :, 0:HALF].rearrange("p i c -> p c i"),
                     op=ALU.add,
                 )
-                nc.gpsimd.tensor_tensor(
+                nc.vector.tensor_tensor(
                     out=full_m[:, rows, other],
                     in0=z_rows[:, s, :, HALF:WIDTH],
                     in1=z_rows[:, 1 - s, :, HALF:WIDTH].rearrange("p i c -> p c i"),
                     op=ALU.add,
                 )
-
-            for hh in range(HG):
-                q = slice(hh * WIDTH, (hh + 1) * WIDTH)
-                nc.scalar.copy(
-                    out=full[g][q, WIDTH * WIDTH : WIDTH * WIDTH + WIDTH],
-                    in_=small_acc[g][q, P + hh * WIDTH : P + (hh + 1) * WIDTH],
-                )
-
-        def store(g):
             turned = ring.tile([P, WIDTH * WIDTH + WIDTH], F32, name="turned", align_bytes=64, bufs=1)
             nc.vector.transpose(out=turned[:, 0 : WIDTH * WIDTH], in_=full[g][:, 0 : WIDTH * WIDTH])
             nc.vector.transpose(out=turned[:, WIDTH * WIDTH :], in_=full[g][:, WIDTH * WIDTH :])
@@ -405,8 +405,8 @@ def tile_taylorsoftmaxattention_pa_kernel(
             at(spread, s + 1, STEPS)
             at_group_end(plain_sums, s)
             at(transpose_x, s + 4, PASSES)
-            at(project, s + 3, STEPS)
-            at(gains, s + 2, STEPS)
+            at(keys, s + 3, STEPS)
+            at(values, s + 2, STEPS)
             at(products, s, STEPS)
             at(normalise, s + 2, STEPS)
             at(quantise_small, s + 1, STEPS)

@@ -43,9 +43,9 @@ def tile_taylorsoftmaxattention_pa_kernel(
         ctx.enter_context(tc.manual_schedule())
         const = ctx.enter_context(tc.tile_pool(name="const", bufs=1))
         ring = ctx.enter_context(tc.tile_pool(name="ring", bufs=2))
-        aux_ps = ctx.enter_context(tc.psum_pool(name="aux_ps", bufs=2))
+        aux_ps = ctx.enter_context(tc.psum_pool(name="aux_ps", bufs=3))
         kb_pool = ctx.enter_context(tc.psum_pool(name="kb_pool", bufs=2))
-        kn_pool = ctx.enter_context(tc.psum_pool(name="kn_pool", bufs=2))
+        kn_pool = ctx.enter_context(tc.psum_pool(name="kn_pool", bufs=1))
         acc_ps = ctx.enter_context(tc.psum_pool(name="acc_ps", bufs=1))
 
         w_words = const.tile([P, 2, FEATURES], U32, align_bytes=64)
@@ -116,6 +116,7 @@ def tile_taylorsoftmaxattention_pa_kernel(
 
         xg, kb_ps, gain, win, kn_ps, sm_bf, v_bf, knp, o_sb = {}, {}, {}, {}, {}, {}, {}, {}, {}
         sm_codes, sm_planes, v_codes, v_planes, kk_bf, acc, small_acc, full = {}, {}, {}, {}, {}, {}, {}, {}
+        kt, kb_t, sq_t, ss, vt, v_t, v_ps, there, there_sb = {}, {}, {}, {}, {}, {}, {}, {}, {}
 
         def transpose_x(c):
             xg[c] = ring.tile([P, PACK, P, PACK], BF16, name="xg", align_bytes=64)
@@ -157,21 +158,29 @@ def tile_taylorsoftmaxattention_pa_kernel(
                 nc.tensor.transpose(bank[:, t, :], turned[:, t * P : (t + 1) * P], ident[:])
             return bank
 
-        def keys(s):
+
+        def keys_project(s):
             g, c = divmod(s, PASSES)
-            kt = project_turned(c, g, 0)
-            kb_t = ring.tile([P, PACK * P], F32, name="kb_t")
-            nc.scalar.activation(out=kb_t[:], in_=kt[:], func=ACT.Identity, bias=bias_cols[:, g : g + 1])
-            sq_t = ring.tile([P, PACK * P], F32, name="sq_t")
-            nc.scalar.activation(out=sq_t[:], in_=kt[:], func=ACT.Square, bias=bias_cols[:, g : g + 1])
-            kb_ps[s] = turn_back(kb_t, kb_pool.tile([P, PACK, P], F32, name="kb_ps"))
-            ss = aux_ps.tile([P, PACK, HG], F32, tag="aux")
+            kt[s] = project_turned(c, g, 0)
+
+        def keys_bias(s):
+            g = s // PASSES
+            kb_t[s] = ring.tile([P, PACK * P], F32, name="kb_t")
+            nc.scalar.activation(out=kb_t[s][:], in_=kt[s][:], func=ACT.Identity, bias=bias_cols[:, g : g + 1])
+            sq_t[s] = ring.tile([P, PACK * P], F32, name="sq_t")
+            nc.scalar.activation(out=sq_t[s][:], in_=kt[s][:], func=ACT.Square, bias=bias_cols[:, g : g + 1])
+
+        def keys_turn(s):
+            kb_ps[s] = turn_back(kb_t[s], kb_pool.tile([P, PACK, P], F32, name="kb_ps"))
+            ss[s] = aux_ps.tile([P, PACK, HG], F32, name="ss", tag="aux")
             for t in range(PACK):
                 nc.tensor.matmul(
-                    out=ss[:, t, :], lhsT=sq_t[:, t * P : (t + 1) * P], rhs=head_of_row[:], start=True, stop=True
+                    out=ss[s][:, t, :], lhsT=sq_t[s][:, t * P : (t + 1) * P], rhs=head_of_row[:], start=True, stop=True
                 )
+
+        def keys_gain(s):
             above = ring.tile([P, PACK, HG], F32, name="above")
-            nc.scalar.activation(out=above[:], in_=ss[:], func=ACT.Relu, bias=-EPS * EPS)
+            nc.scalar.activation(out=above[:], in_=ss[s][:], func=ACT.Relu, bias=-EPS * EPS)
             gain[s] = ring.tile([P, PACK, HG], F32, name="gain", bufs=3)
             nc.scalar.activation(
                 out=gain[s][:],
@@ -181,21 +190,28 @@ def tile_taylorsoftmaxattention_pa_kernel(
                 bias=EPS * EPS / (SCALE * SCALE),
             )
 
-        def values(s):
+        def values_project(s):
             g, c = divmod(s, PASSES)
-            vt = project_turned(c, g, 1)
-            v_t = ring.tile([P, PACK * P], F32, name="v_t")
+            vt[s] = project_turned(c, g, 1)
+
+        def values_bias(s):
+            g, c = divmod(s, PASSES)
+            v_t[s] = ring.tile([P, PACK * P], F32, name="v_t")
             nc.scalar.activation(
-                out=v_t[:],
-                in_=vt[:],
+                out=v_t[s][:],
+                in_=vt[s][:],
                 func=ACT.Identity,
                 scale=1.0 / TOKENS,
                 bias=bias_cols[:, GROUPS + g : GROUPS + g + 1],
                 accum_out=vs_cols[:, c, g : g + 1],
             )
-            v_ps = turn_back(v_t, aux_ps.tile([P, PACK, P], F32, name="v_ps", tag="aux"))
+
+        def values_turn(s):
+            v_ps[s] = turn_back(v_t[s], aux_ps.tile([P, PACK, P], F32, name="v_ps", tag="aux"))
+
+        def values_round(s):
             v_bf[s] = ring.tile([P, P, PACK], BF16, name="v_bf", align_bytes=64)
-            nc.scalar.copy(out=v_bf[s][:], in_=v_ps[:].rearrange("p t f -> p f t"))
+            nc.scalar.copy(out=v_bf[s][:], in_=v_ps[s][:].rearrange("p t f -> p f t"))
             if s == STEPS - 1:
                 value_sums()
 
@@ -224,6 +240,20 @@ def tile_taylorsoftmaxattention_pa_kernel(
                 op=ALU.mult,
             )
 
+        def kn_there(s):
+            there[s] = aux_ps.tile([P, HG, P], F32, name="there", tag="aux")
+            for hh in range(HG):
+                nc.tensor.transpose(there[s][:, hh, :], win[s][:, 0, hh, 0:WIDTH, :].rearrange("p d t -> p (d t)"), ident[:])
+
+        def kn_leave(s):
+            there_sb[s] = ring.tile([P, HG, P], F32, name="there_sb")
+            nc.scalar.copy(out=there_sb[s][:], in_=there[s][:])
+
+        def kn_back(s):
+            kn_ps[s] = kn_pool.tile([P, HG, RUN], F32, name="kn_ps")
+            for hh in range(HG):
+                nc.tensor.transpose(kn_ps[s][:, hh, :], there_sb[s][:, hh, :], ident[:])
+
         def spread(s):
             g, c = divmod(s, PASSES)
             kn = win[s][:, 0, :, 0:WIDTH, :]
@@ -232,17 +262,9 @@ def tile_taylorsoftmaxattention_pa_kernel(
             kept = EXT - COPIES + 1
             for l in range(1, COPIES):
                 nc.sync.dma_start(out=win[s][:, l, :, 0:kept, :], in_=win[s][:, 0, :, l : l + kept, :])
-            there = aux_ps.tile([P, HG, P], F32, tag="aux")
-            for hh in range(HG):
-                nc.tensor.transpose(there[:, hh, :], by_head[:, hh, :], ident[:])
             sm_bf[s] = ring.tile([P, 2, HG, RUN], BF16, name="sm_bf", align_bytes=64)
             nc.scalar.activation(out=sm_bf[s][:, 0, :, :], in_=by_head, func=ACT.Square)
             nc.scalar.copy(out=sm_bf[s][:, 1, :, :], in_=by_head)
-            there_sb = ring.tile([P, HG, P], F32, name="there_sb")
-            nc.scalar.copy(out=there_sb[:], in_=there[:])
-            kn_ps[s] = kn_pool.tile([P, HG, RUN], F32, name="kn_ps")
-            for hh in range(HG):
-                nc.tensor.transpose(kn_ps[s][:, hh, :], there_sb[:, hh, :], ident[:])
             if c == 0:
                 knp[g] = ring.tile([P, PASSES * PACK, P + 1], F32, name="knp")
                 nc.scalar.copy(out=knp[g][:, :, P : P + 1], in_=one_cols[:].unsqueeze(2))
@@ -402,12 +424,21 @@ def tile_taylorsoftmaxattention_pa_kernel(
 
         for s in range(-4, STEPS + 1):
             at_group_end(unfold, s - 1)
+            at(kn_there, s + 1, STEPS)
+            at(keys_project, s + 3, STEPS)
+            at(values_project, s + 2, STEPS)
             at(spread, s + 1, STEPS)
+            at(kn_leave, s + 1, STEPS)
+            at(keys_bias, s + 3, STEPS)
+            at(values_bias, s + 2, STEPS)
+            at(keys_turn, s + 3, STEPS)
+            at(values_turn, s + 2, STEPS)
+            at(keys_gain, s + 3, STEPS)
+            at(values_round, s + 2, STEPS)
             at_group_end(plain_sums, s)
             at(transpose_x, s + 4, PASSES)
-            at(keys, s + 3, STEPS)
-            at(values, s + 2, STEPS)
             at(products, s, STEPS)
+            at(kn_back, s + 1, STEPS)
             at(normalise, s + 2, STEPS)
             at(quantise_small, s + 1, STEPS)
             at(quantise_values, s + 1, STEPS)

@@ -27,7 +27,7 @@ EXT = WIDTH + SHIFTS
 HALF = WIDTH // 2
 RUN = WIDTH * PACK
 COPIES = 4
-VECTOR_SHIFTS = 10
+VECTOR_SHIFTS = 11
 MASK_PITCH = P + WIDTH
 EPS = 1e-12
 SCALE = 32.0 ** 0.25

@@ -72,8 +72,9 @@ def tile_taylorsoftmaxattention_pa_kernel(
 
         load_x(0)
         load_weight(0, wk_words, wk_scales)
+        load_x(1)
         load_weight(1, wv_words, wv_scales)
-        for c in range(1, PASSES):
+        for c in range(2, PASSES):
             load_x(c)
 
         bias_rows = const.tile([P, P], BF16)
@@ -118,7 +119,7 @@ def tile_taylorsoftmaxattention_pa_kernel(
         sm_codes, sm_planes, v_codes, v_planes, kk_bf, acc, small_acc, full = {}, {}, {}, {}, {}, {}, {}, {}
         kt, kb_t, sq_t, ss, vt, v_t, v_ps, there, there_sb = {}, {}, {}, {}, {}, {}, {}, {}, {}
 
-        def transpose_x(c):
+        def transpose_x(c, copies):
             xg[c] = ring.tile([P, PACK, P, PACK], BF16, name="xg", align_bytes=64)
             xg_words = xg[c][:].bitcast(F32)
             for half in range(2):
@@ -127,7 +128,7 @@ def tile_taylorsoftmaxattention_pa_kernel(
                     words = x_sb[c][:, 2 * half + s, :].bitcast(F32)
                     for u in range(2):
                         nc.tensor.transpose(xt[:, s, u, :], words[:, u : FEATURES // 2 : 2], ident[:])
-                nc.vector.tensor_copy(
+                copies[half](
                     out=xg_words[:, 2 * half : 2 * half + 2, :, :],
                     in_=xt[:].rearrange("q s u p -> q s p u"),
                 )
@@ -254,14 +255,16 @@ def tile_taylorsoftmaxattention_pa_kernel(
             for hh in range(HG):
                 nc.tensor.transpose(kn_ps[s][:, hh, :], there_sb[s][:, hh, :], ident[:])
 
-        def spread(s):
-            g, c = divmod(s, PASSES)
-            kn = win[s][:, 0, :, 0:WIDTH, :]
-            by_head = kn.rearrange("p h d t -> p h (d t)")
+        def extend(s):
             nc.scalar.copy(out=win[s][:, 0, :, WIDTH:EXT, :], in_=win[s][:, 0, :, 0:SHIFTS, :])
             kept = EXT - COPIES + 1
             for l in range(1, COPIES):
                 nc.sync.dma_start(out=win[s][:, l, :, 0:kept, :], in_=win[s][:, 0, :, l : l + kept, :])
+
+        def round_keys(s):
+            g, c = divmod(s, PASSES)
+            kn = win[s][:, 0, :, 0:WIDTH, :]
+            by_head = kn.rearrange("p h d t -> p h (d t)")
             sm_bf[s] = ring.tile([P, 2, HG, RUN], BF16, name="sm_bf", align_bytes=64)
             nc.scalar.activation(out=sm_bf[s][:, 0, :, :], in_=by_head, func=ACT.Square)
             nc.scalar.copy(out=sm_bf[s][:, 1, :, :], in_=by_head)
@@ -422,12 +425,50 @@ def tile_taylorsoftmaxattention_pa_kernel(
             if 0 <= step < STEPS and step % PASSES == PASSES - 1:
                 stage(step // PASSES)
 
-        for s in range(-4, STEPS + 1):
+        on_vector = (nc.vector.tensor_copy, nc.vector.tensor_copy)
+        transpose_x(0, (nc.vector.tensor_copy, nc.scalar.copy))
+        quantise_x(0)
+        transpose_x(1, on_vector)
+        quantise_x(1)
+        keys_project(0)
+        keys_project(1)
+        keys_bias(0)
+        keys_bias(1)
+        keys_turn(0)
+        keys_gain(0)
+        normalise(0)
+        keys_turn(1)
+        keys_gain(1)
+        kn_there(0)
+        normalise(1)
+        extend(0)
+        kn_leave(0)
+        transpose_x(2, on_vector)
+        kn_back(0)
+        quantise_x(2)
+        transpose_x(3, on_vector)
+        quantise_x(3)
+        keys_project(2)
+        values_project(0)
+        round_keys(0)
+        keys_bias(2)
+        values_bias(0)
+        keys_turn(2)
+        values_turn(0)
+        keys_gain(2)
+        values_round(0)
+        values_project(1)
+        values_bias(1)
+        values_turn(1)
+        values_round(1)
+
+        for s in range(STEPS + 1):
             at_group_end(unfold, s - 1)
             at(kn_there, s + 1, STEPS)
             at(keys_project, s + 3, STEPS)
             at(values_project, s + 2, STEPS)
-            at(spread, s + 1, STEPS)
+            at(extend, s + 1, STEPS)
+            at(round_keys, s + 1, STEPS)
             at(kn_leave, s + 1, STEPS)
             at(keys_bias, s + 3, STEPS)
             at(values_bias, s + 2, STEPS)
@@ -436,14 +477,16 @@ def tile_taylorsoftmaxattention_pa_kernel(
             at(keys_gain, s + 3, STEPS)
             at(values_round, s + 2, STEPS)
             at_group_end(plain_sums, s)
-            at(transpose_x, s + 4, PASSES)
             at(products, s, STEPS)
+            if s == 0:
+                quantise_small(0)
+                quantise_values(0)
+                mask_values(0)
             at(kn_back, s + 1, STEPS)
             at(normalise, s + 2, STEPS)
             at(quantise_small, s + 1, STEPS)
             at(quantise_values, s + 1, STEPS)
             at(mask_values, s + 1, STEPS)
-            at(quantise_x, s + 4, PASSES)
             at_group_end(store, s - 1)
             at(contract, s, STEPS)
         nc.sync.dma_start(out=kv[0].rearrange("(g h) d e -> (h d) g e", g=GROUPS), in_=kv_out[:])

@@ -22,12 +22,16 @@ PASSES = TOKENS // (P * PACK)
 GROUPS = 4
 HG = HEADS // GROUPS
 STEPS = GROUPS * PASSES
-SHIFTS = WIDTH // 2
-EXT = WIDTH + SHIFTS
+RING = WIDTH - 1
+SHIFTS = RING // 2
 HALF = WIDTH // 2
 RUN = WIDTH * PACK
-COPIES = 4
-VECTOR_SHIFTS = 11
+COPIES = 5
+REACH = RING + SHIFTS - COPIES
+REACH_PITCH = REACH + 3
+VECTOR_SHIFTS = 10
+ROW = SHIFTS * WIDTH
+PER_HEAD = ROW + WIDTH
 MASK_PITCH = P + WIDTH
 EPS = 1e-12
 SCALE = 32.0 ** 0.25
@@ -44,8 +48,9 @@ def tile_taylorsoftmaxattention_pa_kernel(
         const = ctx.enter_context(tc.tile_pool(name="const", bufs=1))
         ring = ctx.enter_context(tc.tile_pool(name="ring", bufs=2))
         aux_ps = ctx.enter_context(tc.psum_pool(name="aux_ps", bufs=3))
-        kb_pool = ctx.enter_context(tc.psum_pool(name="kb_pool", bufs=2))
+        kb_pool = ctx.enter_context(tc.psum_pool(name="kb_pool", bufs=1))
         kn_pool = ctx.enter_context(tc.psum_pool(name="kn_pool", bufs=1))
+        gram_ps = ctx.enter_context(tc.psum_pool(name="gram_ps", bufs=1))
         acc_ps = ctx.enter_context(tc.psum_pool(name="acc_ps", bufs=1))
 
         w_words = const.tile([P, 2, FEATURES], U32, align_bytes=64)
@@ -94,8 +99,17 @@ def tile_taylorsoftmaxattention_pa_kernel(
         nc.gpsimd.memset(head_of_row[:], 0.0)
         for hh in range(HG):
             nc.gpsimd.memset(head_of_row[hh * WIDTH : (hh + 1) * WIDTH, hh : hh + 1], 1.0)
-        z = const.tile([P, 2, HALF * (WIDTH + 1)], F32)
+        z = const.tile([P, 2, HALF * WIDTH], F32)
         nc.vector.memset(z[:], 0.0)
+        base = []
+        for k in range(4):
+            base.append(const.tile([P, P + 1, PACK], F32, name="base%d" % k))
+            nc.gpsimd.memset(base[k][:, P : P + 1, :], 1.0)
+        kk = []
+        for k in range(2):
+            kk.append(const.tile([P, HG, PER_HEAD * PACK], BF16, name="kk%d" % k, align_bytes=64))
+            ends = kk[k][:, :, 0 : ROW * PACK].rearrange("p h (l w) -> p h l w", w=RUN)[:, :, :, RING * PACK :]
+            nc.vector.memset(ends, 0.0)
         vs_cols = const.tile([P, PASSES, P], F32)
         nc.vector.memset(vs_cols[:], 0.0)
         masked = []
@@ -115,8 +129,8 @@ def tile_taylorsoftmaxattention_pa_kernel(
             x_codes.append(const.tile([P, FEATURES], U32, name="x_codes%d" % c, align_bytes=64))
             x_planes.append(const.tile([P, FEATURES], U8, name="x_planes%d" % c, align_bytes=64))
 
-        xg, kb_ps, gain, win, kn_ps, sm_bf, v_bf, knp, o_sb = {}, {}, {}, {}, {}, {}, {}, {}, {}
-        sm_codes, sm_planes, v_codes, v_planes, kk_bf, acc, small_acc, full = {}, {}, {}, {}, {}, {}, {}, {}
+        xg, kb_ps, gain, moved, kn_ps, sm_bf, v_bf, gram, o_sb = {}, {}, {}, {}, {}, {}, {}, {}, {}
+        sm_codes, sm_planes, v_codes, v_planes, acc, small_acc, full, full_t = {}, {}, {}, {}, {}, {}, {}, {}
         kt, kb_t, sq_t, ss, vt, v_t, v_ps, there, there_sb = {}, {}, {}, {}, {}, {}, {}, {}, {}
 
         def transpose_x(c, copies):
@@ -172,7 +186,11 @@ def tile_taylorsoftmaxattention_pa_kernel(
             nc.scalar.activation(out=sq_t[s][:], in_=kt[s][:], func=ACT.Square, bias=bias_cols[:, g : g + 1])
 
         def keys_turn(s):
-            kb_ps[s] = turn_back(kb_t[s], kb_pool.tile([P, PACK, P], F32, name="kb_ps"))
+            if s == 0:
+                bank = aux_ps.tile([P, PACK, P], F32, name="kb_first", tag="aux")
+            else:
+                bank = kb_pool.tile([P, PACK, P], F32, name="kb_ps")
+            kb_ps[s] = turn_back(kb_t[s], bank)
             ss[s] = aux_ps.tile([P, PACK, HG], F32, name="ss", tag="aux")
             for t in range(PACK):
                 nc.tensor.matmul(
@@ -232,19 +250,29 @@ def tile_taylorsoftmaxattention_pa_kernel(
                 in_=vsum_sb[:].rearrange("g h e -> g (h e)"),
             )
 
+        def heads_of(s):
+            return base[s % 4][:, 0:P, :].rearrange("p (h d) t -> p h d t", h=HG)
+
         def normalise(s):
-            win[s] = ring.tile([P, COPIES, HG, EXT, PACK], F32, name="win", bufs=4)
             nc.vector.tensor_tensor(
-                out=win[s][:, 0, :, 0:WIDTH, :],
+                out=heads_of(s),
                 in0=kb_ps[s][:].rearrange("p t (h d) -> p h d t", h=HG),
                 in1=gain[s][:].rearrange("p t h -> p h t").unsqueeze(2).to_broadcast([P, HG, WIDTH, PACK]),
                 op=ALU.mult,
             )
+            copies = ring.tile([P, COPIES, HG * REACH_PITCH + 1, PACK], F32, name="moved", bufs=3)
+            moved[s] = copies[:, :, 0 : HG * REACH_PITCH, :].rearrange("p m (h e) t -> p m h e t", h=HG)
+            cycle = heads_of(s)[:, :, 1:WIDTH, :]
+            for m in range(COPIES):
+                front = RING - (m + 1)
+                nc.sync.dma_start(out=moved[s][:, m, :, 0:front, :], in_=cycle[:, :, m + 1 : RING, :])
+                nc.sync.dma_start(out=moved[s][:, m, :, front:REACH, :], in_=cycle[:, :, 0 : REACH - front, :])
 
         def kn_there(s):
             there[s] = aux_ps.tile([P, HG, P], F32, name="there", tag="aux")
             for hh in range(HG):
-                nc.tensor.transpose(there[s][:, hh, :], win[s][:, 0, hh, 0:WIDTH, :].rearrange("p d t -> p (d t)"), ident[:])
+                one_head = base[s % 4][:, hh * WIDTH : (hh + 1) * WIDTH, :]
+                nc.tensor.transpose(there[s][:, hh, :], one_head.rearrange("p d t -> p (d t)"), ident[:])
 
         def kn_leave(s):
             there_sb[s] = ring.tile([P, HG, P], F32, name="there_sb")
@@ -255,58 +283,58 @@ def tile_taylorsoftmaxattention_pa_kernel(
             for hh in range(HG):
                 nc.tensor.transpose(kn_ps[s][:, hh, :], there_sb[s][:, hh, :], ident[:])
 
-        def extend(s):
-            nc.scalar.copy(out=win[s][:, 0, :, WIDTH:EXT, :], in_=win[s][:, 0, :, 0:SHIFTS, :])
-            kept = EXT - COPIES + 1
-            for l in range(1, COPIES):
-                nc.sync.dma_start(out=win[s][:, l, :, 0:kept, :], in_=win[s][:, 0, :, l : l + kept, :])
-
         def round_keys(s):
-            g, c = divmod(s, PASSES)
-            kn = win[s][:, 0, :, 0:WIDTH, :]
-            by_head = kn.rearrange("p h d t -> p h (d t)")
+            by_head = heads_of(s).rearrange("p h d t -> p h (d t)")
             sm_bf[s] = ring.tile([P, 2, HG, RUN], BF16, name="sm_bf", align_bytes=64)
             nc.scalar.activation(out=sm_bf[s][:, 0, :, :], in_=by_head, func=ACT.Square)
             nc.scalar.copy(out=sm_bf[s][:, 1, :, :], in_=by_head)
-            if c == 0:
-                knp[g] = ring.tile([P, PASSES * PACK, P + 1], F32, name="knp")
-                nc.scalar.copy(out=knp[g][:, :, P : P + 1], in_=one_cols[:].unsqueeze(2))
-            nc.scalar.copy(
-                out=knp[g][:, c * PACK : (c + 1) * PACK, 0:P].rearrange("p t (h d) -> p t h d", h=HG),
-                in_=kn.rearrange("p h d t -> p t h d"),
-            )
 
-        def plain_sums(g):
-            gram = aux_ps.tile([P, P + 1], F32, tag="aux")
-            for s in range(PASSES * PACK):
+        def multiply_row(s):
+            for hh in range(HG):
+                row = kk[s % 2][:, hh, ROW * PACK :].rearrange("p (j t) -> p j t", t=PACK)
+                for t in range(PACK):
+                    nc.scalar.activation(
+                        out=row[:, :, t],
+                        in_=base[s % 4][:, hh * WIDTH : (hh + 1) * WIDTH, t],
+                        func=ACT.Copy,
+                        scale=base[s % 4][:, hh * WIDTH, t : t + 1],
+                    )
+
+        def add_plain_sums(s):
+            g, c = divmod(s, PASSES)
+            if c == 0:
+                gram[g] = gram_ps.tile([P, P + 1], F32, name="gram")
+            for t in range(PACK):
                 nc.tensor.matmul(
-                    out=gram[:],
-                    lhsT=knp[g][:, s, 0:P],
-                    rhs=knp[g][:, s, :],
-                    start=(s == 0),
-                    stop=(s == PASSES * PACK - 1),
+                    out=gram[g][:],
+                    lhsT=base[s % 4][:, 0:P, t],
+                    rhs=base[s % 4][:, :, t],
+                    start=(c == 0 and t == 0),
+                    stop=(c == PASSES - 1 and t == PACK - 1),
                 )
+
+        def take_plain_sums(g):
             o_sb[g] = ring.tile([P, WIDTH, WIDTH + 1], F32, name="o_sb")
             for hh in range(HG):
                 q = slice(hh * WIDTH, (hh + 1) * WIDTH)
-                nc.scalar.mul(out=o_sb[g][q, :, 0:1], in_=gram[q, q].unsqueeze(2), mul=1.0 / TOKENS)
-            nc.scalar.mul(out=kv_out[:, g, 0:1], in_=gram[:, P : P + 1], mul=1.0 / TOKENS)
+                nc.scalar.mul(out=o_sb[g][q, :, 0:1], in_=gram[g][q, q].unsqueeze(2), mul=1.0 / TOKENS)
+            nc.scalar.mul(out=kv_out[:, g, 0:1], in_=gram[g][:, P : P + 1], mul=1.0 / TOKENS)
 
         def products(s):
-            kk_bf[s] = ring.tile([P, HG, SHIFTS, RUN], BF16, name="kk_bf", align_bytes=64, bufs=1)
-            for first in range(0, SHIFTS, COPIES):
-                out = kk_bf[s][:, :, first : first + COPIES, :].rearrange("p h l e -> p l h e")
-                moved = win[s][:, :, :, first + 1 : first + 1 + WIDTH, :].rearrange("p l h d t -> p l h (d t)")
-                mine = min(max(VECTOR_SHIFTS - first, 0), COPIES)
-                if mine > 0:
-                    still = kn_ps[s][:].unsqueeze(1).to_broadcast([P, mine, HG, RUN])
-                    nc.vector.tensor_tensor(out=out[:, 0:mine], in0=still, in1=moved[:, 0:mine], op=ALU.mult)
-                if mine < COPIES:
-                    still = win[s][:, 0, :, 0:WIDTH, :].rearrange("p h d t -> p h (d t)")
-                    still = still.unsqueeze(1).to_broadcast([P, COPIES - mine, HG, RUN])
-                    nc.gpsimd.tensor_tensor(
-                        out=out[:, mine:COPIES], in0=still, in1=moved[:, mine:COPIES], op=ALU.mult
-                    )
+            in_psum = kn_ps[s][:, :, PACK:RUN]
+            in_sbuf = heads_of(s)[:, :, 1:WIDTH, :].rearrange("p h d t -> p h (d t)")
+            out = kk[s % 2][:, :, 0 : ROW * PACK].rearrange("p h (l w) -> p l h w", w=RUN)[:, :, :, 0 : RING * PACK]
+            if s > 0:
+                nc.gpsimd.memset(kk[(s - 1) % 2][:, :, (ROW - 1) * PACK : ROW * PACK], 0.0)
+            for start in range(0, SHIFTS, COPIES):
+                engine, factor = (nc.vector, in_psum) if start < VECTOR_SHIFTS else (nc.gpsimd, in_sbuf)
+                others = moved[s][:, :, :, start : start + RING, :]
+                engine.tensor_tensor(
+                    out=out[:, start : start + COPIES],
+                    in0=factor.unsqueeze(1).to_broadcast([P, COPIES, HG, RING * PACK]),
+                    in1=others.rearrange("p m h d t -> p m h (d t)"),
+                    op=ALU.mult,
+                )
 
         def quantise_small(s):
             sm_codes[s] = ring.tile([P, 2 * P], U32, name="sm_codes", align_bytes=64, bufs=3)
@@ -334,18 +362,17 @@ def tile_taylorsoftmaxattention_pa_kernel(
 
         def contract(s):
             g, c = divmod(s, PASSES)
-            per_head = SHIFTS * WIDTH
-            kk_codes = ring.tile([P, HG * per_head], U32, name="kk_codes", align_bytes=64)
-            kk_planes = ring.tile([P, HG * per_head], U8, name="kk_planes", align_bytes=64)
+            kk_codes = ring.tile([P, HG * PER_HEAD], U32, name="kk_codes", align_bytes=64)
+            kk_planes = ring.tile([P, HG * PER_HEAD], U8, name="kk_planes", align_bytes=64)
             for pair in range(HG // 2):
-                cols = slice(2 * pair * per_head, 2 * (pair + 1) * per_head)
+                cols = slice(2 * pair * PER_HEAD, 2 * (pair + 1) * PER_HEAD)
                 nc.vector.quantize_mx(
                     out=kk_codes[:, cols].bitcast(FP8X4),
                     scales=kk_planes[:, cols],
-                    in_=kk_bf[s][:, 2 * pair : 2 * pair + 2, :, :].rearrange("p h l e -> p (h l e)"),
+                    in_=kk[s % 2][:, 2 * pair : 2 * pair + 2, :].rearrange("p h e -> p (h e)"),
                 )
             if c == 0:
-                acc[g] = acc_ps.tile([P, per_head], F32, name="acc")
+                acc[g] = acc_ps.tile([P, PER_HEAD], F32, name="acc")
                 small_acc[g] = acc_ps.tile([P, 2 * P], F32, name="small_acc")
             nc.tensor.matmul_mx(
                 out=small_acc[g][:],
@@ -357,7 +384,7 @@ def tile_taylorsoftmaxattention_pa_kernel(
                 stop=(c == PASSES - 1),
             )
             for hh in range(HG):
-                cols = slice(hh * per_head, (hh + 1) * per_head)
+                cols = slice(hh * PER_HEAD, (hh + 1) * PER_HEAD)
                 nc.tensor.matmul_mx(
                     out=acc[g][:],
                     lhsT=masked[s % 2][:, hh * P : (hh + 1) * P].bitcast(FP8X4),
@@ -369,49 +396,49 @@ def tile_taylorsoftmaxattention_pa_kernel(
                 )
 
         def unfold(g):
-            z_skew = z[:].rearrange("p s (i w) -> p s i w", w=WIDTH + 1)
+            z_skew = z[:].rearrange("p s (i w) -> p s i w", w=RING + 1)
             full[g] = ring.tile([P, WIDTH * WIDTH + WIDTH], F32, name="full", align_bytes=64, bufs=1)
+            matrix = full[g][:, 0 : WIDTH * WIDTH].rearrange("p (a b) -> p a b", b=WIDTH)
             for hh in range(HG):
                 q = slice(hh * WIDTH, (hh + 1) * WIDTH)
                 nc.scalar.mul(
                     out=z_skew[q, :, :, 0:1],
-                    in_=small_acc[g][q, q].rearrange("p (s i) -> p s i", s=2).unsqueeze(3),
+                    in_=small_acc[g][q, hh * WIDTH + 1 : (hh + 1) * WIDTH + 1].rearrange("p (s i) -> p s i", s=2).unsqueeze(3),
                     mul=0.5,
                 )
                 nc.scalar.copy(
                     out=full[g][q, WIDTH * WIDTH : WIDTH * WIDTH + WIDTH],
                     in_=small_acc[g][q, P + hh * WIDTH : P + (hh + 1) * WIDTH],
                 )
-            by_row = acc[g][:].rearrange("p (l s i) -> p s i l", l=SHIFTS, s=2)
-            nc.scalar.copy(out=z_skew[:, :, :, 1:SHIFTS], in_=by_row[:, :, :, 0 : SHIFTS - 1])
-            nc.scalar.copy(out=z_skew[:, 0, :, SHIFTS : SHIFTS + 1], in_=by_row[:, 0, :, SHIFTS - 1 : SHIFTS])
+            by_row = acc[g][:, 0:ROW].rearrange("p (l s i) -> p s i l", l=SHIFTS, s=2)
+            nc.scalar.copy(out=z_skew[:, :, :, 1 : SHIFTS + 1], in_=by_row)
+            nc.scalar.copy(out=matrix[:, 0, :], in_=acc[g][:, ROW:PER_HEAD])
+            nc.scalar.copy(out=matrix[:, 1:WIDTH, 0:1], in_=acc[g][:, ROW + 1 : PER_HEAD].unsqueeze(2))
+
+        def fold(g):
+            z_rows = z[:, :, 0 : HALF * RING].rearrange("p s (i c) -> p s i c", c=RING)
+            matrix = full[g][:, 0 : WIDTH * WIDTH].rearrange("p (a b) -> p a b", b=WIDTH)
+            low, high = slice(1, HALF + 1), slice(HALF + 1, WIDTH)
+            upper, lower = z_rows[:, 0, :, :], z_rows[:, 1, 0 : RING - HALF, :]
+            for rows, cols, one, other in (
+                (low, low, upper[:, :, 0:HALF], upper[:, :, 0:HALF]),
+                (low, high, upper[:, :, HALF:RING], lower[:, :, RING - HALF : RING]),
+                (high, low, lower[:, :, RING - HALF : RING], upper[:, :, HALF:RING]),
+                (high, high, lower[:, :, 0 : RING - HALF], lower[:, :, 0 : RING - HALF]),
+            ):
+                nc.vector.tensor_tensor(
+                    out=matrix[:, rows, cols], in0=one, in1=other.rearrange("p i c -> p c i"), op=ALU.add
+                )
+            full_t[g] = ring.tile([P, WIDTH * WIDTH + WIDTH], F32, name="full_t", align_bytes=64, bufs=1)
+            nc.vector.transpose(out=full_t[g][:, 0 : WIDTH * WIDTH], in_=full[g][:, 0 : WIDTH * WIDTH])
+            nc.vector.transpose(out=full_t[g][:, WIDTH * WIDTH :], in_=full[g][:, WIDTH * WIDTH :])
 
         def store(g):
-            z_rows = z[:, :, 0 : HALF * WIDTH].rearrange("p s (i c) -> p s i c", c=WIDTH)
-            full_m = full[g][:, 0 : WIDTH * WIDTH].rearrange("p (a b) -> p a b", b=WIDTH)
-            for s in range(2):
-                rows = slice(s * HALF, (s + 1) * HALF)
-                other = slice((1 - s) * HALF, (2 - s) * HALF)
-                nc.vector.tensor_tensor(
-                    out=full_m[:, rows, rows],
-                    in0=z_rows[:, s, :, 0:HALF],
-                    in1=z_rows[:, s, :, 0:HALF].rearrange("p i c -> p c i"),
-                    op=ALU.add,
-                )
-                nc.vector.tensor_tensor(
-                    out=full_m[:, rows, other],
-                    in0=z_rows[:, s, :, HALF:WIDTH],
-                    in1=z_rows[:, 1 - s, :, HALF:WIDTH].rearrange("p i c -> p c i"),
-                    op=ALU.add,
-                )
-            turned = ring.tile([P, WIDTH * WIDTH + WIDTH], F32, name="turned", align_bytes=64, bufs=1)
-            nc.vector.transpose(out=turned[:, 0 : WIDTH * WIDTH], in_=full[g][:, 0 : WIDTH * WIDTH])
-            nc.vector.transpose(out=turned[:, WIDTH * WIDTH :], in_=full[g][:, WIDTH * WIDTH :])
             nc.scalar.copy(
                 out=o_sb[g][:, :, 1 : WIDTH + 1],
-                in_=turned[:, 0 : WIDTH * WIDTH].rearrange("p (j e) -> p j e", e=WIDTH),
+                in_=full_t[g][:, 0 : WIDTH * WIDTH].rearrange("p (j e) -> p j e", e=WIDTH),
             )
-            nc.scalar.copy(out=kv_out[:, g, 1 : WIDTH + 1], in_=turned[:, WIDTH * WIDTH :])
+            nc.scalar.copy(out=kv_out[:, g, 1 : WIDTH + 1], in_=full_t[g][:, WIDTH * WIDTH :])
             nc.sync.dma_start(
                 out=kv_mod[0, g * HG : (g + 1) * HG].rearrange("h i j e -> (h i) (j e)"),
                 in_=o_sb[g][:].rearrange("p j e -> p (j e)"),
@@ -441,8 +468,8 @@ def tile_taylorsoftmaxattention_pa_kernel(
         keys_gain(1)
         kn_there(0)
         normalise(1)
-        extend(0)
         kn_leave(0)
+        multiply_row(0)
         transpose_x(2, on_vector)
         kn_back(0)
         quantise_x(2)
@@ -450,7 +477,6 @@ def tile_taylorsoftmaxattention_pa_kernel(
         quantise_x(3)
         keys_project(2)
         values_project(0)
-        round_keys(0)
         keys_bias(2)
         values_bias(0)
         keys_turn(2)
@@ -461,32 +487,35 @@ def tile_taylorsoftmaxattention_pa_kernel(
         values_bias(1)
         values_turn(1)
         values_round(1)
+        round_keys(0)
 
         for s in range(STEPS + 1):
-            at_group_end(unfold, s - 1)
             at(kn_there, s + 1, STEPS)
             at(keys_project, s + 3, STEPS)
             at(values_project, s + 2, STEPS)
-            at(extend, s + 1, STEPS)
-            at(round_keys, s + 1, STEPS)
             at(kn_leave, s + 1, STEPS)
             at(keys_bias, s + 3, STEPS)
             at(values_bias, s + 2, STEPS)
-            at(keys_turn, s + 3, STEPS)
+            at_group_end(unfold, s - 1)
             at(values_turn, s + 2, STEPS)
-            at(keys_gain, s + 3, STEPS)
             at(values_round, s + 2, STEPS)
-            at_group_end(plain_sums, s)
+            at(multiply_row, s + 1, STEPS)
+            at_group_end(store, s - 2)
             at(products, s, STEPS)
             if s == 0:
-                quantise_small(0)
                 quantise_values(0)
                 mask_values(0)
             at(kn_back, s + 1, STEPS)
             at(normalise, s + 2, STEPS)
-            at(quantise_small, s + 1, STEPS)
+            at(keys_turn, s + 3, STEPS)
+            at(add_plain_sums, s, STEPS)
+            at(keys_gain, s + 3, STEPS)
+            at(round_keys, s + 1, STEPS)
+            at_group_end(take_plain_sums, s)
+            at(quantise_small, s, STEPS)
             at(quantise_values, s + 1, STEPS)
             at(mask_values, s + 1, STEPS)
-            at_group_end(store, s - 1)
+            at_group_end(fold, s - 1)
             at(contract, s, STEPS)
+        store(GROUPS - 1)
         nc.sync.dma_start(out=kv[0].rearrange("(g h) d e -> (h d) g e", g=GROUPS), in_=kv_out[:])

@@ -26,7 +26,7 @@ RING = WIDTH - 1
 SHIFTS = RING // 2
 HALF = WIDTH // 2
 RUN = WIDTH * PACK
-COPIES = 5
+COPIES = 1
 REACH = RING + SHIFTS - COPIES
 REACH_PITCH = REACH + 3
 VECTOR_SHIFTS = 10

@@ -113,7 +113,7 @@ def tile_taylorsoftmaxattention_pa_kernel(
         vs_cols = const.tile([P, PASSES, P], F32)
         nc.vector.memset(vs_cols[:], 0.0)
         masked = []
-        for k in range(2):
+        for k in range(3):
             masked.append(const.tile([P, HG * MASK_PITCH], U32, name="masked%d" % k, align_bytes=64))
             nc.vector.memset(masked[k][:].bitcast(I32), 0)
         kv_out = const.tile([P, GROUPS, WIDTH + 1], F32)
@@ -130,7 +130,7 @@ def tile_taylorsoftmaxattention_pa_kernel(
             x_planes.append(const.tile([P, FEATURES], U8, name="x_planes%d" % c, align_bytes=64))
 
         xg, kb_ps, gain, moved, kn_ps, sm_bf, v_bf, gram, o_sb = {}, {}, {}, {}, {}, {}, {}, {}, {}
-        sm_codes, sm_planes, v_codes, v_planes, acc, small_acc, full, full_t = {}, {}, {}, {}, {}, {}, {}, {}
+        sm_codes, sm_planes, v_codes, v_planes, acc, small_acc, full, full_t, kk_codes, kk_planes = {}, {}, {}, {}, {}, {}, {}, {}, {}, {}
         kt, kb_t, sq_t, ss, vt, v_t, v_ps, there, there_sb = {}, {}, {}, {}, {}, {}, {}, {}, {}
 
         def transpose_x(c, copies):
@@ -300,11 +300,11 @@ def tile_taylorsoftmaxattention_pa_kernel(
                         scale=base[s % 4][:, hh * WIDTH, t : t + 1],
                     )
 
-        def add_plain_sums(s):
+        def add_plain_sums(s, slots):
             g, c = divmod(s, PASSES)
-            if c == 0:
+            if c == 0 and slots[0] == 0:
                 gram[g] = gram_ps.tile([P, P + 1], F32, name="gram")
-            for t in range(PACK):
+            for t in slots:
                 nc.tensor.matmul(
                     out=gram[g][:],
                     lhsT=base[s % 4][:, 0:P, t],
@@ -356,23 +356,24 @@ def tile_taylorsoftmaxattention_pa_kernel(
 
         def mask_values(s):
             nc.sync.dma_start(
-                out=masked[s % 2][:].bitcast(I32).rearrange("p (h w) -> p h w", w=MASK_PITCH)[:, :, 0:WIDTH],
+                out=masked[s % 3][:].bitcast(I32).rearrange("p (h w) -> p h w", w=MASK_PITCH)[:, :, 0:WIDTH],
                 in_=v_codes[s][:].bitcast(I32).rearrange("p (h e) -> p h e", h=HG),
             )
 
-        def contract(s):
-            g, c = divmod(s, PASSES)
-            kk_codes = ring.tile([P, HG * PER_HEAD], U32, name="kk_codes", align_bytes=64)
-            kk_planes = ring.tile([P, HG * PER_HEAD], U8, name="kk_planes", align_bytes=64)
+        def quantise_products(s):
+            kk_codes[s] = ring.tile([P, HG * PER_HEAD], U32, name="kk_codes", align_bytes=64)
+            kk_planes[s] = ring.tile([P, HG * PER_HEAD], U8, name="kk_planes", align_bytes=64)
             for pair in range(HG // 2):
                 cols = slice(2 * pair * PER_HEAD, 2 * (pair + 1) * PER_HEAD)
                 nc.vector.quantize_mx(
-                    out=kk_codes[:, cols].bitcast(FP8X4),
-                    scales=kk_planes[:, cols],
+                    out=kk_codes[s][:, cols].bitcast(FP8X4),
+                    scales=kk_planes[s][:, cols],
                     in_=kk[s % 2][:, 2 * pair : 2 * pair + 2, :].rearrange("p h e -> p (h e)"),
                 )
+
+        def contract_small(s):
+            g, c = divmod(s, PASSES)
             if c == 0:
-                acc[g] = acc_ps.tile([P, PER_HEAD], F32, name="acc")
                 small_acc[g] = acc_ps.tile([P, 2 * P], F32, name="small_acc")
             nc.tensor.matmul_mx(
                 out=small_acc[g][:],
@@ -383,14 +384,19 @@ def tile_taylorsoftmaxattention_pa_kernel(
                 start=(c == 0),
                 stop=(c == PASSES - 1),
             )
-            for hh in range(HG):
+
+        def contract(s, heads):
+            g, c = divmod(s, PASSES)
+            if c == 0 and heads[0] == 0:
+                acc[g] = acc_ps.tile([P, PER_HEAD], F32, name="acc")
+            for hh in heads:
                 cols = slice(hh * PER_HEAD, (hh + 1) * PER_HEAD)
                 nc.tensor.matmul_mx(
                     out=acc[g][:],
-                    lhsT=masked[s % 2][:, hh * P : (hh + 1) * P].bitcast(FP8X4),
+                    lhsT=masked[s % 3][:, hh * P : (hh + 1) * P].bitcast(FP8X4),
                     lhsT_scale=v_planes[s][:],
-                    rhs=kk_codes[:, cols].bitcast(FP8X4),
-                    rhs_scale=kk_planes[:, cols],
+                    rhs=kk_codes[s][:, cols].bitcast(FP8X4),
+                    rhs_scale=kk_planes[s][:, cols],
                     start=(c == 0 and hh == 0),
                     stop=(c == PASSES - 1 and hh == HG - 1),
                 )
@@ -490,32 +496,45 @@ def tile_taylorsoftmaxattention_pa_kernel(
         round_keys(0)
 
         for s in range(STEPS + 1):
+            before = s - 1
             at(kn_there, s + 1, STEPS)
             at(keys_project, s + 3, STEPS)
             at(values_project, s + 2, STEPS)
+            if before >= 0:
+                contract(before, (0, 1))
+                if before % PASSES == PASSES - 1:
+                    contract(before, (2, 3))
+                    contract_small(before)
             at(kn_leave, s + 1, STEPS)
             at(keys_bias, s + 3, STEPS)
             at(values_bias, s + 2, STEPS)
-            at_group_end(unfold, s - 1)
             at(values_turn, s + 2, STEPS)
             at(values_round, s + 2, STEPS)
             at(multiply_row, s + 1, STEPS)
-            at_group_end(store, s - 2)
+            at_group_end(store, before - 2)
+            at_group_end(unfold, before)
+            at(round_keys, s + 1, STEPS)
             at(products, s, STEPS)
             if s == 0:
                 quantise_values(0)
                 mask_values(0)
+            if s < STEPS:
+                add_plain_sums(s, (0, 1))
             at(kn_back, s + 1, STEPS)
+            if s < STEPS:
+                add_plain_sums(s, (2, 3))
             at(normalise, s + 2, STEPS)
             at(keys_turn, s + 3, STEPS)
-            at(add_plain_sums, s, STEPS)
+            if 0 <= before and before % PASSES != PASSES - 1:
+                contract(before, (2, 3))
+                contract_small(before)
             at(keys_gain, s + 3, STEPS)
-            at(round_keys, s + 1, STEPS)
             at_group_end(take_plain_sums, s)
             at(quantise_small, s, STEPS)
             at(quantise_values, s + 1, STEPS)
             at(mask_values, s + 1, STEPS)
-            at_group_end(fold, s - 1)
-            at(contract, s, STEPS)
+            at_group_end(fold, before - 1)
+            at(quantise_products, s, STEPS)
+        fold(GROUPS - 1)
         store(GROUPS - 1)
         nc.sync.dma_start(out=kv[0].rearrange("(g h) d e -> (h d) g e", g=GROUPS), in_=kv_out[:])

@@ -103,8 +103,11 @@ def tile_taylorsoftmaxattention_pa_kernel(
         nc.vector.memset(z[:], 0.0)
         base = []
         for k in range(4):
-            base.append(const.tile([P, P + 1, PACK], F32, name="base%d" % k))
-            nc.gpsimd.memset(base[k][:, P : P + 1, :], 1.0)
+            base.append(const.tile([P, P, PACK], F32, name="base%d" % k))
+        knp = []
+        for k in range(3):
+            knp.append(const.tile([P, PACK, P + 1], F32, name="knp%d" % k))
+            nc.gpsimd.memset(knp[k][:, :, P : P + 1], 1.0)
         kk = []
         for k in range(2):
             kk.append(const.tile([P, HG, PER_HEAD * PACK], BF16, name="kk%d" % k, align_bytes=64))
@@ -288,6 +291,7 @@ def tile_taylorsoftmaxattention_pa_kernel(
             sm_bf[s] = ring.tile([P, 2, HG, RUN], BF16, name="sm_bf", align_bytes=64)
             nc.scalar.activation(out=sm_bf[s][:, 0, :, :], in_=by_head, func=ACT.Square)
             nc.scalar.copy(out=sm_bf[s][:, 1, :, :], in_=by_head)
+            nc.scalar.copy(out=knp[s % 3][:, :, 0:P].rearrange("p t f -> p f t"), in_=base[s % 4][:])
 
         def multiply_row(s):
             for hh in range(HG):
@@ -307,8 +311,8 @@ def tile_taylorsoftmaxattention_pa_kernel(
             for t in slots:
                 nc.tensor.matmul(
                     out=gram[g][:],
-                    lhsT=base[s % 4][:, 0:P, t],
-                    rhs=base[s % 4][:, :, t],
+                    lhsT=knp[s % 3][:, t, 0:P],
+                    rhs=knp[s % 3][:, t, :],
                     start=(c == 0 and t == 0),
                     stop=(c == PASSES - 1 and t == PACK - 1),
                 )
@@ -363,12 +367,13 @@ def tile_taylorsoftmaxattention_pa_kernel(
         def quantise_products(s):
             kk_codes[s] = ring.tile([P, HG * PER_HEAD], U32, name="kk_codes", align_bytes=64)
             kk_planes[s] = ring.tile([P, HG * PER_HEAD], U8, name="kk_planes", align_bytes=64)
-            for pair in range(HG // 2):
-                cols = slice(2 * pair * PER_HEAD, 2 * (pair + 1) * PER_HEAD)
+            wide = 1 if s == STEPS - 1 else 2
+            for first in range(0, HG, wide):
+                cols = slice(first * PER_HEAD, (first + wide) * PER_HEAD)
                 nc.vector.quantize_mx(
                     out=kk_codes[s][:, cols].bitcast(FP8X4),
                     scales=kk_planes[s][:, cols],
-                    in_=kk[s % 2][:, 2 * pair : 2 * pair + 2, :].rearrange("p h e -> p (h e)"),
+                    in_=kk[s % 2][:, first : first + wide, :].rearrange("p h e -> p (h e)"),
                 )
 
         def contract_small(s):
@@ -403,8 +408,15 @@ def tile_taylorsoftmaxattention_pa_kernel(
 
         def unfold(g):
             z_skew = z[:].rearrange("p s (i w) -> p s i w", w=RING + 1)
-            full[g] = ring.tile([P, WIDTH * WIDTH + WIDTH], F32, name="full", align_bytes=64, bufs=1)
             matrix = full[g][:, 0 : WIDTH * WIDTH].rearrange("p (a b) -> p a b", b=WIDTH)
+            by_row = acc[g][:, 0:ROW].rearrange("p (l s i) -> p s i l", l=SHIFTS, s=2)
+            nc.scalar.copy(out=z_skew[:, :, :, 1 : SHIFTS + 1], in_=by_row)
+            nc.scalar.copy(out=matrix[:, 0, :], in_=acc[g][:, ROW:PER_HEAD])
+            nc.scalar.copy(out=matrix[:, 1:WIDTH, 0:1], in_=acc[g][:, ROW + 1 : PER_HEAD].unsqueeze(2))
+
+        def unfold_small(g):
+            z_skew = z[:].rearrange("p s (i w) -> p s i w", w=RING + 1)
+            full[g] = ring.tile([P, WIDTH * WIDTH + WIDTH], F32, name="full", align_bytes=64, bufs=1)
             for hh in range(HG):
                 q = slice(hh * WIDTH, (hh + 1) * WIDTH)
                 nc.scalar.mul(
@@ -416,39 +428,52 @@ def tile_taylorsoftmaxattention_pa_kernel(
                     out=full[g][q, WIDTH * WIDTH : WIDTH * WIDTH + WIDTH],
                     in_=small_acc[g][q, P + hh * WIDTH : P + (hh + 1) * WIDTH],
                 )
-            by_row = acc[g][:, 0:ROW].rearrange("p (l s i) -> p s i l", l=SHIFTS, s=2)
-            nc.scalar.copy(out=z_skew[:, :, :, 1 : SHIFTS + 1], in_=by_row)
-            nc.scalar.copy(out=matrix[:, 0, :], in_=acc[g][:, ROW:PER_HEAD])
-            nc.scalar.copy(out=matrix[:, 1:WIDTH, 0:1], in_=acc[g][:, ROW + 1 : PER_HEAD].unsqueeze(2))
 
-        def fold(g):
+        def fold(g, half):
             z_rows = z[:, :, 0 : HALF * RING].rearrange("p s (i c) -> p s i c", c=RING)
             matrix = full[g][:, 0 : WIDTH * WIDTH].rearrange("p (a b) -> p a b", b=WIDTH)
             low, high = slice(1, HALF + 1), slice(HALF + 1, WIDTH)
             upper, lower = z_rows[:, 0, :, :], z_rows[:, 1, 0 : RING - HALF, :]
-            for rows, cols, one, other in (
-                (low, low, upper[:, :, 0:HALF], upper[:, :, 0:HALF]),
-                (low, high, upper[:, :, HALF:RING], lower[:, :, RING - HALF : RING]),
-                (high, low, lower[:, :, RING - HALF : RING], upper[:, :, HALF:RING]),
-                (high, high, lower[:, :, 0 : RING - HALF], lower[:, :, 0 : RING - HALF]),
-            ):
+            if half == 0:
+                full_t[g] = ring.tile([P, WIDTH * WIDTH + WIDTH], F32, name="full_t", align_bytes=64, bufs=1)
+                nc.vector.transpose(out=full_t[g][:, WIDTH * WIDTH :], in_=full[g][:, WIDTH * WIDTH :])
+                sums = (
+                    (low, low, upper[:, :, 0:HALF], upper[:, :, 0:HALF]),
+                    (low, high, upper[:, :, HALF:RING], lower[:, :, RING - HALF : RING]),
+                )
+            else:
+                sums = (
+                    (high, low, lower[:, :, RING - HALF : RING], upper[:, :, HALF:RING]),
+                    (high, high, lower[:, :, 0 : RING - HALF], lower[:, :, 0 : RING - HALF]),
+                )
+            for rows, cols, one, other in sums:
                 nc.vector.tensor_tensor(
                     out=matrix[:, rows, cols], in0=one, in1=other.rearrange("p i c -> p c i"), op=ALU.add
                 )
-            full_t[g] = ring.tile([P, WIDTH * WIDTH + WIDTH], F32, name="full_t", align_bytes=64, bufs=1)
-            nc.vector.transpose(out=full_t[g][:, 0 : WIDTH * WIDTH], in_=full[g][:, 0 : WIDTH * WIDTH])
-            nc.vector.transpose(out=full_t[g][:, WIDTH * WIDTH :], in_=full[g][:, WIDTH * WIDTH :])
+            cols = slice(half * HALF * WIDTH, (half + 1) * HALF * WIDTH)
+            nc.vector.transpose(out=full_t[g][:, cols], in_=full[g][:, cols])
 
-        def store(g):
+        def store(g, half):
+            j = slice(half * HALF, (half + 1) * HALF)
+            if half == 0:
+                nc.scalar.copy(out=kv_out[:, g, 1 : WIDTH + 1], in_=full_t[g][:, WIDTH * WIDTH :])
+                if g == GROUPS - 1:
+                    nc.sync.dma_start(out=kv[0].rearrange("(g h) d e -> (h d) g e", g=GROUPS), in_=kv_out[:])
             nc.scalar.copy(
-                out=o_sb[g][:, :, 1 : WIDTH + 1],
-                in_=full_t[g][:, 0 : WIDTH * WIDTH].rearrange("p (j e) -> p j e", e=WIDTH),
+                out=o_sb[g][:, j, 1 : WIDTH + 1],
+                in_=full_t[g][:, half * HALF * WIDTH : (half + 1) * HALF * WIDTH].rearrange("p (j e) -> p j e", e=WIDTH),
             )
-            nc.scalar.copy(out=kv_out[:, g, 1 : WIDTH + 1], in_=full_t[g][:, WIDTH * WIDTH :])
             nc.sync.dma_start(
-                out=kv_mod[0, g * HG : (g + 1) * HG].rearrange("h i j e -> (h i) (j e)"),
-                in_=o_sb[g][:].rearrange("p j e -> p (j e)"),
+                out=kv_mod[0, g * HG : (g + 1) * HG].rearrange("h i j e -> (h i) j e")[:, j, :], in_=o_sb[g][:, j, :]
             )
+
+        def fold_all(g):
+            fold(g, 0)
+            fold(g, 1)
+
+        def store_all(g):
+            store(g, 0)
+            store(g, 1)
 
         def at(stage, step, count):
             if 0 <= step < count:
@@ -501,17 +526,19 @@ def tile_taylorsoftmaxattention_pa_kernel(
             at(keys_project, s + 3, STEPS)
             at(values_project, s + 2, STEPS)
             if before >= 0:
+                if before % PASSES == PASSES - 1:
+                    contract_small(before)
                 contract(before, (0, 1))
                 if before % PASSES == PASSES - 1:
                     contract(before, (2, 3))
-                    contract_small(before)
             at(kn_leave, s + 1, STEPS)
             at(keys_bias, s + 3, STEPS)
             at(values_bias, s + 2, STEPS)
             at(values_turn, s + 2, STEPS)
             at(values_round, s + 2, STEPS)
             at(multiply_row, s + 1, STEPS)
-            at_group_end(store, before - 2)
+            at_group_end(store_all, before - 2)
+            at_group_end(unfold_small, before)
             at_group_end(unfold, before)
             at(round_keys, s + 1, STEPS)
             at(products, s, STEPS)
@@ -533,8 +560,8 @@ def tile_taylorsoftmaxattention_pa_kernel(
             at(quantise_small, s, STEPS)
             at(quantise_values, s + 1, STEPS)
             at(mask_values, s + 1, STEPS)
-            at_group_end(fold, before - 1)
+            at_group_end(fold_all, before - 1)
             at(quantise_products, s, STEPS)
-        fold(GROUPS - 1)
-        store(GROUPS - 1)
-        nc.sync.dma_start(out=kv[0].rearrange("(g h) d e -> (h d) g e", g=GROUPS), in_=kv_out[:])
+        for half in range(2):
+            fold(GROUPS - 1, half)
+            store(GROUPS - 1, half)

@@ -26,8 +26,8 @@ RING = WIDTH - 1
 SHIFTS = RING // 2
 HALF = WIDTH // 2
 RUN = WIDTH * PACK
-COPIES = 1
-REACH = RING + SHIFTS - COPIES
+COPIES = 2
+REACH = RING + (SHIFTS - 1) // COPIES * COPIES
 REACH_PITCH = REACH + 3
 VECTOR_SHIFTS = 10
 ROW = SHIFTS * WIDTH
@@ -60,9 +60,11 @@ def tile_taylorsoftmaxattention_pa_kernel(
         for c in range(PASSES):
             x_sb.append(const.tile([P, PACK, FEATURES], BF16, name="x_sb%d" % c))
 
-        def load_x(c):
-            rows = x[0, c * P * PACK : (c + 1) * P * PACK, :]
-            nc.sync.dma_start(out=x_sb[c][:], in_=rows.rearrange("(p t) k -> p t k", t=PACK))
+        def load_x(c, pieces=1):
+            rows = x[0, c * P * PACK : (c + 1) * P * PACK, :].rearrange("(p t) k -> p t k", t=PACK)
+            for t in range(0, PACK, PACK // pieces):
+                slots = slice(t, t + PACK // pieces)
+                nc.sync.dma_start(out=x_sb[c][:, slots, :], in_=rows[:, slots, :])
 
         def load_weight(which, words, scales):
             nc.sync.dma_start(
@@ -75,7 +77,7 @@ def tile_taylorsoftmaxattention_pa_kernel(
                     in_=scales[0, r:16:4, :].bitcast(I32),
                 )
 
-        load_x(0)
+        load_x(0, 2)
         load_weight(0, wk_words, wk_scales)
         load_x(1)
         load_weight(1, wv_words, wv_scales)
@@ -194,6 +196,8 @@ def tile_taylorsoftmaxattention_pa_kernel(
             else:
                 bank = kb_pool.tile([P, PACK, P], F32, name="kb_ps")
             kb_ps[s] = turn_back(kb_t[s], bank)
+
+        def keys_norm(s):
             ss[s] = aux_ps.tile([P, PACK, HG], F32, name="ss", tag="aux")
             for t in range(PACK):
                 nc.tensor.matmul(
@@ -332,10 +336,11 @@ def tile_taylorsoftmaxattention_pa_kernel(
                 nc.gpsimd.memset(kk[(s - 1) % 2][:, :, (ROW - 1) * PACK : ROW * PACK], 0.0)
             for start in range(0, SHIFTS, COPIES):
                 engine, factor = (nc.vector, in_psum) if start < VECTOR_SHIFTS else (nc.gpsimd, in_sbuf)
-                others = moved[s][:, :, :, start : start + RING, :]
+                count = min(COPIES, SHIFTS - start)
+                others = moved[s][:, 0:count, :, start : start + RING, :]
                 engine.tensor_tensor(
-                    out=out[:, start : start + COPIES],
-                    in0=factor.unsqueeze(1).to_broadcast([P, COPIES, HG, RING * PACK]),
+                    out=out[:, start : start + count],
+                    in0=factor.unsqueeze(1).to_broadcast([P, count, HG, RING * PACK]),
                     in1=others.rearrange("p m h d t -> p m h (d t)"),
                     op=ALU.mult,
                 )
@@ -442,10 +447,8 @@ def tile_taylorsoftmaxattention_pa_kernel(
                     (low, high, upper[:, :, HALF:RING], lower[:, :, RING - HALF : RING]),
                 )
             else:
-                sums = (
-                    (high, low, lower[:, :, RING - HALF : RING], upper[:, :, HALF:RING]),
-                    (high, high, lower[:, :, 0 : RING - HALF], lower[:, :, 0 : RING - HALF]),
-                )
+                nc.scalar.copy(out=matrix[:, high, low], in_=matrix[:, low, high].rearrange("p i c -> p c i"))
+                sums = ((high, high, lower[:, :, 0 : RING - HALF], lower[:, :, 0 : RING - HALF]),)
             for rows, cols, one, other in sums:
                 nc.vector.tensor_tensor(
                     out=matrix[:, rows, cols], in0=one, in1=other.rearrange("p i c -> p c i"), op=ALU.add
@@ -492,9 +495,11 @@ def tile_taylorsoftmaxattention_pa_kernel(
         keys_project(1)
         keys_bias(0)
         keys_bias(1)
+        keys_norm(0)
         keys_turn(0)
         keys_gain(0)
         normalise(0)
+        keys_norm(1)
         keys_turn(1)
         keys_gain(1)
         kn_there(0)
@@ -510,6 +515,7 @@ def tile_taylorsoftmaxattention_pa_kernel(
         values_project(0)
         keys_bias(2)
         values_bias(0)
+        keys_norm(2)
         keys_turn(2)
         values_turn(0)
         keys_gain(2)
@@ -522,21 +528,33 @@ def tile_taylorsoftmaxattention_pa_kernel(
 
         for s in range(STEPS + 1):
             before = s - 1
+            last_pass = before >= 0 and before % PASSES == PASSES - 1
             at(kn_there, s + 1, STEPS)
             at(keys_project, s + 3, STEPS)
             at(values_project, s + 2, STEPS)
-            if before >= 0:
-                if before % PASSES == PASSES - 1:
-                    contract_small(before)
-                contract(before, (0, 1))
-                if before % PASSES == PASSES - 1:
-                    contract(before, (2, 3))
+            if last_pass:
+                contract_small(before)
+                contract(before, (0, 1, 2, 3))
+            elif before >= 0:
+                contract(before, (0,))
+            if s < STEPS:
+                add_plain_sums(s, (0, 1))
+            if before >= 0 and not last_pass:
+                contract(before, (1,))
             at(kn_leave, s + 1, STEPS)
             at(keys_bias, s + 3, STEPS)
             at(values_bias, s + 2, STEPS)
             at(values_turn, s + 2, STEPS)
             at(values_round, s + 2, STEPS)
             at(multiply_row, s + 1, STEPS)
+            if s < STEPS:
+                add_plain_sums(s, (2,))
+            at(keys_norm, s + 3, STEPS)
+            at(keys_gain, s + 3, STEPS)
+            if s < STEPS:
+                add_plain_sums(s, (3,))
+            if before >= 0 and not last_pass:
+                contract(before, (2,))
             at_group_end(store_all, before - 2)
             at_group_end(unfold_small, before)
             at_group_end(unfold, before)
@@ -545,17 +563,12 @@ def tile_taylorsoftmaxattention_pa_kernel(
             if s == 0:
                 quantise_values(0)
                 mask_values(0)
-            if s < STEPS:
-                add_plain_sums(s, (0, 1))
             at(kn_back, s + 1, STEPS)
-            if s < STEPS:
-                add_plain_sums(s, (2, 3))
             at(normalise, s + 2, STEPS)
             at(keys_turn, s + 3, STEPS)
-            if 0 <= before and before % PASSES != PASSES - 1:
-                contract(before, (2, 3))
+            if before >= 0 and not last_pass:
+                contract(before, (3,))
                 contract_small(before)
-            at(keys_gain, s + 3, STEPS)
             at_group_end(take_plain_sums, s)
             at(quantise_small, s, STEPS)
             at(quantise_values, s + 1, STEPS)

@@ -66,11 +66,13 @@ def tile_taylorsoftmaxattention_pa_kernel(
                 slots = slice(t, t + PACK // pieces)
                 nc.sync.dma_start(out=x_sb[c][:, slots, :], in_=rows[:, slots, :])
 
-        def load_weight(which, words, scales):
+        def load_words(which, words):
             nc.sync.dma_start(
                 out=w_words[:, which, :].bitcast(I32),
                 in_=words[0].rearrange("p n t -> p (n t)").bitcast(I32),
             )
+
+        def load_scales(which, scales):
             for r in range(4):
                 nc.sync.dma_start(
                     out=w_planes[r:P:32, which, :].bitcast(I32),
@@ -78,9 +80,11 @@ def tile_taylorsoftmaxattention_pa_kernel(
                 )
 
         load_x(0, 2)
-        load_weight(0, wk_words, wk_scales)
+        load_words(0, wk_words)
+        load_scales(0, wk_scales)
         load_x(1)
-        load_weight(1, wv_words, wv_scales)
+        load_scales(1, wv_scales)
+        load_words(1, wv_words)
         for c in range(2, PASSES):
             load_x(c)
 
@@ -102,7 +106,7 @@ def tile_taylorsoftmaxattention_pa_kernel(
         for hh in range(HG):
             nc.gpsimd.memset(head_of_row[hh * WIDTH : (hh + 1) * WIDTH, hh : hh + 1], 1.0)
         z = const.tile([P, 2, HALF * WIDTH], F32)
-        nc.vector.memset(z[:], 0.0)
+        nc.gpsimd.memset(z[:], 0.0)
         base = []
         for k in range(4):
             base.append(const.tile([P, P, PACK], F32, name="base%d" % k))
@@ -116,41 +120,48 @@ def tile_taylorsoftmaxattention_pa_kernel(
             ends = kk[k][:, :, 0 : ROW * PACK].rearrange("p h (l w) -> p h l w", w=RUN)[:, :, :, RING * PACK :]
             nc.vector.memset(ends, 0.0)
         vs_cols = const.tile([P, PASSES, P], F32)
-        nc.vector.memset(vs_cols[:], 0.0)
+        nc.gpsimd.memset(vs_cols[:], 0.0)
         masked = []
         for k in range(3):
             masked.append(const.tile([P, HG * MASK_PITCH], U32, name="masked%d" % k, align_bytes=64))
-            nc.vector.memset(masked[k][:].bitcast(I32), 0)
+            nc.gpsimd.memset(masked[k][:].bitcast(I32), 0)
         kv_out = const.tile([P, GROUPS, WIDTH + 1], F32)
 
-        bias_t = aux_ps.tile([P, P], BF16, tag="aux")
-        nc.tensor.transpose(bias_t[:], bias_rows[:], ident_bf[:])
         bias_cols = const.tile([P, 2 * GROUPS], F32)
-        nc.scalar.copy(out=bias_cols[:, 0:GROUPS], in_=bias_t[:, 0:GROUPS])
-        nc.scalar.mul(out=bias_cols[:, GROUPS : 2 * GROUPS], in_=bias_t[:, GROUPS : 2 * GROUPS], mul=1.0 / TOKENS)
 
         x_codes, x_planes = [], []
         for c in range(PASSES):
             x_codes.append(const.tile([P, FEATURES], U32, name="x_codes%d" % c, align_bytes=64))
             x_planes.append(const.tile([P, FEATURES], U8, name="x_planes%d" % c, align_bytes=64))
 
-        xg, kb_ps, gain, moved, kn_ps, sm_bf, v_bf, gram, o_sb = {}, {}, {}, {}, {}, {}, {}, {}, {}
+        xt, xg, kb_ps, gain, moved, kn_ps, sm_bf, v_bf, gram, o_sb = {}, {}, {}, {}, {}, {}, {}, {}, {}, {}
         sm_codes, sm_planes, v_codes, v_planes, acc, small_acc, full, full_t, kk_codes, kk_planes = {}, {}, {}, {}, {}, {}, {}, {}, {}, {}
         kt, kb_t, sq_t, ss, vt, v_t, v_ps, there, there_sb = {}, {}, {}, {}, {}, {}, {}, {}, {}
 
-        def transpose_x(c, copies):
-            xg[c] = ring.tile([P, PACK, P, PACK], BF16, name="xg", align_bytes=64)
-            xg_words = xg[c][:].bitcast(F32)
+        def turn_biases():
+            bias_t = aux_ps.tile([P, P], BF16, tag="aux")
+            nc.tensor.transpose(bias_t[:], bias_rows[:], ident_bf[:])
+            nc.scalar.copy(out=bias_cols[:, 0:GROUPS], in_=bias_t[:, 0:GROUPS])
+            nc.scalar.mul(out=bias_cols[:, GROUPS : 2 * GROUPS], in_=bias_t[:, GROUPS : 2 * GROUPS], mul=1.0 / TOKENS)
+
+        def turn_x(c):
+            xt[c] = []
             for half in range(2):
-                xt = aux_ps.tile([P, 2, 2, P], F32, tag="aux")
+                xt[c].append(aux_ps.tile([P, 2, 2, P], F32, name="xt", tag="aux"))
                 for s in range(2):
                     words = x_sb[c][:, 2 * half + s, :].bitcast(F32)
                     for u in range(2):
-                        nc.tensor.transpose(xt[:, s, u, :], words[:, u : FEATURES // 2 : 2], ident[:])
+                        nc.tensor.transpose(xt[c][half][:, s, u, :], words[:, u : FEATURES // 2 : 2], ident[:])
+
+        def lift_x(c, copies):
+            xg[c] = ring.tile([P, PACK, P, PACK], BF16, name="xg", align_bytes=64)
+            xg_words = xg[c][:].bitcast(F32)
+            for half in range(2):
                 copies[half](
                     out=xg_words[:, 2 * half : 2 * half + 2, :, :],
-                    in_=xt[:].rearrange("q s u p -> q s p u"),
+                    in_=xt[c][half][:].rearrange("q s u p -> q s p u"),
                 )
+            quantise_x(c)
 
         def quantise_x(c):
             nc.vector.quantize_mx(
@@ -185,17 +196,13 @@ def tile_taylorsoftmaxattention_pa_kernel(
 
         def keys_bias(s):
             g = s // PASSES
-            kb_t[s] = ring.tile([P, PACK * P], F32, name="kb_t")
-            nc.scalar.activation(out=kb_t[s][:], in_=kt[s][:], func=ACT.Identity, bias=bias_cols[:, g : g + 1])
             sq_t[s] = ring.tile([P, PACK * P], F32, name="sq_t")
             nc.scalar.activation(out=sq_t[s][:], in_=kt[s][:], func=ACT.Square, bias=bias_cols[:, g : g + 1])
+            kb_t[s] = ring.tile([P, PACK * P], F32, name="kb_t")
+            nc.scalar.activation(out=kb_t[s][:], in_=kt[s][:], func=ACT.Identity, bias=bias_cols[:, g : g + 1])
 
         def keys_turn(s):
-            if s == 0:
-                bank = aux_ps.tile([P, PACK, P], F32, name="kb_first", tag="aux")
-            else:
-                bank = kb_pool.tile([P, PACK, P], F32, name="kb_ps")
-            kb_ps[s] = turn_back(kb_t[s], bank)
+            kb_ps[s] = turn_back(kb_t[s], kb_pool.tile([P, PACK, P], F32, name="kb_ps"))
 
         def keys_norm(s):
             ss[s] = aux_ps.tile([P, PACK, HG], F32, name="ss", tag="aux")
@@ -236,7 +243,7 @@ def tile_taylorsoftmaxattention_pa_kernel(
             v_ps[s] = turn_back(v_t[s], aux_ps.tile([P, PACK, P], F32, name="v_ps", tag="aux"))
 
         def values_round(s):
-            v_bf[s] = ring.tile([P, P, PACK], BF16, name="v_bf", align_bytes=64)
+            v_bf[s] = ring.tile([P, P, PACK], BF16, name="v_bf", align_bytes=64, bufs=3)
             nc.scalar.copy(out=v_bf[s][:], in_=v_ps[s][:].rearrange("p t f -> p f t"))
             if s == STEPS - 1:
                 value_sums()
@@ -261,6 +268,7 @@ def tile_taylorsoftmaxattention_pa_kernel(
             return base[s % 4][:, 0:P, :].rearrange("p (h d) t -> p h d t", h=HG)
 
         def normalise(s):
+            move = nc.vector.tensor_copy if s == 0 else nc.sync.dma_start
             nc.vector.tensor_tensor(
                 out=heads_of(s),
                 in0=kb_ps[s][:].rearrange("p t (h d) -> p h d t", h=HG),
@@ -272,8 +280,8 @@ def tile_taylorsoftmaxattention_pa_kernel(
             cycle = heads_of(s)[:, :, 1:WIDTH, :]
             for m in range(COPIES):
                 front = RING - (m + 1)
-                nc.sync.dma_start(out=moved[s][:, m, :, 0:front, :], in_=cycle[:, :, m + 1 : RING, :])
-                nc.sync.dma_start(out=moved[s][:, m, :, front:REACH, :], in_=cycle[:, :, 0 : REACH - front, :])
+                move(out=moved[s][:, m, :, 0:front, :], in_=cycle[:, :, m + 1 : RING, :])
+                move(out=moved[s][:, m, :, front:REACH, :], in_=cycle[:, :, 0 : REACH - front, :])
 
         def kn_there(s):
             there[s] = aux_ps.tile([P, HG, P], F32, name="there", tag="aux")
@@ -297,6 +305,24 @@ def tile_taylorsoftmaxattention_pa_kernel(
             nc.scalar.copy(out=sm_bf[s][:, 1, :, :], in_=by_head)
             nc.scalar.copy(out=knp[s % 3][:, :, 0:P].rearrange("p t f -> p f t"), in_=base[s % 4][:])
 
+        def multiply_row_early(s):
+            nc.gpsimd.tensor_tensor(
+                out=kk[s % 2][:, :, ROW * PACK :].rearrange("p h (j t) -> p h j t", t=PACK),
+                in0=heads_of(s)[:, :, 0:1, :].to_broadcast([P, HG, WIDTH, PACK]),
+                in1=heads_of(s),
+                op=ALU.mult,
+            )
+
+        def round_keys_early(s):
+            by_head = heads_of(s).rearrange("p h d t -> p h (d t)")
+            sm_bf[s] = ring.tile([P, 2, HG, RUN], BF16, name="sm_bf", align_bytes=64)
+            nc.gpsimd.tensor_tensor(out=sm_bf[s][:, 0, :, :], in0=by_head, in1=by_head, op=ALU.mult)
+            for out, in_ in (
+                (sm_bf[s][:, 1, :, :], by_head),
+                (knp[s % 3][:, :, 0:P], base[s % 4][:].rearrange("p f t -> p t f")),
+            ):
+                nc.gpsimd.tensor_scalar(out=out, in0=in_, scalar1=1.0, scalar2=0.0, op0=ALU.mult, op1=ALU.add)
+
         def multiply_row(s):
             for hh in range(HG):
                 row = kk[s % 2][:, hh, ROW * PACK :].rearrange("p (j t) -> p j t", t=PACK)
@@ -308,11 +334,11 @@ def tile_taylorsoftmaxattention_pa_kernel(
                         scale=base[s % 4][:, hh * WIDTH, t : t + 1],
                     )
 
-        def add_plain_sums(s, slots):
+        def add_plain_sums(s):
             g, c = divmod(s, PASSES)
-            if c == 0 and slots[0] == 0:
+            if c == 0:
                 gram[g] = gram_ps.tile([P, P + 1], F32, name="gram")
-            for t in slots:
+            for t in range(PACK):
                 nc.tensor.matmul(
                     out=gram[g][:],
                     lhsT=knp[s % 3][:, t, 0:P],
@@ -381,10 +407,11 @@ def tile_taylorsoftmaxattention_pa_kernel(
                     in_=kk[s % 2][:, first : first + wide, :].rearrange("p h e -> p (h e)"),
                 )
 
-        def contract_small(s):
+        def contract(s):
             g, c = divmod(s, PASSES)
             if c == 0:
                 small_acc[g] = acc_ps.tile([P, 2 * P], F32, name="small_acc")
+                acc[g] = acc_ps.tile([P, PER_HEAD], F32, name="acc")
             nc.tensor.matmul_mx(
                 out=small_acc[g][:],
                 lhsT=v_codes[s][:].bitcast(FP8X4),
@@ -394,12 +421,7 @@ def tile_taylorsoftmaxattention_pa_kernel(
                 start=(c == 0),
                 stop=(c == PASSES - 1),
             )
-
-        def contract(s, heads):
-            g, c = divmod(s, PASSES)
-            if c == 0 and heads[0] == 0:
-                acc[g] = acc_ps.tile([P, PER_HEAD], F32, name="acc")
-            for hh in heads:
+            for hh in range(HG):
                 cols = slice(hh * PER_HEAD, (hh + 1) * PER_HEAD)
                 nc.tensor.matmul_mx(
                     out=acc[g][:],
@@ -487,88 +509,97 @@ def tile_taylorsoftmaxattention_pa_kernel(
                 stage(step // PASSES)
 
         on_vector = (nc.vector.tensor_copy, nc.vector.tensor_copy)
-        transpose_x(0, (nc.vector.tensor_copy, nc.scalar.copy))
-        quantise_x(0)
-        transpose_x(1, on_vector)
-        quantise_x(1)
+
+        def keys_chain(s):
+            keys_project(s)
+            keys_bias(s)
+            keys_norm(s)
+            keys_turn(s)
+            keys_gain(s)
+
+        turn_x(0)
+        lift_x(0, (nc.vector.tensor_copy, nc.scalar.copy))
+        turn_biases()
         keys_project(0)
-        keys_project(1)
         keys_bias(0)
-        keys_bias(1)
+        turn_x(1)
+        lift_x(1, on_vector)
         keys_norm(0)
         keys_turn(0)
         keys_gain(0)
         normalise(0)
+        multiply_row_early(0)
+        round_keys_early(0)
+        kn_there(0)
+        turn_x(2)
+        keys_project(1)
+        kn_leave(0)
+        kn_back(0)
+        lift_x(2, on_vector)
+        keys_bias(1)
         keys_norm(1)
         keys_turn(1)
         keys_gain(1)
-        kn_there(0)
-        normalise(1)
-        kn_leave(0)
-        multiply_row(0)
-        transpose_x(2, on_vector)
-        kn_back(0)
-        quantise_x(2)
-        transpose_x(3, on_vector)
-        quantise_x(3)
         keys_project(2)
         values_project(0)
         keys_bias(2)
         values_bias(0)
         keys_norm(2)
-        keys_turn(2)
         values_turn(0)
-        keys_gain(2)
         values_round(0)
         values_project(1)
         values_bias(1)
         values_turn(1)
         values_round(1)
-        round_keys(0)
 
-        for s in range(STEPS + 1):
+        products(0)
+        normalise(1)
+        kn_there(1)
+        kn_leave(1)
+        kn_back(1)
+        multiply_row_early(1)
+        keys_turn(2)
+        keys_gain(2)
+        add_plain_sums(0)
+        turn_x(3)
+        values_project(2)
+        values_bias(2)
+        values_turn(2)
+        values_round(2)
+        quantise_small(0)
+        quantise_products(0)
+        for s in range(2):
+            quantise_values(s)
+            mask_values(s)
+        normalise(2)
+        kn_there(2)
+        lift_x(3, on_vector)
+        round_keys(1)
+        keys_chain(3)
+
+        for s in range(1, STEPS + 1):
             before = s - 1
-            last_pass = before >= 0 and before % PASSES == PASSES - 1
-            at(kn_there, s + 1, STEPS)
             at(keys_project, s + 3, STEPS)
             at(values_project, s + 2, STEPS)
-            if last_pass:
-                contract_small(before)
-                contract(before, (0, 1, 2, 3))
-            elif before >= 0:
-                contract(before, (0,))
-            if s < STEPS:
-                add_plain_sums(s, (0, 1))
-            if before >= 0 and not last_pass:
-                contract(before, (1,))
+            at(contract, before, STEPS)
             at(kn_leave, s + 1, STEPS)
             at(keys_bias, s + 3, STEPS)
             at(values_bias, s + 2, STEPS)
             at(values_turn, s + 2, STEPS)
             at(values_round, s + 2, STEPS)
             at(multiply_row, s + 1, STEPS)
-            if s < STEPS:
-                add_plain_sums(s, (2,))
+            at(add_plain_sums, s, STEPS)
             at(keys_norm, s + 3, STEPS)
-            at(keys_gain, s + 3, STEPS)
-            if s < STEPS:
-                add_plain_sums(s, (3,))
-            if before >= 0 and not last_pass:
-                contract(before, (2,))
             at_group_end(store_all, before - 2)
             at_group_end(unfold_small, before)
             at_group_end(unfold, before)
             at(round_keys, s + 1, STEPS)
             at(products, s, STEPS)
-            if s == 0:
-                quantise_values(0)
-                mask_values(0)
             at(kn_back, s + 1, STEPS)
             at(normalise, s + 2, STEPS)
+            at(kn_there, s + 2, STEPS)
             at(keys_turn, s + 3, STEPS)
-            if before >= 0 and not last_pass:
-                contract(before, (3,))
-                contract_small(before)
+            at(keys_gain, s + 3, STEPS)
             at_group_end(take_plain_sums, s)
             at(quantise_small, s, STEPS)
             at(quantise_values, s + 1, STEPS)

@@ -360,13 +360,16 @@ def tile_taylorsoftmaxattention_pa_kernel(
             out = kk[s % 2][:, :, 0 : ROW * PACK].rearrange("p h (l w) -> p l h w", w=RUN)[:, :, :, 0 : RING * PACK]
             if s > 0:
                 nc.gpsimd.memset(kk[(s - 1) % 2][:, :, (ROW - 1) * PACK : ROW * PACK], 0.0)
-            for start in range(0, SHIFTS, COPIES):
-                engine, factor = (nc.vector, in_psum) if start < VECTOR_SHIFTS else (nc.gpsimd, in_sbuf)
-                count = min(COPIES, SHIFTS - start)
-                others = moved[s][:, 0:count, :, start : start + RING, :]
+            shares = [(start, COPIES, slice(0, HG), start < VECTOR_SHIFTS) for start in range(0, SHIFTS - 1, COPIES)]
+            shares.append((SHIFTS - 1, 1, slice(0, HG // 2), True))
+            shares.append((SHIFTS - 1, 1, slice(HG // 2, HG), False))
+            for start, count, heads, is_vector in shares:
+                engine, factor = (nc.vector, in_psum) if is_vector else (nc.gpsimd, in_sbuf)
+                factor = factor[:, heads, :]
+                others = moved[s][:, 0:count, heads, start : start + RING, :]
                 engine.tensor_tensor(
-                    out=out[:, start : start + count],
-                    in0=factor.unsqueeze(1).to_broadcast([P, count, HG, RING * PACK]),
+                    out=out[:, start : start + count, heads, :],
+                    in0=factor.unsqueeze(1).to_broadcast([P, count, heads.stop - heads.start, RING * PACK]),
                     in1=others.rearrange("p m h d t -> p m h (d t)"),
                     op=ALU.mult,
                 )

@@ -26,7 +26,7 @@ RING = WIDTH - 1
 SHIFTS = RING // 2
 HALF = WIDTH // 2
 RUN = WIDTH * PACK
-COPIES = 2
+COPIES = 3
 REACH = RING + (SHIFTS - 1) // COPIES * COPIES
 REACH_PITCH = REACH + 3
 VECTOR_SHIFTS = 10
@@ -359,20 +359,18 @@ def tile_taylorsoftmaxattention_pa_kernel(
             in_sbuf = heads_of(s)[:, :, 1:WIDTH, :].rearrange("p h d t -> p h (d t)")
             out = kk[s % 2][:, :, 0 : ROW * PACK].rearrange("p h (l w) -> p l h w", w=RUN)[:, :, :, 0 : RING * PACK]
             if s > 0:
-                nc.gpsimd.memset(kk[(s - 1) % 2][:, :, (ROW - 1) * PACK : ROW * PACK], 0.0)
-            shares = [(start, COPIES, slice(0, HG), start < VECTOR_SHIFTS) for start in range(0, SHIFTS - 1, COPIES)]
-            shares.append((SHIFTS - 1, 1, slice(0, HG // 2), True))
-            shares.append((SHIFTS - 1, 1, slice(HG // 2, HG), False))
-            for start, count, heads, is_vector in shares:
-                engine, factor = (nc.vector, in_psum) if is_vector else (nc.gpsimd, in_sbuf)
-                factor = factor[:, heads, :]
-                others = moved[s][:, 0:count, heads, start : start + RING, :]
-                engine.tensor_tensor(
-                    out=out[:, start : start + count, heads, :],
-                    in0=factor.unsqueeze(1).to_broadcast([P, count, heads.stop - heads.start, RING * PACK]),
-                    in1=others.rearrange("p m h d t -> p m h (d t)"),
-                    op=ALU.mult,
-                )
+                nc.gpsimd.memset(kk[(s - 1) % 2][:, 0 : HG // 2, (ROW - 1) * PACK : ROW * PACK], 0.0)
+            for start in range(0, SHIFTS, COPIES):
+                mine = min(max(VECTOR_SHIFTS - start, 0), COPIES)
+                for engine, factor, low, high in ((nc.vector, in_psum, 0, mine), (nc.gpsimd, in_sbuf, mine, COPIES)):
+                    if low < high:
+                        others = moved[s][:, low:high, :, start : start + RING, :]
+                        engine.tensor_tensor(
+                            out=out[:, start + low : start + high],
+                            in0=factor.unsqueeze(1).to_broadcast([P, high - low, HG, RING * PACK]),
+                            in1=others.rearrange("p m h d t -> p m h (d t)"),
+                            op=ALU.mult,
+                        )
 
         def quantise_small(s):
             sm_codes[s] = ring.tile([P, 2 * P], U32, name="sm_codes", align_bytes=64, bufs=3)
@@ -459,27 +457,25 @@ def tile_taylorsoftmaxattention_pa_kernel(
                     in_=small_acc[g][q, P + hh * WIDTH : P + (hh + 1) * WIDTH],
                 )
 
-        def fold(g, half):
+        def fold(g):
             z_rows = z[:, :, 0 : HALF * RING].rearrange("p s (i c) -> p s i c", c=RING)
             matrix = full[g][:, 0 : WIDTH * WIDTH].rearrange("p (a b) -> p a b", b=WIDTH)
             low, high = slice(1, HALF + 1), slice(HALF + 1, WIDTH)
             upper, lower = z_rows[:, 0, :, :], z_rows[:, 1, 0 : RING - HALF, :]
-            if half == 0:
-                full_t[g] = ring.tile([P, WIDTH * WIDTH + WIDTH], F32, name="full_t", align_bytes=64, bufs=1)
-                nc.vector.transpose(out=full_t[g][:, WIDTH * WIDTH :], in_=full[g][:, WIDTH * WIDTH :])
-                sums = (
-                    (low, low, upper[:, :, 0:HALF], upper[:, :, 0:HALF]),
-                    (low, high, upper[:, :, HALF:RING], lower[:, :, RING - HALF : RING]),
-                )
-            else:
-                nc.scalar.copy(out=matrix[:, high, low], in_=matrix[:, low, high].rearrange("p i c -> p c i"))
-                sums = ((high, high, lower[:, :, 0 : RING - HALF], lower[:, :, 0 : RING - HALF]),)
-            for rows, cols, one, other in sums:
+            full_t[g] = ring.tile([P, WIDTH * WIDTH + WIDTH], F32, name="full_t", align_bytes=64, bufs=1)
+            nc.vector.transpose(out=full_t[g][:, WIDTH * WIDTH :], in_=full[g][:, WIDTH * WIDTH :])
+            for rows, cols, one, other in (
+                (low, high, upper[:, :, HALF:RING], lower[:, :, RING - HALF : RING]),
+                (low, low, upper[:, :, 0:HALF], upper[:, :, 0:HALF]),
+                (high, high, lower[:, :, 0 : RING - HALF], lower[:, :, 0 : RING - HALF]),
+            ):
                 nc.vector.tensor_tensor(
                     out=matrix[:, rows, cols], in0=one, in1=other.rearrange("p i c -> p c i"), op=ALU.add
                 )
-            cols = slice(half * HALF * WIDTH, (half + 1) * HALF * WIDTH)
-            nc.vector.transpose(out=full_t[g][:, cols], in_=full[g][:, cols])
+            nc.scalar.copy(out=matrix[:, high, low], in_=matrix[:, low, high].rearrange("p i c -> p c i"))
+            for half in range(2):
+                cols = slice(half * HALF * WIDTH, (half + 1) * HALF * WIDTH)
+                nc.vector.transpose(out=full_t[g][:, cols], in_=full[g][:, cols])
 
         def store(g, half):
             j = slice(half * HALF, (half + 1) * HALF)
@@ -494,10 +490,6 @@ def tile_taylorsoftmaxattention_pa_kernel(
             nc.sync.dma_start(
                 out=kv_mod[0, g * HG : (g + 1) * HG].rearrange("h i j e -> (h i) j e")[:, j, :], in_=o_sb[g][:, j, :]
             )
-
-        def fold_all(g):
-            fold(g, 0)
-            fold(g, 1)
 
         def store_all(g):
             store(g, 0)
@@ -607,8 +599,7 @@ def tile_taylorsoftmaxattention_pa_kernel(
             at(quantise_small, s, STEPS)
             at(quantise_values, s + 1, STEPS)
             at(mask_values, s + 1, STEPS)
-            at_group_end(fold_all, before - 1)
+            at_group_end(fold, before - 1)
             at(quantise_products, s, STEPS)
-        for half in range(2):
-            fold(GROUPS - 1, half)
-            store(GROUPS - 1, half)
+        fold(GROUPS - 1)
+        store_all(GROUPS - 1)

@@ -26,9 +26,10 @@ RING = WIDTH - 1
 SHIFTS = RING // 2
 HALF = WIDTH // 2
 RUN = WIDTH * PACK
-COPIES = 3
-REACH = RING + (SHIFTS - 1) // COPIES * COPIES
-REACH_PITCH = REACH + 3
+COPIES = 5
+EXT = WIDTH + SHIFTS
+KEPT = EXT - COPIES + 1
+PITCH = 48
 VECTOR_SHIFTS = 10
 ROW = SHIFTS * WIDTH
 PER_HEAD = ROW + WIDTH
@@ -107,9 +108,6 @@ def tile_taylorsoftmaxattention_pa_kernel(
             nc.gpsimd.memset(head_of_row[hh * WIDTH : (hh + 1) * WIDTH, hh : hh + 1], 1.0)
         z = const.tile([P, 2, HALF * WIDTH], F32)
         nc.gpsimd.memset(z[:], 0.0)
-        base = []
-        for k in range(4):
-            base.append(const.tile([P, P, PACK], F32, name="base%d" % k))
         knp = []
         for k in range(3):
             knp.append(const.tile([P, PACK, P + 1], F32, name="knp%d" % k))
@@ -134,7 +132,7 @@ def tile_taylorsoftmaxattention_pa_kernel(
             x_codes.append(const.tile([P, FEATURES], U32, name="x_codes%d" % c, align_bytes=64))
             x_planes.append(const.tile([P, FEATURES], U8, name="x_planes%d" % c, align_bytes=64))
 
-        xt, xg, kb_ps, gain, moved, kn_ps, sm_bf, v_bf, gram, o_sb = {}, {}, {}, {}, {}, {}, {}, {}, {}, {}
+        xt, xg, kb_ps, gain, win, kn_ps, sm_bf, v_bf, gram, o_sb = {}, {}, {}, {}, {}, {}, {}, {}, {}, {}
         sm_codes, sm_planes, v_codes, v_planes, acc, small_acc, full, full_t, kk_codes, kk_planes = {}, {}, {}, {}, {}, {}, {}, {}, {}, {}
         kt, kb_t, sq_t, ss, vt, v_t, v_ps, there, there_sb = {}, {}, {}, {}, {}, {}, {}, {}, {}
 
@@ -265,29 +263,28 @@ def tile_taylorsoftmaxattention_pa_kernel(
             )
 
         def heads_of(s):
-            return base[s % 4][:, 0:P, :].rearrange("p (h d) t -> p h d t", h=HG)
+            return win[s][:, 0, :, 0:WIDTH, :]
 
         def normalise(s):
-            move = nc.vector.tensor_copy if s == 0 else nc.sync.dma_start
+            win[s] = ring.tile([P, COPIES, HG, PITCH, PACK], F32, name="win", bufs=3)
             nc.vector.tensor_tensor(
                 out=heads_of(s),
                 in0=kb_ps[s][:].rearrange("p t (h d) -> p h d t", h=HG),
                 in1=gain[s][:].rearrange("p t h -> p h t").unsqueeze(2).to_broadcast([P, HG, WIDTH, PACK]),
                 op=ALU.mult,
             )
-            copies = ring.tile([P, COPIES, HG * REACH_PITCH + 1, PACK], F32, name="moved", bufs=3)
-            moved[s] = copies[:, :, 0 : HG * REACH_PITCH, :].rearrange("p m (h e) t -> p m h e t", h=HG)
-            cycle = heads_of(s)[:, :, 1:WIDTH, :]
-            for m in range(COPIES):
-                front = RING - (m + 1)
-                move(out=moved[s][:, m, :, 0:front, :], in_=cycle[:, :, m + 1 : RING, :])
-                move(out=moved[s][:, m, :, front:REACH, :], in_=cycle[:, :, 0 : REACH - front, :])
+
+        def spread(s):
+            extend = nc.vector.tensor_copy if s < 2 else nc.scalar.copy
+            extend(out=win[s][:, 0, :, WIDTH:EXT, :], in_=win[s][:, 0, :, 1 : 1 + SHIFTS, :])
+            for l in range(COPIES - 1, 0, -1):
+                move = nc.vector.tensor_copy if s == 0 and l < COPIES - 1 else nc.sync.dma_start
+                move(out=win[s][:, l, :, 0:KEPT, :], in_=win[s][:, 0, :, l : l + KEPT, :])
 
         def kn_there(s):
             there[s] = aux_ps.tile([P, HG, P], F32, name="there", tag="aux")
             for hh in range(HG):
-                one_head = base[s % 4][:, hh * WIDTH : (hh + 1) * WIDTH, :]
-                nc.tensor.transpose(there[s][:, hh, :], one_head.rearrange("p d t -> p (d t)"), ident[:])
+                nc.tensor.transpose(there[s][:, hh, :], win[s][:, 0, hh, 0:WIDTH, :].rearrange("p d t -> p (d t)"), ident[:])
 
         def kn_leave(s):
             there_sb[s] = ring.tile([P, HG, P], F32, name="there_sb")
@@ -303,7 +300,7 @@ def tile_taylorsoftmaxattention_pa_kernel(
             sm_bf[s] = ring.tile([P, 2, HG, RUN], BF16, name="sm_bf", align_bytes=64)
             nc.scalar.activation(out=sm_bf[s][:, 0, :, :], in_=by_head, func=ACT.Square)
             nc.scalar.copy(out=sm_bf[s][:, 1, :, :], in_=by_head)
-            nc.scalar.copy(out=knp[s % 3][:, :, 0:P].rearrange("p t f -> p f t"), in_=base[s % 4][:])
+            nc.scalar.copy(out=knp[s % 3][:, :, 0:P].rearrange("p t (h d) -> p h d t", h=HG), in_=heads_of(s))
 
         def multiply_row_early(s):
             nc.gpsimd.tensor_tensor(
@@ -317,11 +314,19 @@ def tile_taylorsoftmaxattention_pa_kernel(
             by_head = heads_of(s).rearrange("p h d t -> p h (d t)")
             sm_bf[s] = ring.tile([P, 2, HG, RUN], BF16, name="sm_bf", align_bytes=64)
             nc.gpsimd.tensor_tensor(out=sm_bf[s][:, 0, :, :], in0=by_head, in1=by_head, op=ALU.mult)
-            for out, in_ in (
-                (sm_bf[s][:, 1, :, :], by_head),
-                (knp[s % 3][:, :, 0:P], base[s % 4][:].rearrange("p f t -> p t f")),
-            ):
-                nc.gpsimd.tensor_scalar(out=out, in0=in_, scalar1=1.0, scalar2=0.0, op0=ALU.mult, op1=ALU.add)
+            nc.gpsimd.tensor_scalar(
+                out=sm_bf[s][:, 1, :, :], in0=by_head, scalar1=1.0, scalar2=0.0, op0=ALU.mult, op1=ALU.add
+            )
+
+        def copy_keys_early(s):
+            nc.gpsimd.tensor_scalar(
+                out=knp[s % 3][:, :, 0:P].rearrange("p t (h d) -> p h d t", h=HG),
+                in0=heads_of(s),
+                scalar1=1.0,
+                scalar2=0.0,
+                op0=ALU.mult,
+                op1=ALU.add,
+            )
 
         def multiply_row(s):
             for hh in range(HG):
@@ -329,9 +334,9 @@ def tile_taylorsoftmaxattention_pa_kernel(
                 for t in range(PACK):
                     nc.scalar.activation(
                         out=row[:, :, t],
-                        in_=base[s % 4][:, hh * WIDTH : (hh + 1) * WIDTH, t],
+                        in_=win[s][:, 0, hh, 0:WIDTH, t],
                         func=ACT.Copy,
-                        scale=base[s % 4][:, hh * WIDTH, t : t + 1],
+                        scale=win[s][:, 0, hh, 0, t : t + 1],
                     )
 
         def add_plain_sums(s):
@@ -360,17 +365,15 @@ def tile_taylorsoftmaxattention_pa_kernel(
             out = kk[s % 2][:, :, 0 : ROW * PACK].rearrange("p h (l w) -> p l h w", w=RUN)[:, :, :, 0 : RING * PACK]
             if s > 0:
                 nc.gpsimd.memset(kk[(s - 1) % 2][:, 0 : HG // 2, (ROW - 1) * PACK : ROW * PACK], 0.0)
-            for start in range(0, SHIFTS, COPIES):
-                mine = min(max(VECTOR_SHIFTS - start, 0), COPIES)
-                for engine, factor, low, high in ((nc.vector, in_psum, 0, mine), (nc.gpsimd, in_sbuf, mine, COPIES)):
-                    if low < high:
-                        others = moved[s][:, low:high, :, start : start + RING, :]
-                        engine.tensor_tensor(
-                            out=out[:, start + low : start + high],
-                            in0=factor.unsqueeze(1).to_broadcast([P, high - low, HG, RING * PACK]),
-                            in1=others.rearrange("p m h d t -> p m h (d t)"),
-                            op=ALU.mult,
-                        )
+            for first in range(1, SHIFTS + 1, COPIES):
+                engine, factor = (nc.vector, in_psum) if first <= VECTOR_SHIFTS else (nc.gpsimd, in_sbuf)
+                others = win[s][:, :, :, 1 + first : 1 + first + RING, :]
+                engine.tensor_tensor(
+                    out=out[:, first - 1 : first - 1 + COPIES],
+                    in0=factor.unsqueeze(1).to_broadcast([P, COPIES, HG, RING * PACK]),
+                    in1=others.rearrange("p l h d t -> p l h (d t)"),
+                    op=ALU.mult,
+                )
 
         def quantise_small(s):
             sm_codes[s] = ring.tile([P, 2 * P], U32, name="sm_codes", align_bytes=64, bufs=3)
@@ -438,7 +441,8 @@ def tile_taylorsoftmaxattention_pa_kernel(
             z_skew = z[:].rearrange("p s (i w) -> p s i w", w=RING + 1)
             matrix = full[g][:, 0 : WIDTH * WIDTH].rearrange("p (a b) -> p a b", b=WIDTH)
             by_row = acc[g][:, 0:ROW].rearrange("p (l s i) -> p s i l", l=SHIFTS, s=2)
-            nc.scalar.copy(out=z_skew[:, :, :, 1 : SHIFTS + 1], in_=by_row)
+            for s in range(2):
+                nc.scalar.copy(out=z_skew[:, s, :, 1 : SHIFTS + 1], in_=by_row[:, s])
             nc.scalar.copy(out=matrix[:, 0, :], in_=acc[g][:, ROW:PER_HEAD])
             nc.scalar.copy(out=matrix[:, 1:WIDTH, 0:1], in_=acc[g][:, ROW + 1 : PER_HEAD].unsqueeze(2))
 
@@ -465,8 +469,8 @@ def tile_taylorsoftmaxattention_pa_kernel(
             full_t[g] = ring.tile([P, WIDTH * WIDTH + WIDTH], F32, name="full_t", align_bytes=64, bufs=1)
             nc.vector.transpose(out=full_t[g][:, WIDTH * WIDTH :], in_=full[g][:, WIDTH * WIDTH :])
             for rows, cols, one, other in (
-                (low, high, upper[:, :, HALF:RING], lower[:, :, RING - HALF : RING]),
                 (low, low, upper[:, :, 0:HALF], upper[:, :, 0:HALF]),
+                (low, high, upper[:, :, HALF:RING], lower[:, :, RING - HALF : RING]),
                 (high, high, lower[:, :, 0 : RING - HALF], lower[:, :, 0 : RING - HALF]),
             ):
                 nc.vector.tensor_tensor(
@@ -504,6 +508,7 @@ def tile_taylorsoftmaxattention_pa_kernel(
                 stage(step // PASSES)
 
         on_vector = (nc.vector.tensor_copy, nc.vector.tensor_copy)
+        on_both = (nc.vector.tensor_copy, nc.scalar.copy)
 
         def keys_chain(s):
             keys_project(s)
@@ -513,7 +518,7 @@ def tile_taylorsoftmaxattention_pa_kernel(
             keys_gain(s)
 
         turn_x(0)
-        lift_x(0, (nc.vector.tensor_copy, nc.scalar.copy))
+        lift_x(0, on_both)
         turn_biases()
         keys_project(0)
         keys_bias(0)
@@ -523,6 +528,7 @@ def tile_taylorsoftmaxattention_pa_kernel(
         keys_turn(0)
         keys_gain(0)
         normalise(0)
+        spread(0)
         multiply_row_early(0)
         round_keys_early(0)
         kn_there(0)
@@ -548,52 +554,62 @@ def tile_taylorsoftmaxattention_pa_kernel(
         values_round(1)
 
         products(0)
+        copy_keys_early(0)
         normalise(1)
+        spread(1)
         kn_there(1)
         kn_leave(1)
         kn_back(1)
         multiply_row_early(1)
         keys_turn(2)
         keys_gain(2)
-        add_plain_sums(0)
-        turn_x(3)
         values_project(2)
         values_bias(2)
+        turn_x(3)
         values_turn(2)
         values_round(2)
+        add_plain_sums(0)
         quantise_small(0)
         quantise_products(0)
         for s in range(2):
             quantise_values(s)
             mask_values(s)
         normalise(2)
+        spread(2)
         kn_there(2)
+        kn_leave(2)
         lift_x(3, on_vector)
-        round_keys(1)
         keys_chain(3)
+        round_keys(1)
 
         for s in range(1, STEPS + 1):
             before = s - 1
             at(keys_project, s + 3, STEPS)
             at(values_project, s + 2, STEPS)
             at(contract, before, STEPS)
-            at(kn_leave, s + 1, STEPS)
+            if s > 1:
+                at(kn_leave, s + 1, STEPS)
             at(keys_bias, s + 3, STEPS)
             at(values_bias, s + 2, STEPS)
+            at(multiply_row, s + 1, STEPS)
             at(values_turn, s + 2, STEPS)
             at(values_round, s + 2, STEPS)
-            at(multiply_row, s + 1, STEPS)
-            at(add_plain_sums, s, STEPS)
-            at(keys_norm, s + 3, STEPS)
+            if s > 1:
+                at(add_plain_sums, s, STEPS)
+                at(keys_norm, s + 3, STEPS)
             at_group_end(store_all, before - 2)
             at_group_end(unfold_small, before)
             at_group_end(unfold, before)
             at(round_keys, s + 1, STEPS)
             at(products, s, STEPS)
             at(kn_back, s + 1, STEPS)
+            if s == 1:
+                add_plain_sums(s)
+                keys_norm(s + 3)
             at(normalise, s + 2, STEPS)
             at(kn_there, s + 2, STEPS)
             at(keys_turn, s + 3, STEPS)
+            at(spread, s + 2, STEPS)
             at(keys_gain, s + 3, STEPS)
             at_group_end(take_plain_sums, s)
             at(quantise_small, s, STEPS)

from contextlib import ExitStack

import concourse.mybir as mybir
from concourse.masks import make_identity

F32 = mybir.dt.float32
BF16 = mybir.dt.bfloat16
I32 = mybir.dt.int32
U32 = mybir.dt.uint32
U8 = mybir.dt.uint8
FP8X4 = mybir.dt.float8_e4m3fn_x4
ALU = mybir.AluOpType
ACT = mybir.ActivationFunctionType

P = 128
PACK = 4
TOKENS = 2048
FEATURES = 512
HEADS = 16
WIDTH = 32
PASSES = TOKENS // (P * PACK)
GROUPS = 4
HG = HEADS // GROUPS
STEPS = GROUPS * PASSES
RING = WIDTH - 1
SHIFTS = RING // 2
HALF = WIDTH // 2
RUN = WIDTH * PACK
COPIES = 5
EXT = WIDTH + SHIFTS
KEPT = EXT - COPIES + 1
PITCH = 48
VECTOR_SHIFTS = 10
ROW = SHIFTS * WIDTH
PER_HEAD = ROW + WIDTH
MASK_PITCH = P + WIDTH
EPS = 1e-12
SCALE = 32.0 ** 0.25

FLOPS = 2 * TOKENS * FEATURES * FEATURES * 2 + 2 * HEADS * TOKENS * WIDTH * (WIDTH * WIDTH + WIDTH)


def tile_taylorsoftmaxattention_pa_kernel(
    tc, x, wk_words, wk_scales, bk, wv_words, wv_scales, bv, kv_mod, kv, vsum
):
    nc = tc.nc
    with ExitStack() as ctx:
        ctx.enter_context(tc.manual_schedule())
        const = ctx.enter_context(tc.tile_pool(name="const", bufs=1))
        ring = ctx.enter_context(tc.tile_pool(name="ring", bufs=2))
        aux_ps = ctx.enter_context(tc.psum_pool(name="aux_ps", bufs=3))
        kb_pool = ctx.enter_context(tc.psum_pool(name="kb_pool", bufs=1))
        kn_pool = ctx.enter_context(tc.psum_pool(name="kn_pool", bufs=1))
        gram_ps = ctx.enter_context(tc.psum_pool(name="gram_ps", bufs=1))
        acc_ps = ctx.enter_context(tc.psum_pool(name="acc_ps", bufs=1))

        w_words = const.tile([P, 2, FEATURES], U32, align_bytes=64)
        w_planes = const.tile([P, 2, FEATURES], U8, align_bytes=64)
        nc.vector.memset(w_planes[:].rearrange("p w n -> p (w n)").bitcast(I32), 0)
        x_sb = []
        for c in range(PASSES):
            x_sb.append(const.tile([P, PACK, FEATURES], BF16, name="x_sb%d" % c))

        def load_x(c, pieces=1):
            rows = x[0, c * P * PACK : (c + 1) * P * PACK, :].rearrange("(p t) k -> p t k", t=PACK)
            for t in range(0, PACK, PACK // pieces):
                slots = slice(t, t + PACK // pieces)
                nc.sync.dma_start(out=x_sb[c][:, slots, :], in_=rows[:, slots, :])

        def load_words(which, words):
            nc.sync.dma_start(
                out=w_words[:, which, :].bitcast(I32),
                in_=words[0].rearrange("p n t -> p (n t)").bitcast(I32),
            )

        def load_scales(which, scales):
            for r in range(4):
                nc.sync.dma_start(
                    out=w_planes[r:P:32, which, :].bitcast(I32),
                    in_=scales[0, r:16:4, :].bitcast(I32),
                )

        load_x(0, 2)
        load_words(0, wk_words)
        load_scales(0, wk_scales)
        load_x(1)
        load_scales(1, wv_scales)
        load_words(1, wv_words)
        for c in range(2, PASSES):
            load_x(c)

        bias_rows = const.tile([P, P], BF16)
        nc.vector.memset(bias_rows[:], 0.0)
        nc.scalar.dma_start(out=bias_rows[0:GROUPS, :], in_=bk.rearrange("(g f) -> g f", g=GROUPS))
        nc.scalar.dma_start(out=bias_rows[GROUPS : 2 * GROUPS, :], in_=bv.rearrange("(g f) -> g f", g=GROUPS))

        one_cols = const.tile([P, PASSES * PACK], F32)
        nc.vector.memset(one_cols[:], 1.0)
        warm = const.tile([P, 1], F32)
        nc.scalar.activation(out=warm[:], in_=one_cols[:, 0:1], func=ACT.Abs_reciprocal_sqrt)
        ident = const.tile([P, P], F32)
        make_identity(nc, ident[:])
        ident_bf = const.tile([P, P], BF16)
        make_identity(nc, ident_bf[:])
        head_of_row = const.tile([P, HG], F32)
        nc.gpsimd.memset(head_of_row[:], 0.0)
        for hh in range(HG):
            nc.gpsimd.memset(head_of_row[hh * WIDTH : (hh + 1) * WIDTH, hh : hh + 1], 1.0)
        z = const.tile([P, 2, HALF * WIDTH], F32)
        nc.gpsimd.memset(z[:], 0.0)
        knp = []
        for k in range(3):
            knp.append(const.tile([P, PACK, P + 1], F32, name="knp%d" % k))
            nc.gpsimd.memset(knp[k][:, :, P : P + 1], 1.0)
        kk = []
        for k in range(2):
            kk.append(const.tile([P, HG, PER_HEAD * PACK], BF16, name="kk%d" % k, align_bytes=64))
            ends = kk[k][:, :, 0 : ROW * PACK].rearrange("p h (l w) -> p h l w", w=RUN)[:, :, :, RING * PACK :]
            nc.vector.memset(ends, 0.0)
        vs_cols = const.tile([P, PASSES, P], F32)
        nc.gpsimd.memset(vs_cols[:], 0.0)
        masked = []
        for k in range(3):
            masked.append(const.tile([P, HG * MASK_PITCH], U32, name="masked%d" % k, align_bytes=64))
            nc.gpsimd.memset(masked[k][:].bitcast(I32), 0)
        kv_out = const.tile([P, GROUPS, WIDTH + 1], F32)

        bias_cols = const.tile([P, 2 * GROUPS], F32)

        x_codes, x_planes = [], []
        for c in range(PASSES):
            x_codes.append(const.tile([P, FEATURES], U32, name="x_codes%d" % c, align_bytes=64))
            x_planes.append(const.tile([P, FEATURES], U8, name="x_planes%d" % c, align_bytes=64))

        xt, xg, kb_ps, gain, win, kn_ps, sm_bf, v_bf, gram, o_sb = {}, {}, {}, {}, {}, {}, {}, {}, {}, {}
        sm_codes, sm_planes, v_codes, v_planes, acc, small_acc, full, full_t, kk_codes, kk_planes = {}, {}, {}, {}, {}, {}, {}, {}, {}, {}
        kt, kb_t, sq_t, ss, vt, v_t, v_ps, there, there_sb = {}, {}, {}, {}, {}, {}, {}, {}, {}

        def turn_biases():
            bias_t = aux_ps.tile([P, P], BF16, tag="aux")
            nc.tensor.transpose(bias_t[:], bias_rows[:], ident_bf[:])
            nc.scalar.copy(out=bias_cols[:, 0:GROUPS], in_=bias_t[:, 0:GROUPS])
            nc.scalar.mul(out=bias_cols[:, GROUPS : 2 * GROUPS], in_=bias_t[:, GROUPS : 2 * GROUPS], mul=1.0 / TOKENS)

        def turn_x(c):
            xt[c] = []
            for half in range(2):
                xt[c].append(aux_ps.tile([P, 2, 2, P], F32, name="xt", tag="aux"))
                for s in range(2):
                    words = x_sb[c][:, 2 * half + s, :].bitcast(F32)
                    for u in range(2):
                        nc.tensor.transpose(xt[c][half][:, s, u, :], words[:, u : FEATURES // 2 : 2], ident[:])

        def lift_x(c, copies):
            xg[c] = ring.tile([P, PACK, P, PACK], BF16, name="xg", align_bytes=64)
            xg_words = xg[c][:].bitcast(F32)
            for half in range(2):
                copies[half](
                    out=xg_words[:, 2 * half : 2 * half + 2, :, :],
                    in_=xt[c][half][:].rearrange("q s u p -> q s p u"),
                )
            quantise_x(c)

        def quantise_x(c):
            nc.vector.quantize_mx(
                out=x_codes[c][:].bitcast(FP8X4),
                scales=x_planes[c][:],
                in_=xg[c][:].rearrange("q t p j -> q (t p j)"),
            )

        def project_turned(c, g, which):
            bank = aux_ps.tile([P, PACK * P], F32, tag="aux")
            cols = slice(g * P, (g + 1) * P)
            nc.tensor.matmul_mx(
                out=bank[:],
                lhsT=w_words[:, which, cols].bitcast(FP8X4),
                lhsT_scale=w_planes[:, which, cols],
                rhs=x_codes[c][:].bitcast(FP8X4),
                rhs_scale=x_planes[c][:],
                start=True,
                stop=True,
            )
            return bank

        def turn_back(turned, bank):
            for t in range(PACK):
                nc.tensor.transpose(bank[:, t, :], turned[:, t * P : (t + 1) * P], ident[:])
            return bank


        def keys_project(s):
            g, c = divmod(s, PASSES)
            kt[s] = project_turned(c, g, 0)

        def keys_bias(s):
            g = s // PASSES
            sq_t[s] = ring.tile([P, PACK * P], F32, name="sq_t")
            nc.scalar.activation(out=sq_t[s][:], in_=kt[s][:], func=ACT.Square, bias=bias_cols[:, g : g + 1])
            kb_t[s] = ring.tile([P, PACK * P], F32, name="kb_t")
            nc.scalar.activation(out=kb_t[s][:], in_=kt[s][:], func=ACT.Identity, bias=bias_cols[:, g : g + 1])

        def keys_turn(s):
            kb_ps[s] = turn_back(kb_t[s], kb_pool.tile([P, PACK, P], F32, name="kb_ps"))

        def keys_norm(s):
            ss[s] = aux_ps.tile([P, PACK, HG], F32, name="ss", tag="aux")
            for t in range(PACK):
                nc.tensor.matmul(
                    out=ss[s][:, t, :], lhsT=sq_t[s][:, t * P : (t + 1) * P], rhs=head_of_row[:], start=True, stop=True
                )

        def keys_gain(s):
            above = ring.tile([P, PACK, HG], F32, name="above")
            nc.scalar.activation(out=above[:], in_=ss[s][:], func=ACT.Relu, bias=-EPS * EPS)
            gain[s] = ring.tile([P, PACK, HG], F32, name="gain", bufs=3)
            nc.scalar.activation(
                out=gain[s][:],
                in_=above[:],
                func=ACT.Abs_reciprocal_sqrt,
                scale=1.0 / (SCALE * SCALE),
                bias=EPS * EPS / (SCALE * SCALE),
            )

        def values_project(s):
            g, c = divmod(s, PASSES)
            vt[s] = project_turned(c, g, 1)

        def values_bias(s):
            g, c = divmod(s, PASSES)
            v_t[s] = ring.tile([P, PACK * P], F32, name="v_t")
            nc.scalar.activation(
                out=v_t[s][:],
                in_=vt[s][:],
                func=ACT.Identity,
                scale=1.0 / TOKENS,
                bias=bias_cols[:, GROUPS + g : GROUPS + g + 1],
                accum_out=vs_cols[:, c, g : g + 1],
            )

        def values_turn(s):
            v_ps[s] = turn_back(v_t[s], aux_ps.tile([P, PACK, P], F32, name="v_ps", tag="aux"))

        def values_round(s):
            v_bf[s] = ring.tile([P, P, PACK], BF16, name="v_bf", align_bytes=64, bufs=3)
            nc.scalar.copy(out=v_bf[s][:], in_=v_ps[s][:].rearrange("p t f -> p f t"))
            if s == STEPS - 1:
                value_sums()

        def value_sums():
            total = aux_ps.tile([P, P], F32, tag="aux")
            for c in range(PASSES):
                nc.tensor.matmul(
                    out=total[:], lhsT=vs_cols[:, c, :], rhs=ident[:], start=(c == 0), stop=(c == PASSES - 1)
                )
            vsum_sb = const.tile([GROUPS, HG, WIDTH + 1], F32)
            nc.scalar.copy(out=vsum_sb[:, :, 0:1], in_=one_cols[0:GROUPS, 0:HG].unsqueeze(2))
            nc.scalar.copy(
                out=vsum_sb[:, :, 1 : WIDTH + 1], in_=total[0:GROUPS, :].rearrange("g (h e) -> g h e", h=HG)
            )
            nc.sync.dma_start(
                out=vsum.rearrange("b (g h) o e -> (b g) (h o e)", g=GROUPS),
                in_=vsum_sb[:].rearrange("g h e -> g (h e)"),
            )

        def heads_of(s):
            return win[s][:, 0, :, 0:WIDTH, :]

        def normalise(s):
            win[s] = ring.tile([P, COPIES, HG, PITCH, PACK], F32, name="win", bufs=3)
            nc.vector.tensor_tensor(
                out=heads_of(s),
                in0=kb_ps[s][:].rearrange("p t (h d) -> p h d t", h=HG),
                in1=gain[s][:].rearrange("p t h -> p h t").unsqueeze(2).to_broadcast([P, HG, WIDTH, PACK]),
                op=ALU.mult,
            )

        def spread(s):
            extend = nc.vector.tensor_copy if s < 2 else nc.scalar.copy
            extend(out=win[s][:, 0, :, WIDTH:EXT, :], in_=win[s][:, 0, :, 1 : 1 + SHIFTS, :])
            for l in range(COPIES - 1, 0, -1):
                move = nc.vector.tensor_copy if s == 0 and l < COPIES - 1 else nc.sync.dma_start
                move(out=win[s][:, l, :, 0:KEPT, :], in_=win[s][:, 0, :, l : l + KEPT, :])

        def kn_there(s):
            there[s] = aux_ps.tile([P, HG, P], F32, name="there", tag="aux")
            for hh in range(HG):
                nc.tensor.transpose(there[s][:, hh, :], win[s][:, 0, hh, 0:WIDTH, :].rearrange("p d t -> p (d t)"), ident[:])

        def kn_leave(s):
            there_sb[s] = ring.tile([P, HG, P], F32, name="there_sb")
            nc.scalar.copy(out=there_sb[s][:], in_=there[s][:])

        def kn_back(s):
            kn_ps[s] = kn_pool.tile([P, HG, RUN], F32, name="kn_ps")
            for hh in range(HG):
                nc.tensor.transpose(kn_ps[s][:, hh, :], there_sb[s][:, hh, :], ident[:])

        def round_keys(s):
            by_head = heads_of(s).rearrange("p h d t -> p h (d t)")
            sm_bf[s] = ring.tile([P, 2, HG, RUN], BF16, name="sm_bf", align_bytes=64)
            nc.scalar.activation(out=sm_bf[s][:, 0, :, :], in_=by_head, func=ACT.Square)
            nc.scalar.copy(out=sm_bf[s][:, 1, :, :], in_=by_head)
            nc.scalar.copy(out=knp[s % 3][:, :, 0:P].rearrange("p t (h d) -> p h d t", h=HG), in_=heads_of(s))

        def multiply_row_early(s):
            nc.gpsimd.tensor_tensor(
                out=kk[s % 2][:, :, ROW * PACK :].rearrange("p h (j t) -> p h j t", t=PACK),
                in0=heads_of(s)[:, :, 0:1, :].to_broadcast([P, HG, WIDTH, PACK]),
                in1=heads_of(s),
                op=ALU.mult,
            )

        def round_keys_early(s):
            by_head = heads_of(s).rearrange("p h d t -> p h (d t)")
            sm_bf[s] = ring.tile([P, 2, HG, RUN], BF16, name="sm_bf", align_bytes=64)
            nc.gpsimd.tensor_tensor(out=sm_bf[s][:, 0, :, :], in0=by_head, in1=by_head, op=ALU.mult)
            nc.gpsimd.tensor_scalar(
                out=sm_bf[s][:, 1, :, :], in0=by_head, scalar1=1.0, scalar2=0.0, op0=ALU.mult, op1=ALU.add
            )

        def copy_keys_early(s):
            nc.gpsimd.tensor_scalar(
                out=knp[s % 3][:, :, 0:P].rearrange("p t (h d) -> p h d t", h=HG),
                in0=heads_of(s),
                scalar1=1.0,
                scalar2=0.0,
                op0=ALU.mult,
                op1=ALU.add,
            )

        def multiply_row(s):
            for hh in range(HG):
                row = kk[s % 2][:, hh, ROW * PACK :].rearrange("p (j t) -> p j t", t=PACK)
                for t in range(PACK):
                    nc.scalar.activation(
                        out=row[:, :, t],
                        in_=win[s][:, 0, hh, 0:WIDTH, t],
                        func=ACT.Copy,
                        scale=win[s][:, 0, hh, 0, t : t + 1],
                    )

        def add_plain_sums(s):
            g, c = divmod(s, PASSES)
            if c == 0:
                gram[g] = gram_ps.tile([P, P + 1], F32, name="gram")
            for t in range(PACK):
                nc.tensor.matmul(
                    out=gram[g][:],
                    lhsT=knp[s % 3][:, t, 0:P],
                    rhs=knp[s % 3][:, t, :],
                    start=(c == 0 and t == 0),
                    stop=(c == PASSES - 1 and t == PACK - 1),
                )

        def take_plain_sums(g):
            o_sb[g] = ring.tile([P, WIDTH, WIDTH + 1], F32, name="o_sb")
            for hh in range(HG):
                q = slice(hh * WIDTH, (hh + 1) * WIDTH)
                nc.scalar.mul(out=o_sb[g][q, :, 0:1], in_=gram[g][q, q].unsqueeze(2), mul=1.0 / TOKENS)
            nc.scalar.mul(out=kv_out[:, g, 0:1], in_=gram[g][:, P : P + 1], mul=1.0 / TOKENS)

        def products(s):
            in_psum = kn_ps[s][:, :, PACK:RUN]
            in_sbuf = heads_of(s)[:, :, 1:WIDTH, :].rearrange("p h d t -> p h (d t)")
            out = kk[s % 2][:, :, 0 : ROW * PACK].rearrange("p h (l w) -> p l h w", w=RUN)[:, :, :, 0 : RING * PACK]
            if s > 0:
                nc.gpsimd.memset(kk[(s - 1) % 2][:, 0 : HG // 2, (ROW - 1) * PACK : ROW * PACK], 0.0)
            for first in range(1, SHIFTS + 1, COPIES):
                engine, factor = (nc.vector, in_psum) if first <= VECTOR_SHIFTS else (nc.gpsimd, in_sbuf)
                others = win[s][:, :, :, 1 + first : 1 + first + RING, :]
                engine.tensor_tensor(
                    out=out[:, first - 1 : first - 1 + COPIES],
                    in0=factor.unsqueeze(1).to_broadcast([P, COPIES, HG, RING * PACK]),
                    in1=others.rearrange("p l h d t -> p l h (d t)"),
                    op=ALU.mult,
                )

        def quantise_small(s):
            sm_codes[s] = ring.tile([P, 2 * P], U32, name="sm_codes", align_bytes=64, bufs=3)
            sm_planes[s] = ring.tile([P, 2 * P], U8, name="sm_planes", align_bytes=64, bufs=3)
            nc.vector.quantize_mx(
                out=sm_codes[s][:].bitcast(FP8X4),
                scales=sm_planes[s][:],
                in_=sm_bf[s][:].rearrange("p k h e -> p (k h e)"),
            )

        def quantise_values(s):
            v_codes[s] = ring.tile([P, P], U32, name="v_codes", align_bytes=64, bufs=3)
            v_planes[s] = ring.tile([P, P], U8, name="v_planes", align_bytes=64, bufs=3)
            nc.vector.quantize_mx(
                out=v_codes[s][:].bitcast(FP8X4),
                scales=v_planes[s][:],
                in_=v_bf[s][:].rearrange("p f t -> p (f t)"),
            )

        def mask_values(s):
            nc.sync.dma_start(
                out=masked[s % 3][:].bitcast(I32).rearrange("p (h w) -> p h w", w=MASK_PITCH)[:, :, 0:WIDTH],
                in_=v_codes[s][:].bitcast(I32).rearrange("p (h e) -> p h e", h=HG),
            )

        def quantise_products(s):
            kk_codes[s] = ring.tile([P, HG * PER_HEAD], U32, name="kk_codes", align_bytes=64)
            kk_planes[s] = ring.tile([P, HG * PER_HEAD], U8, name="kk_planes", align_bytes=64)
            wide = 1 if s == STEPS - 1 else 2
            for first in range(0, HG, wide):
                cols = slice(first * PER_HEAD, (first + wide) * PER_HEAD)
                nc.vector.quantize_mx(
                    out=kk_codes[s][:, cols].bitcast(FP8X4),
                    scales=kk_planes[s][:, cols],
                    in_=kk[s % 2][:, first : first + wide, :].rearrange("p h e -> p (h e)"),
                )

        def contract(s):
            g, c = divmod(s, PASSES)
            if c == 0:
                small_acc[g] = acc_ps.tile([P, 2 * P], F32, name="small_acc")
                acc[g] = acc_ps.tile([P, PER_HEAD], F32, name="acc")
            nc.tensor.matmul_mx(
                out=small_acc[g][:],
                lhsT=v_codes[s][:].bitcast(FP8X4),
                lhsT_scale=v_planes[s][:],
                rhs=sm_codes[s][:].bitcast(FP8X4),
                rhs_scale=sm_planes[s][:],
                start=(c == 0),
                stop=(c == PASSES - 1),
            )
            for hh in range(HG):
                cols = slice(hh * PER_HEAD, (hh + 1) * PER_HEAD)
                nc.tensor.matmul_mx(
                    out=acc[g][:],
                    lhsT=masked[s % 3][:, hh * P : (hh + 1) * P].bitcast(FP8X4),
                    lhsT_scale=v_planes[s][:],
                    rhs=kk_codes[s][:, cols].bitcast(FP8X4),
                    rhs_scale=kk_planes[s][:, cols],
                    start=(c == 0 and hh == 0),
                    stop=(c == PASSES - 1 and hh == HG - 1),
                )

        def unfold(g):
            z_skew = z[:].rearrange("p s (i w) -> p s i w", w=RING + 1)
            matrix = full[g][:, 0 : WIDTH * WIDTH].rearrange("p (a b) -> p a b", b=WIDTH)
            by_row = acc[g][:, 0:ROW].rearrange("p (l s i) -> p s i l", l=SHIFTS, s=2)
            for s in range(2):
                nc.scalar.copy(out=z_skew[:, s, :, 1 : SHIFTS + 1], in_=by_row[:, s])
            nc.scalar.copy(out=matrix[:, 0, :], in_=acc[g][:, ROW:PER_HEAD])
            nc.scalar.copy(out=matrix[:, 1:WIDTH, 0:1], in_=acc[g][:, ROW + 1 : PER_HEAD].unsqueeze(2))

        def unfold_small(g):
            z_skew = z[:].rearrange("p s (i w) -> p s i w", w=RING + 1)
            full[g] = ring.tile([P, WIDTH * WIDTH + WIDTH], F32, name="full", align_bytes=64, bufs=1)
            for hh in range(HG):
                q = slice(hh * WIDTH, (hh + 1) * WIDTH)
                nc.scalar.mul(
                    out=z_skew[q, :, :, 0:1],
                    in_=small_acc[g][q, hh * WIDTH + 1 : (hh + 1) * WIDTH + 1].rearrange("p (s i) -> p s i", s=2).unsqueeze(3),
                    mul=0.5,
                )
                nc.scalar.copy(
                    out=full[g][q, WIDTH * WIDTH : WIDTH * WIDTH + WIDTH],
                    in_=small_acc[g][q, P + hh * WIDTH : P + (hh + 1) * WIDTH],
                )

        def fold(g):
            z_rows = z[:, :, 0 : HALF * RING].rearrange("p s (i c) -> p s i c", c=RING)
            matrix = full[g][:, 0 : WIDTH * WIDTH].rearrange("p (a b) -> p a b", b=WIDTH)
            low, high = slice(1, HALF + 1), slice(HALF + 1, WIDTH)
            upper, lower = z_rows[:, 0, :, :], z_rows[:, 1, 0 : RING - HALF, :]
            full_t[g] = ring.tile([P, WIDTH * WIDTH + WIDTH], F32, name="full_t", align_bytes=64, bufs=1)
            nc.vector.transpose(out=full_t[g][:, WIDTH * WIDTH :], in_=full[g][:, WIDTH * WIDTH :])
            for rows, cols, one, other in (
                (low, low, upper[:, :, 0:HALF], upper[:, :, 0:HALF]),
                (low, high, upper[:, :, HALF:RING], lower[:, :, RING - HALF : RING]),
                (high, high, lower[:, :, 0 : RING - HALF], lower[:, :, 0 : RING - HALF]),
            ):
                nc.vector.tensor_tensor(
                    out=matrix[:, rows, cols], in0=one, in1=other.rearrange("p i c -> p c i"), op=ALU.add
                )
            nc.scalar.copy(out=matrix[:, high, low], in_=matrix[:, low, high].rearrange("p i c -> p c i"))
            for half in range(2):
                cols = slice(half * HALF * WIDTH, (half + 1) * HALF * WIDTH)
                nc.vector.transpose(out=full_t[g][:, cols], in_=full[g][:, cols])

        def store(g, half):
            j = slice(half * HALF, (half + 1) * HALF)
            if half == 0:
                nc.scalar.copy(out=kv_out[:, g, 1 : WIDTH + 1], in_=full_t[g][:, WIDTH * WIDTH :])
                if g == GROUPS - 1:
                    nc.sync.dma_start(out=kv[0].rearrange("(g h) d e -> (h d) g e", g=GROUPS), in_=kv_out[:])
            nc.scalar.copy(
                out=o_sb[g][:, j, 1 : WIDTH + 1],
                in_=full_t[g][:, half * HALF * WIDTH : (half + 1) * HALF * WIDTH].rearrange("p (j e) -> p j e", e=WIDTH),
            )
            nc.sync.dma_start(
                out=kv_mod[0, g * HG : (g + 1) * HG].rearrange("h i j e -> (h i) j e")[:, j, :], in_=o_sb[g][:, j, :]
            )

        def store_all(g):
            store(g, 0)
            store(g, 1)

        def at(stage, step, count):
            if 0 <= step < count:
                stage(step)

        def at_group_end(stage, step):
            if 0 <= step < STEPS and step % PASSES == PASSES - 1:
                stage(step // PASSES)

        on_vector = (nc.vector.tensor_copy, nc.vector.tensor_copy)
        on_both = (nc.vector.tensor_copy, nc.scalar.copy)

        def keys_chain(s):
            keys_project(s)
            keys_bias(s)
            keys_norm(s)
            keys_turn(s)
            keys_gain(s)

        turn_x(0)
        lift_x(0, on_both)
        turn_biases()
        keys_project(0)
        keys_bias(0)
        turn_x(1)
        lift_x(1, on_vector)
        keys_norm(0)
        keys_turn(0)
        keys_gain(0)
        normalise(0)
        spread(0)
        multiply_row_early(0)
        round_keys_early(0)
        kn_there(0)
        turn_x(2)
        keys_project(1)
        kn_leave(0)
        kn_back(0)
        lift_x(2, on_vector)
        keys_bias(1)
        keys_norm(1)
        keys_turn(1)
        keys_gain(1)
        keys_project(2)
        values_project(0)
        keys_bias(2)
        values_bias(0)
        keys_norm(2)
        values_turn(0)
        values_round(0)
        values_project(1)
        values_bias(1)
        values_turn(1)
        values_round(1)

        products(0)
        copy_keys_early(0)
        normalise(1)
        spread(1)
        kn_there(1)
        kn_leave(1)
        kn_back(1)
        multiply_row_early(1)
        keys_turn(2)
        keys_gain(2)
        values_project(2)
        values_bias(2)
        turn_x(3)
        values_turn(2)
        values_round(2)
        add_plain_sums(0)
        quantise_small(0)
        quantise_products(0)
        for s in range(2):
            quantise_values(s)
            mask_values(s)
        normalise(2)
        spread(2)
        kn_there(2)
        kn_leave(2)
        lift_x(3, on_vector)
        keys_chain(3)
        round_keys(1)

        for s in range(1, STEPS + 1):
            before = s - 1
            at(keys_project, s + 3, STEPS)
            at(values_project, s + 2, STEPS)
            at(contract, before, STEPS)
            if s > 1:
                at(kn_leave, s + 1, STEPS)
            at(keys_bias, s + 3, STEPS)
            at(values_bias, s + 2, STEPS)
            at(multiply_row, s + 1, STEPS)
            at(values_turn, s + 2, STEPS)
            at(values_round, s + 2, STEPS)
            if s > 1:
                at(add_plain_sums, s, STEPS)
                at(keys_norm, s + 3, STEPS)
            at_group_end(store_all, before - 2)
            at_group_end(unfold_small, before)
            at_group_end(unfold, before)
            at(round_keys, s + 1, STEPS)
            at(products, s, STEPS)
            at(kn_back, s + 1, STEPS)
            if s == 1:
                add_plain_sums(s)
                keys_norm(s + 3)
            at(normalise, s + 2, STEPS)
            at(kn_there, s + 2, STEPS)
            at(keys_turn, s + 3, STEPS)
            at(spread, s + 2, STEPS)
            at(keys_gain, s + 3, STEPS)
            at_group_end(take_plain_sums, s)
            at(quantise_small, s, STEPS)
            at(quantise_values, s + 1, STEPS)
            at(mask_values, s + 1, STEPS)
            at_group_end(fold, before - 1)
            at(quantise_products, s, STEPS)
        fold(GROUPS - 1)
        store_all(GROUPS - 1)
